import numpy as np
import ml_dtypes


def mxq(x, axis, fmt="e4m3"):
    dtype, down = {"e4m3": (ml_dtypes.float8_e4m3fn, 7), "e5m2": (ml_dtypes.float8_e5m2, 14)}[fmt]
    v = np.moveaxis(np.asarray(x, np.float32).astype(ml_dtypes.bfloat16).astype(np.float64), axis, -1)
    blocks = v.reshape(v.shape[:-1] + (-1, 32))
    amax = np.abs(blocks).max(-1, keepdims=True)
    byte = np.maximum(np.where(amax > 0, np.frexp(amax)[1] - 1 + 127, 0) - down, 1)
    scale = np.exp2(byte - 127.0)
    codes = (blocks / scale).astype(np.float32).astype(dtype).astype(np.float64)
    return np.moveaxis((codes * scale).reshape(v.shape), -1, axis)


WIDE = False


def mx_kscale(k):
    if not WIDE:
        return np.ones(k)
    levels = np.array([10, -10, 5, -5, 0])
    a = np.random.permutation(np.resize(levels, k // 512 * 4)).reshape(k // 512, 4)
    idx = np.arange(k)
    return np.exp2(a[idx // 512, idx % 128 // 32])


BF16 = ml_dtypes.bfloat16


def bf(x):
    return np.asarray(x, np.float32).astype(BF16)


def f64(x):
    return np.asarray(x).astype(np.float64)


B, S, D, H, L = 8, 512, 512, 2, 128


def setup_inputs():
    s = mx_kscale(D)
    return {"q": bf(np.random.standard_normal((B, S, H, L)) * 1.5),
            "k": bf(np.random.standard_normal((B, S, H, L)) * 1.5),
            "x": bf(np.random.standard_normal((B, S, D)) * s),
            "Wv": bf(np.random.standard_normal((H * D, D)) / np.sqrt(D) / s),
            "mask": np.tril(np.ones((S, S), np.int32))[None, :, :]}


def reference(q, k, x, Wv, mask):
    v = mxq(f64(x), 2, "e4m3") @ mxq(f64(Wv), 1, "e4m3").T
    scores = (f64(q).transpose(0, 2, 1, 3) @ f64(k).transpose(0, 2, 3, 1)) * (1.0 / np.sqrt(L))
    scores = np.where(f64(mask)[:, None, :, :] == 0, -np.inf, scores)
    e = np.exp(scores - scores.max(-1, keepdims=True))
    attn = e / e.sum(-1, keepdims=True)
    a2 = attn.transpose(0, 2, 1, 3).reshape(B, S, H * S)
    v2 = v.reshape(B, S, H, D).transpose(0, 2, 1, 3).reshape(B, H * S, D)
    return mxq(a2, 2, "e4m3") @ mxq(v2, 1, "e4m3")

@@ -1,0 +1,442 @@
+from contextlib import ExitStack
+import math
+
+import concourse.mybir as mybir
+from concourse.masks import make_identity
+
+F32 = mybir.dt.float32
+BF16 = mybir.dt.bfloat16
+I32 = mybir.dt.int32
+U32 = mybir.dt.uint32
+U8 = mybir.dt.uint8
+FP8X4 = mybir.dt.float8_e4m3fn_x4
+ALU = mybir.AluOpType
+ACT = mybir.ActivationFunctionType
+AX = mybir.AxisListType
+
+B, S, D, H, L = 8, 512, 512, 2, 128
+P = 128
+NT = S // P
+FLOPS = 2 * B * S * D * H * D + 2 * B * H * S * S * L + 2 * B * S * H * S * D
+SCALE = 1.0 / math.sqrt(L)
+BIG = float(2 ** 100)
+MANUAL = True
+AW = (256, 256, 512, 512)
+SEGS = (((0, 0), (1, 0)), ((2, 0), (3, 0)), ((2, 1), (3, 1)))
+
+ORDER = (
+    ("INIT",), ("LQ", 0), ("LK", 0), ("LM",), ("LX", 0), ("LW", 0), ("LW", 1), ("LX", 1), ("LQ", 1), ("LK", 1),
+    ("LX", 2), ("LQ", 2), ("LK", 2), ("LX", 3), ("LQ", 3), ("LK", 3), ("LX", 4), ("LQ", 4), ("LK", 4), ("LX", 5),
+    ("LQ", 5), ("LK", 5), ("LX", 6), ("LQ", 6), ("LK", 6), ("LX", 7), ("LQ", 7), ("LK", 7), ("TQ", 0, 0),
+    ("CQ", 0, 0, "v"), ("TQ", 0, 1), ("CQ", 0, 1, "s"), ("MB",), ("SC", 0, 3, 0), ("SC", 0, 3, 1), ("SC", 0, 2, 0),
+    ("SC", 0, 2, 1), ("RM", 0, 3, 0), ("RM", 0, 3, 1), ("NM", 0, 3), ("SC", 0, 1), ("EX", 0, 3, 0), ("EX", 0, 3, 1),
+    ("RM", 0, 2, 0), ("RM", 0, 2, 1), ("NM", 0, 2), ("SC", 0, 0), ("EX", 0, 2, 0), ("EX", 0, 2, 1), ("RM", 0, 1),
+    ("NM", 0, 1), ("RC", 0, 3), ("NO", 0, 3, 0), ("NO", 0, 3, 1), ("EX", 0, 1, 0), ("EX", 0, 1, 1), ("RM", 0, 0),
+    ("NM", 0, 0), ("RC", 0, 2), ("NO", 0, 2, 0), ("NO", 0, 2, 1), ("EX", 0, 0, 0), ("EX", 0, 0, 1), ("TX", 0, 0),
+    ("CX", 0, 0, "s"), ("TX", 0, 1), ("CX", 0, 1, "s"), ("TW", 0), ("CW", 0, "v"), ("TW", 1), ("CW", 1, "s"),
+    ("QX", 0), ("TW", 2), ("CW", 2, "v"), ("RC", 0, 1), ("NO", 0, 1, 0), ("NO", 0, 1, 1), ("RC", 0, 0),
+    ("NO", 0, 0, 0), ("NO", 0, 0, 1), ("TW", 3), ("CW", 3, "s"), ("QW", 0), ("QW", 1), ("MV", 0, 0),
+    ("CV", 0, 0, "s"), ("MV", 0, 1), ("CV", 0, 1, "v"), ("MV", 0, 2), ("CV", 0, 2, "s"), ("MV", 0, 3),
+    ("CV", 0, 3, "s"), ("MV", 0, 4), ("CV", 0, 4, "v"), ("MV", 0, 5), ("CV", 0, 5, "s"), ("QV", 0, 0), ("MV", 0, 6),
+    ("CV", 0, 6, "s"), ("MV", 0, 7), ("CV", 0, 7, "v"), ("QV", 0, 1), ("TX", 1, 0), ("CX", 1, 0, "s"), ("TX", 1, 1),
+    ("CX", 1, 1, "s"), ("TQ", 1, 0), ("CQ", 1, 0, "v"), ("TQ", 1, 1), ("CQ", 1, 1, "s"), ("QX", 1), ("SC", 1, 3, 0),
+    ("SC", 1, 3, 1), ("SC", 1, 2, 0), ("SC", 1, 2, 1), ("RM", 1, 3, 0), ("RM", 1, 3, 1), ("NM", 1, 3), ("SC", 1, 1),
+    ("EX", 1, 3, 0), ("EX", 1, 3, 1), ("RM", 1, 2, 0), ("RM", 1, 2, 1), ("NM", 1, 2), ("SC", 1, 0), ("EX", 1, 2, 0),
+    ("EX", 1, 2, 1), ("RM", 1, 1), ("NM", 1, 1), ("RC", 1, 3), ("NO", 1, 3, 0), ("NO", 1, 3, 1), ("EX", 1, 1, 0),
+    ("EX", 1, 1, 1), ("RM", 1, 0), ("NM", 1, 0), ("RC", 1, 2), ("NO", 1, 2, 0), ("NO", 1, 2, 1), ("EX", 1, 0, 0),
+    ("EX", 1, 0, 1), ("TA", 0, 0), ("CA", 0, 0, "v"), ("RC", 1, 1), ("NO", 1, 1, 0), ("NO", 1, 1, 1), ("RC", 1, 0),
+    ("NO", 1, 0, 0), ("NO", 1, 0, 1), ("TA", 0, 1), ("CA", 0, 1, "v"), ("TA", 0, 2), ("CA", 0, 2, "s"), ("QA", 0, 0),
+    ("TX", 2, 0), ("CX", 2, 0, "s"), ("TX", 2, 1), ("CX", 2, 1, "s"), ("QA", 0, 1), ("TQ", 2, 0), ("CQ", 2, 0, "v"),
+    ("TQ", 2, 1), ("CQ", 2, 1, "s"), ("QX", 2), ("MV", 1, 0), ("CV", 1, 0, "s"), ("MV", 1, 1), ("CV", 1, 1, "v"),
+    ("MV", 1, 2), ("CV", 1, 2, "s"), ("MV", 1, 3), ("CV", 1, 3, "s"), ("MV", 1, 4), ("CV", 1, 4, "v"), ("MV", 1, 5),
+    ("CV", 1, 5, "s"), ("QV", 1, 0), ("MV", 1, 6), ("CV", 1, 6, "s"), ("MV", 1, 7), ("CV", 1, 7, "v"), ("FO", 0, 0),
+    ("CO", 0, 0, "s"), ("QV", 1, 1), ("FO", 0, 1), ("CO", 0, 1, "s"), ("ST", 0, 0), ("FO", 0, 2), ("CO", 0, 2, "v"),
+    ("FO", 0, 3), ("CO", 0, 3, "s"), ("ST", 0, 1), ("SC", 2, 3, 0), ("SC", 2, 3, 1), ("SC", 2, 2, 0), ("SC", 2, 2, 1),
+    ("RM", 2, 3, 0), ("RM", 2, 3, 1), ("NM", 2, 3), ("SC", 2, 1), ("EX", 2, 3, 0), ("EX", 2, 3, 1), ("RM", 2, 2, 0),
+    ("RM", 2, 2, 1), ("NM", 2, 2), ("SC", 2, 0), ("EX", 2, 2, 0), ("EX", 2, 2, 1), ("RM", 2, 1), ("NM", 2, 1),
+    ("RC", 2, 3), ("NO", 2, 3, 0), ("NO", 2, 3, 1), ("EX", 2, 1, 0), ("EX", 2, 1, 1), ("RM", 2, 0), ("NM", 2, 0),
+    ("RC", 2, 2), ("NO", 2, 2, 0), ("NO", 2, 2, 1), ("EX", 2, 0, 0), ("EX", 2, 0, 1), ("TA", 1, 0), ("CA", 1, 0, "v"),
+    ("RC", 2, 1), ("NO", 2, 1, 0), ("NO", 2, 1, 1), ("RC", 2, 0), ("NO", 2, 0, 0), ("NO", 2, 0, 1), ("TA", 1, 1),
+    ("CA", 1, 1, "v"), ("TA", 1, 2), ("CA", 1, 2, "s"), ("QA", 1, 0), ("TX", 3, 0), ("CX", 3, 0, "s"), ("TX", 3, 1),
+    ("CX", 3, 1, "s"), ("QA", 1, 1), ("TQ", 3, 0), ("CQ", 3, 0, "v"), ("TQ", 3, 1), ("CQ", 3, 1, "s"), ("QX", 3),
+    ("MV", 2, 0), ("CV", 2, 0, "s"), ("MV", 2, 1), ("CV", 2, 1, "v"), ("MV", 2, 2), ("CV", 2, 2, "s"), ("MV", 2, 3),
+    ("CV", 2, 3, "s"), ("MV", 2, 4), ("CV", 2, 4, "v"), ("MV", 2, 5), ("CV", 2, 5, "s"), ("QV", 2, 0), ("MV", 2, 6),
+    ("CV", 2, 6, "s"), ("MV", 2, 7), ("CV", 2, 7, "v"), ("FO", 1, 0), ("CO", 1, 0, "s"), ("QV", 2, 1), ("FO", 1, 1),
+    ("CO", 1, 1, "s"), ("ST", 1, 0), ("FO", 1, 2), ("CO", 1, 2, "v"), ("FO", 1, 3), ("CO", 1, 3, "s"), ("ST", 1, 1),
+    ("SC", 3, 3, 0), ("SC", 3, 3, 1), ("SC", 3, 2, 0), ("SC", 3, 2, 1), ("RM", 3, 3, 0), ("RM", 3, 3, 1),
+    ("NM", 3, 3), ("SC", 3, 1), ("EX", 3, 3, 0), ("EX", 3, 3, 1), ("RM", 3, 2, 0), ("RM", 3, 2, 1), ("NM", 3, 2),
+    ("SC", 3, 0), ("EX", 3, 2, 0), ("EX", 3, 2, 1), ("RM", 3, 1), ("NM", 3, 1), ("RC", 3, 3), ("NO", 3, 3, 0),
+    ("NO", 3, 3, 1), ("EX", 3, 1, 0), ("EX", 3, 1, 1), ("RM", 3, 0), ("NM", 3, 0), ("RC", 3, 2), ("NO", 3, 2, 0),
+    ("NO", 3, 2, 1), ("EX", 3, 0, 0), ("EX", 3, 0, 1), ("TA", 2, 0), ("CA", 2, 0, "v"), ("RC", 3, 1), ("NO", 3, 1, 0),
+    ("NO", 3, 1, 1), ("RC", 3, 0), ("NO", 3, 0, 0), ("NO", 3, 0, 1), ("TA", 2, 1), ("CA", 2, 1, "v"), ("TA", 2, 2),
+    ("CA", 2, 2, "s"), ("QA", 2, 0), ("TX", 4, 0), ("CX", 4, 0, "s"), ("TX", 4, 1), ("CX", 4, 1, "s"), ("QA", 2, 1),
+    ("TQ", 4, 0), ("CQ", 4, 0, "v"), ("TQ", 4, 1), ("CQ", 4, 1, "s"), ("QX", 4), ("MV", 3, 0), ("CV", 3, 0, "s"),
+    ("MV", 3, 1), ("CV", 3, 1, "v"), ("MV", 3, 2), ("CV", 3, 2, "s"), ("MV", 3, 3), ("CV", 3, 3, "s"), ("MV", 3, 4),
+    ("CV", 3, 4, "v"), ("MV", 3, 5), ("CV", 3, 5, "s"), ("QV", 3, 0), ("MV", 3, 6), ("CV", 3, 6, "s"), ("MV", 3, 7),
+    ("CV", 3, 7, "v"), ("FO", 2, 0), ("CO", 2, 0, "s"), ("QV", 3, 1), ("FO", 2, 1), ("CO", 2, 1, "s"), ("ST", 2, 0),
+    ("FO", 2, 2), ("CO", 2, 2, "v"), ("FO", 2, 3), ("CO", 2, 3, "s"), ("ST", 2, 1), ("SC", 4, 3, 0), ("SC", 4, 3, 1),
+    ("SC", 4, 2, 0), ("SC", 4, 2, 1), ("RM", 4, 3, 0), ("RM", 4, 3, 1), ("NM", 4, 3), ("SC", 4, 1), ("EX", 4, 3, 0),
+    ("EX", 4, 3, 1), ("RM", 4, 2, 0), ("RM", 4, 2, 1), ("NM", 4, 2), ("SC", 4, 0), ("EX", 4, 2, 0), ("EX", 4, 2, 1),
+    ("RM", 4, 1), ("NM", 4, 1), ("RC", 4, 3), ("NO", 4, 3, 0), ("NO", 4, 3, 1), ("EX", 4, 1, 0), ("EX", 4, 1, 1),
+    ("RM", 4, 0), ("NM", 4, 0), ("RC", 4, 2), ("NO", 4, 2, 0), ("NO", 4, 2, 1), ("EX", 4, 0, 0), ("EX", 4, 0, 1),
+    ("TA", 3, 0), ("CA", 3, 0, "v"), ("RC", 4, 1), ("NO", 4, 1, 0), ("NO", 4, 1, 1), ("RC", 4, 0), ("NO", 4, 0, 0),
+    ("NO", 4, 0, 1), ("TA", 3, 1), ("CA", 3, 1, "v"), ("TA", 3, 2), ("CA", 3, 2, "s"), ("QA", 3, 0), ("TX", 5, 0),
+    ("CX", 5, 0, "s"), ("TX", 5, 1), ("CX", 5, 1, "s"), ("QA", 3, 1), ("TQ", 5, 0), ("CQ", 5, 0, "v"), ("TQ", 5, 1),
+    ("CQ", 5, 1, "s"), ("QX", 5), ("MV", 4, 0), ("CV", 4, 0, "s"), ("MV", 4, 1), ("CV", 4, 1, "v"), ("MV", 4, 2),
+    ("CV", 4, 2, "s"), ("MV", 4, 3), ("CV", 4, 3, "s"), ("MV", 4, 4), ("CV", 4, 4, "v"), ("MV", 4, 5),
+    ("CV", 4, 5, "s"), ("QV", 4, 0), ("MV", 4, 6), ("CV", 4, 6, "s"), ("MV", 4, 7), ("CV", 4, 7, "v"), ("FO", 3, 0),
+    ("CO", 3, 0, "s"), ("QV", 4, 1), ("FO", 3, 1), ("CO", 3, 1, "s"), ("ST", 3, 0), ("FO", 3, 2), ("CO", 3, 2, "v"),
+    ("FO", 3, 3), ("CO", 3, 3, "s"), ("ST", 3, 1), ("SC", 5, 3, 0), ("SC", 5, 3, 1), ("SC", 5, 2, 0), ("SC", 5, 2, 1),
+    ("RM", 5, 3, 0), ("RM", 5, 3, 1), ("NM", 5, 3), ("SC", 5, 1), ("EX", 5, 3, 0), ("EX", 5, 3, 1), ("RM", 5, 2, 0),
+    ("RM", 5, 2, 1), ("NM", 5, 2), ("SC", 5, 0), ("EX", 5, 2, 0), ("EX", 5, 2, 1), ("RM", 5, 1), ("NM", 5, 1),
+    ("RC", 5, 3), ("NO", 5, 3, 0), ("NO", 5, 3, 1), ("EX", 5, 1, 0), ("EX", 5, 1, 1), ("RM", 5, 0), ("NM", 5, 0),
+    ("RC", 5, 2), ("NO", 5, 2, 0), ("NO", 5, 2, 1), ("EX", 5, 0, 0), ("EX", 5, 0, 1), ("TA", 4, 0), ("CA", 4, 0, "v"),
+    ("RC", 5, 1), ("NO", 5, 1, 0), ("NO", 5, 1, 1), ("RC", 5, 0), ("NO", 5, 0, 0), ("NO", 5, 0, 1), ("TA", 4, 1),
+    ("CA", 4, 1, "v"), ("TA", 4, 2), ("CA", 4, 2, "s"), ("QA", 4, 0), ("TX", 6, 0), ("CX", 6, 0, "s"), ("TX", 6, 1),
+    ("CX", 6, 1, "s"), ("QA", 4, 1), ("TQ", 6, 0), ("CQ", 6, 0, "v"), ("TQ", 6, 1), ("CQ", 6, 1, "s"), ("QX", 6),
+    ("MV", 5, 0), ("CV", 5, 0, "s"), ("MV", 5, 1), ("CV", 5, 1, "v"), ("MV", 5, 2), ("CV", 5, 2, "s"), ("MV", 5, 3),
+    ("CV", 5, 3, "s"), ("MV", 5, 4), ("CV", 5, 4, "v"), ("MV", 5, 5), ("CV", 5, 5, "s"), ("QV", 5, 0), ("MV", 5, 6),
+    ("CV", 5, 6, "s"), ("MV", 5, 7), ("CV", 5, 7, "v"), ("FO", 4, 0), ("CO", 4, 0, "s"), ("QV", 5, 1), ("FO", 4, 1),
+    ("CO", 4, 1, "s"), ("ST", 4, 0), ("FO", 4, 2), ("CO", 4, 2, "v"), ("FO", 4, 3), ("CO", 4, 3, "s"), ("ST", 4, 1),
+    ("SC", 6, 3, 0), ("SC", 6, 3, 1), ("SC", 6, 2, 0), ("SC", 6, 2, 1), ("RM", 6, 3, 0), ("RM", 6, 3, 1),
+    ("NM", 6, 3), ("SC", 6, 1), ("EX", 6, 3, 0), ("EX", 6, 3, 1), ("RM", 6, 2, 0), ("RM", 6, 2, 1), ("NM", 6, 2),
+    ("SC", 6, 0), ("EX", 6, 2, 0), ("EX", 6, 2, 1), ("RM", 6, 1), ("NM", 6, 1), ("RC", 6, 3), ("NO", 6, 3, 0),
+    ("NO", 6, 3, 1), ("EX", 6, 1, 0), ("EX", 6, 1, 1), ("RM", 6, 0), ("NM", 6, 0), ("RC", 6, 2), ("NO", 6, 2, 0),
+    ("NO", 6, 2, 1), ("EX", 6, 0, 0), ("EX", 6, 0, 1), ("TA", 5, 0), ("CA", 5, 0, "v"), ("RC", 6, 1), ("NO", 6, 1, 0),
+    ("NO", 6, 1, 1), ("RC", 6, 0), ("NO", 6, 0, 0), ("NO", 6, 0, 1), ("TA", 5, 1), ("CA", 5, 1, "v"), ("TA", 5, 2),
+    ("CA", 5, 2, "s"), ("QA", 5, 0), ("TX", 7, 0), ("CX", 7, 0, "s"), ("TX", 7, 1), ("CX", 7, 1, "s"), ("QA", 5, 1),
+    ("TQ", 7, 0), ("CQ", 7, 0, "v"), ("TQ", 7, 1), ("CQ", 7, 1, "s"), ("QX", 7), ("MV", 6, 0), ("CV", 6, 0, "s"),
+    ("MV", 6, 1), ("CV", 6, 1, "v"), ("MV", 6, 2), ("CV", 6, 2, "s"), ("MV", 6, 3), ("CV", 6, 3, "s"), ("MV", 6, 4),
+    ("CV", 6, 4, "v"), ("MV", 6, 5), ("CV", 6, 5, "s"), ("QV", 6, 0), ("MV", 6, 6), ("CV", 6, 6, "s"), ("MV", 6, 7),
+    ("CV", 6, 7, "v"), ("FO", 5, 0), ("CO", 5, 0, "s"), ("QV", 6, 1), ("FO", 5, 1), ("CO", 5, 1, "s"), ("ST", 5, 0),
+    ("FO", 5, 2), ("CO", 5, 2, "v"), ("FO", 5, 3), ("CO", 5, 3, "s"), ("ST", 5, 1), ("SC", 7, 3, 0), ("SC", 7, 3, 1),
+    ("SC", 7, 2, 0), ("SC", 7, 2, 1), ("RM", 7, 3, 0), ("RM", 7, 3, 1), ("NM", 7, 3), ("SC", 7, 1), ("EX", 7, 3, 0),
+    ("EX", 7, 3, 1), ("RM", 7, 2, 0), ("RM", 7, 2, 1), ("NM", 7, 2), ("SC", 7, 0), ("EX", 7, 2, 0), ("EX", 7, 2, 1),
+    ("RM", 7, 1), ("NM", 7, 1), ("RC", 7, 3), ("NO", 7, 3, 0), ("NO", 7, 3, 1), ("EX", 7, 1, 0), ("EX", 7, 1, 1),
+    ("RM", 7, 0), ("NM", 7, 0), ("RC", 7, 2), ("NO", 7, 2, 0), ("NO", 7, 2, 1), ("EX", 7, 0, 0), ("EX", 7, 0, 1),
+    ("TA", 6, 0), ("CA", 6, 0, "v"), ("RC", 7, 1), ("NO", 7, 1, 0), ("NO", 7, 1, 1), ("RC", 7, 0), ("NO", 7, 0, 0),
+    ("NO", 7, 0, 1), ("TA", 6, 1), ("CA", 6, 1, "v"), ("TA", 6, 2), ("CA", 6, 2, "s"), ("QA", 6, 0), ("QA", 6, 1),
+    ("MV", 7, 0), ("CV", 7, 0, "s"), ("MV", 7, 1), ("CV", 7, 1, "v"), ("MV", 7, 2), ("CV", 7, 2, "s"), ("MV", 7, 3),
+    ("CV", 7, 3, "s"), ("MV", 7, 4), ("CV", 7, 4, "v"), ("MV", 7, 5), ("CV", 7, 5, "s"), ("QV", 7, 0), ("MV", 7, 6),
+    ("CV", 7, 6, "s"), ("MV", 7, 7), ("CV", 7, 7, "v"), ("QV", 7, 1), ("TA", 7, 0), ("CA", 7, 0, "v"), ("TA", 7, 1),
+    ("CA", 7, 1, "v"), ("TA", 7, 2), ("CA", 7, 2, "s"), ("QA", 7, 0), ("QA", 7, 1), ("FO", 6, 0), ("CO", 6, 0, "s"),
+    ("FO", 6, 1), ("CO", 6, 1, "s"), ("ST", 6, 0), ("FO", 6, 2), ("CO", 6, 2, "v"), ("FO", 6, 3), ("CO", 6, 3, "s"),
+    ("ST", 6, 1), ("FO", 7, 0), ("CO", 7, 0, "s"), ("FO", 7, 1), ("CO", 7, 1, "s"), ("ST", 7, 0), ("FO", 7, 2),
+    ("CO", 7, 2, "v"), ("FO", 7, 3), ("CO", 7, 3, "s"), ("ST", 7, 1),
+)
+
+
+def tile_multiheadattention_pa_t_kernel(tc, q, k, x, Wv, mask, out):
+    nc = tc.nc
+    with ExitStack() as ctx:
+        if MANUAL:
+            ctx.enter_context(tc.manual_schedule())
+        const = ctx.enter_context(tc.tile_pool(name="const", bufs=1))
+        loads = ctx.enter_context(tc.tile_pool(name="loads", bufs=1))
+        work = ctx.enter_context(tc.tile_pool(name="work", bufs=2))
+        small = ctx.enter_context(tc.tile_pool(name="small", bufs=8))
+        psum = ctx.enter_context(tc.psum_pool(name="psum", bufs=8))
+        st = {}
+
+        def copy(eng, dst, src):
+            if eng == "v":
+                nc.vector.tensor_copy(out=dst, in_=src)
+            else:
+                nc.scalar.copy(out=dst, in_=src)
+
+        x_sb = [loads.tile([P, NT * D], BF16, name="x_sb%d" % b) for b in range(B)]
+        q_sb = [loads.tile([P, NT * H * L], BF16, name="q_sb%d" % b) for b in range(B)]
+        k_sb = [loads.tile([P, NT * H * L], BF16, name="k_sb%d" % b) for b in range(B)]
+        wv_sb = loads.tile([P, 8 * D], BF16, name="wv_sb")
+        mk_i = loads.tile([P, NT * 2 * P], I32, name="mk_i")
+        mask32 = mask.bitcast(I32)
+        wv_view = Wv.rearrange("(r p) d -> p r d", p=P)
+
+        def LX(b):
+            nc.sync.dma_start(
+                out=x_sb[b][:].rearrange("p (a d) -> p a d", a=NT), in_=x[b].rearrange("(a p) d -> p a d", p=P)
+            )
+
+        def LQ(b):
+            nc.sync.dma_start(
+                out=q_sb[b][:].rearrange("p (a c) -> p a c", a=NT), in_=q[b].rearrange("(a p) h l -> p a (h l)", p=P)
+            )
+
+        def LK(b):
+            nc.sync.dma_start(
+                out=k_sb[b][:].rearrange("p (a c) -> p a c", a=NT), in_=k[b].rearrange("(a p) h l -> p a (h l)", p=P)
+            )
+
+        def LW(half):
+            nc.sync.dma_start(
+                out=wv_sb[:, half * 4 * D : (half + 1) * 4 * D].rearrange("p (r d) -> p r d", r=4),
+                in_=wv_view[:, half * 4 : (half + 1) * 4, :],
+            )
+
+        def LM():
+            for it in range(NT):
+                nc.sync.dma_start(
+                    out=mk_i[:, it * 2 * P : (it + 1) * 2 * P],
+                    in_=mask32[0, it * P : (it + 1) * P, it * 2 * P : (it + 1) * 2 * P],
+                )
+
+        id_f = const.tile([P, P], F32, name="id_f")
+        id_bf = const.tile([P, P], BF16, name="id_bf")
+        mk_f = const.tile([P, NT * P], F32, name="mk_f")
+        mb = const.tile([P, NT * P], BF16, name="mb")
+        a_sb = [[const.tile([P, H * AW[it]], BF16, name="a_sb%d_%d" % (par, it)) for it in range(NT)] for par in range(2)]
+        wvg = const.tile([P, 8 * D], BF16, name="wvg", align_bytes=64)
+        wvw = const.tile([P, H * D], U32, name="wvw", align_bytes=64)
+        wvs = const.tile([P, H * D], U8, name="wvs", align_bytes=64)
+
+        def INIT():
+            make_identity(nc, id_bf[:])
+            make_identity(nc, id_f[:])
+            for par in range(2):
+                for it in range(NT):
+                    n = (it + 1) * P
+                    if n < AW[it]:
+                        nc.gpsimd.memset(a_sb[par][it][:].rearrange("p (h j) -> p h j", h=H)[:, :, n:], 0.0)
+
+        def MB():
+            nc.vector.tensor_copy(out=mk_f[:], in_=mk_i[:].rearrange("p (j w) -> p j w", w=2)[:, :, 0])
+            nc.vector.tensor_scalar(out=mb[:], in0=mk_f[:], scalar1=1.0, scalar2=BIG, op0=ALU.subtract, op1=ALU.mult)
+
+        def TW(g):
+            src = wv_sb[:].bitcast(F32)
+            ps = psum.tile([P, 2, 2, P], F32, name="ps_wv", tag="bank")
+            for rr in range(2):
+                for u in range(2):
+                    o = (2 * g + rr) * 256 + u * P
+                    nc.tensor.transpose(ps[:, rr, u, :], src[:, o : o + P], id_f[:])
+            st[("TW", g)] = ps
+
+        def CW(g, eng):
+            dst = wvg[:].bitcast(F32).rearrange("w (r c u) -> w r c u", r=8, u=2)
+            copy(eng, dst[:, 2 * g : 2 * g + 2, :, :], st[("TW", g)][:].rearrange("w r u c -> w r c u"))
+
+        def QW(h):
+            nc.vector.quantize_mx(
+                out=wvw[:, h * D : (h + 1) * D].bitcast(FP8X4),
+                scales=wvs[:, h * D : (h + 1) * D],
+                in_=wvg[:, h * 4 * D : (h + 1) * 4 * D],
+            )
+
+        def TX(b, g):
+            src = x_sb[b][:].bitcast(F32)
+            ps = psum.tile([P, 2, 2, P], F32, name="ps_x", tag="bank")
+            for a2 in range(2):
+                for u in range(2):
+                    o = (2 * g + a2) * 256 + u * P
+                    nc.tensor.transpose(ps[:, a2, u, :], src[:, o : o + P], id_f[:])
+            st[("TX", b, g)] = ps
+
+        def CX(b, g, eng):
+            if ("xg", b) not in st:
+                xg_new = work.tile([P, NT * D], BF16, name="xg", align_bytes=64)
+                st[("xg", b)] = xg_new
+            dst = st[("xg", b)][:].bitcast(F32).rearrange("w (a p u) -> w a p u", a=NT, u=2)
+            copy(eng, dst[:, 2 * g : 2 * g + 2, :, :], st[("TX", b, g)][:].rearrange("w a u p -> w a p u"))
+
+        def QX(b):
+            xw = work.tile([P, S], U32, name="xw", align_bytes=64)
+            xs = work.tile([P, S], U8, name="xs", align_bytes=64)
+            nc.vector.quantize_mx(out=xw[:].bitcast(FP8X4), scales=xs[:], in_=st[("xg", b)][:])
+            st[("xw", b)] = (xw, xs)
+
+        def TQ(b, i):
+            src = (q_sb[b], k_sb[b])[i]
+            ps = psum.tile([P, H, NT, P], BF16, name="ps_qk", tag="bank")
+            for h in range(H):
+                for a in range(NT):
+                    o = a * H * L + h * L
+                    nc.tensor.transpose(ps[:, h, a, :], src[:, o : o + L], id_bf[:])
+            st[("TQ", b, i)] = ps
+
+        def CQ(b, i, eng):
+            dst = work.tile([P, H * S], BF16, name="qkT%d" % i)
+            copy(eng, dst[:], st[("TQ", b, i)][:].rearrange("l h a p -> l (h a p)"))
+            st[("qk", b, i)] = dst
+
+        def sc_head(b, it, h, view):
+            qT = st[("qk", b, 0)]
+            kT = st[("qk", b, 1)]
+            n = (it + 1) * P
+            lhsT = qT[:, h * S + it * P : h * S + (it + 1) * P]
+            if it > 0:
+                nc.tensor.matmul(out=view[:, 0 : it * P], lhsT=lhsT, rhs=kT[:, h * S : h * S + it * P], start=True, stop=True)
+            nc.tensor.matmul(out=view[:, it * P : n], lhsT=lhsT, rhs=kT[:, h * S + it * P : h * S + n], start=True, stop=False)
+            nc.tensor.matmul(out=view[:, it * P : n], lhsT=id_bf[:], rhs=mb[:, it * P : (it + 1) * P], start=False, stop=True)
+
+        def SC(b, it, h=0):
+            n = (it + 1) * P
+            if it < 2:
+                ps = psum.tile([P, H, n], F32, name="ps_s", tag="bank")
+                for hh in range(H):
+                    sc_head(b, it, hh, ps[:, hh, :])
+                    st[("S", b, it, hh)] = ps[:, hh, :]
+                st[("S2", b, it)] = ps
+            else:
+                ps1 = psum.tile([P, n], F32, name="ps_s1", tag="bank")
+                sc_head(b, it, h, ps1[:])
+                st[("S", b, it, h)] = ps1[:]
+
+        def RM(b, it, h=0):
+            if ("mx", b, it) not in st:
+                mx_new = small.tile([P, H], F32, name="mx")
+                st[("mx", b, it)] = mx_new
+            mx = st[("mx", b, it)]
+            if it < 2:
+                nc.vector.tensor_reduce(out=mx[:], in_=st[("S2", b, it)][:], axis=AX.X, op=ALU.max)
+            else:
+                nc.vector.tensor_reduce(out=mx[:, h : h + 1], in_=st[("S", b, it, h)], axis=AX.X, op=ALU.max)
+
+        def NM(b, it):
+            nm = small.tile([P, H], F32, name="nm")
+            nc.vector.tensor_scalar(out=nm[:], in0=st[("mx", b, it)][:], scalar1=-SCALE, scalar2=None, op0=ALU.mult)
+            st[("nm", b, it)] = nm
+
+        def EX(b, it, h):
+            n = (it + 1) * P
+            if ("e", b, it) not in st:
+                e_new = work.tile([P, H * n], F32, name="e_sb%d" % it)
+                sm_new = small.tile([P, H], F32, name="sm")
+                st[("e", b, it)] = (e_new, sm_new)
+            e_sb, sm = st[("e", b, it)]
+            nc.scalar.activation(
+                out=e_sb[:, h * n : (h + 1) * n],
+                in_=st[("S", b, it, h)],
+                func=ACT.Exp,
+                bias=st[("nm", b, it)][:, h : h + 1],
+                scale=SCALE,
+                accum_out=sm[:, h : h + 1],
+            )
+
+        def RC(b, it):
+            rc = small.tile([P, H], F32, name="rc")
+            nc.vector.reciprocal(out=rc[:], in_=st[("e", b, it)][1][:])
+            st[("rc", b, it)] = rc
+
+        def NO(b, it, h):
+            n = (it + 1) * P
+            nc.gpsimd.tensor_scalar(
+                out=a_sb[b % 2][it][:, h * AW[it] : h * AW[it] + n],
+                in0=st[("e", b, it)][0][:, h * n : (h + 1) * n],
+                scalar1=st[("rc", b, it)][:, h : h + 1],
+                scalar2=0.0,
+                op0=ALU.mult,
+                op1=ALU.add,
+            )
+
+        def MV(b, j):
+            xw, xs = st[("xw", b)]
+            U = j // 4
+            c = j % 4
+            ps = psum.tile([P, 4, P], F32, name="ps_v", tag="bank")
+            for h in range(H):
+                for blk in range(2):
+                    a = 2 * U + blk
+                    col = h * D + c * P
+                    nc.tensor.matmul_mx(
+                        out=ps[:, 2 * h + blk, :],
+                        lhsT=xw[:, a * P : (a + 1) * P].bitcast(FP8X4),
+                        lhsT_scale=xs[:, a * P : (a + 1) * P],
+                        rhs=wvw[:, col : col + P].bitcast(FP8X4),
+                        rhs_scale=wvs[:, col : col + P],
+                        start=True,
+                        stop=True,
+                    )
+            st[("MV", b, j)] = ps
+
+        def CV(b, j, eng):
+            if ("vg", b) not in st:
+                vg_new = work.tile([P, 2 * 4 * D], BF16, name="vg", align_bytes=64)
+                st[("vg", b)] = vg_new
+            o = j * 4 * P
+            copy(
+                eng,
+                st[("vg", b)][:, o : o + 4 * P].rearrange("p (d t) -> p d t", t=4),
+                st[("MV", b, j)][:].rearrange("p t d -> p d t"),
+            )
+
+        def QV(b, U):
+            if ("vw", b) not in st:
+                vw_new = work.tile([P, 2 * D], U32, name="vw", align_bytes=64)
+                vs_new = work.tile([P, 2 * D], U8, name="vs", align_bytes=64)
+                st[("vw", b)] = (vw_new, vs_new)
+            vw, vs = st[("vw", b)]
+            nc.vector.quantize_mx(
+                out=vw[:, U * D : (U + 1) * D].bitcast(FP8X4),
+                scales=vs[:, U * D : (U + 1) * D],
+                in_=st[("vg", b)][:, U * 4 * D : (U + 1) * 4 * D],
+            )
+
+        def TA(b, g):
+            ps = psum.tile([P, 2, 4, P], BF16, name="ps_a", tag="bank")
+            for gi in range(2):
+                it, U = SEGS[g][gi]
+                at = a_sb[b % 2][it]
+                for h in range(H):
+                    for blk in range(2):
+                        o = h * AW[it] + (2 * U + blk) * P
+                        nc.tensor.transpose(ps[:, gi, 2 * h + blk, :], at[:, o : o + P], id_bf[:])
+            st[("TA", b, g)] = ps
+
+        def CA(b, g, eng):
+            if ("ag", b) not in st:
+                ag_new = work.tile([P, 6 * 4 * P], BF16, name="ag", align_bytes=64)
+                st[("ag", b)] = ag_new
+            copy(
+                eng,
+                st[("ag", b)][:, g * 1024 : (g + 1) * 1024].rearrange("p (g i t) -> p g i t", g=2, t=4),
+                st[("TA", b, g)][:].rearrange("p g t i -> p g i t"),
+            )
+
+        def QA(b, part):
+            if ("aw", b) not in st:
+                aw_new = work.tile([P, 6 * P], U32, name="aw", align_bytes=64)
+                as_new = work.tile([P, 6 * P], U8, name="asc", align_bytes=64)
+                st[("aw", b)] = (aw_new, as_new)
+            aw, asc = st[("aw", b)]
+            lo, hi = ((0, 256), (256, 768))[part]
+            nc.vector.quantize_mx(out=aw[:, lo:hi].bitcast(FP8X4), scales=asc[:, lo:hi], in_=st[("ag", b)][:, 4 * lo : 4 * hi])
+
+        def FO(b, it):
+            aw, asc = st[("aw", b)]
+            vw, vs = st[("vw", b)]
+            po = psum.tile([P, D], F32, name="po", tag="bank")
+            passes = [(it, 0)] + ([(it + 2, 1)] if it >= 2 else [])
+            for i, (seg, U) in enumerate(passes):
+                nc.tensor.matmul_mx(
+                    out=po[:],
+                    lhsT=aw[:, seg * P : (seg + 1) * P].bitcast(FP8X4),
+                    lhsT_scale=asc[:, seg * P : (seg + 1) * P],
+                    rhs=vw[:, U * D : (U + 1) * D].bitcast(FP8X4),
+                    rhs_scale=vs[:, U * D : (U + 1) * D],
+                    start=(i == 0),
+                    stop=(i == len(passes) - 1),
+                )
+            st[("FO", b, it)] = po
+
+        def CO(b, it, eng):
+            if ("o", b) not in st:
+                o_new = work.tile([P, NT * D], F32, name="o_sb")
+                st[("o", b)] = o_new
+            copy(eng, st[("o", b)][:, it * D : (it + 1) * D], st[("FO", b, it)][:])
+
+        def ST(b, pr):
+            nc.sync.dma_start(
+                out=out[b, 2 * pr * P : (2 * pr + 2) * P, :].rearrange("(a p) d -> p a d", p=P),
+                in_=st[("o", b)][:, 2 * pr * D : (2 * pr + 2) * D].rearrange("p (a d) -> p a d", a=2),
+            )
+
+        def ST4(b, it):
+            nc.sync.dma_start(out=out[b, it * P : (it + 1) * P, :], in_=st[("o", b)][:, it * D : (it + 1) * D])
+
+        steps = {
+            "LX": LX, "LQ": LQ, "LK": LK, "LW": LW, "LM": LM, "INIT": INIT, "MB": MB, "TW": TW, "CW": CW, "QW": QW,
+            "TX": TX, "CX": CX, "QX": QX, "TQ": TQ, "CQ": CQ, "SC": SC, "RM": RM, "NM": NM, "EX": EX, "RC": RC,
+            "NO": NO, "MV": MV, "CV": CV, "QV": QV, "TA": TA, "CA": CA, "QA": QA, "FO": FO, "CO": CO, "ST": ST, "ST4": ST4,
+        }
+        for step in ORDER:
+            steps[step[0]](*step[1:])

@@ -25,104 +25,108 @@ AW = (256, 256, 512, 512)
 SEGS = (((0, 0), (1, 0)), ((2, 0), (3, 0)), ((2, 1), (3, 1)))
 
 ORDER = (
-    ("INIT",), ("LQ", 0), ("LK", 0), ("LM",), ("LX", 0), ("LW", 0), ("LW", 1), ("LX", 1), ("LQ", 1), ("LK", 1),
+    ("INIT",), ("LQ", 0), ("LK", 0), ("LM",), ("LX", 0), ("LW", 0), ("LW", 1), ("LQ", 1), ("LK", 1), ("LX", 1),
     ("LX", 2), ("LQ", 2), ("LK", 2), ("LX", 3), ("LQ", 3), ("LK", 3), ("LX", 4), ("LQ", 4), ("LK", 4), ("LX", 5),
     ("LQ", 5), ("LK", 5), ("LX", 6), ("LQ", 6), ("LK", 6), ("LX", 7), ("LQ", 7), ("LK", 7), ("TQ", 0, 0),
     ("CQ", 0, 0, "v"), ("TQ", 0, 1), ("CQ", 0, 1, "s"), ("MB",), ("SC", 0, 3, 0), ("SC", 0, 3, 1), ("SC", 0, 2, 0),
-    ("SC", 0, 2, 1), ("RM", 0, 3, 0), ("RM", 0, 3, 1), ("NM", 0, 3), ("SC", 0, 1), ("EX", 0, 3, 0), ("EX", 0, 3, 1),
-    ("RM", 0, 2, 0), ("RM", 0, 2, 1), ("NM", 0, 2), ("SC", 0, 0), ("EX", 0, 2, 0), ("EX", 0, 2, 1), ("RM", 0, 1),
-    ("NM", 0, 1), ("RC", 0, 3), ("NO", 0, 3, 0), ("NO", 0, 3, 1), ("EX", 0, 1, 0), ("EX", 0, 1, 1), ("RM", 0, 0),
-    ("NM", 0, 0), ("RC", 0, 2), ("NO", 0, 2, 0), ("NO", 0, 2, 1), ("EX", 0, 0, 0), ("EX", 0, 0, 1), ("TX", 0, 0),
-    ("CX", 0, 0, "s"), ("TX", 0, 1), ("CX", 0, 1, "s"), ("TW", 0), ("CW", 0, "v"), ("TW", 1), ("CW", 1, "s"),
-    ("QX", 0), ("TW", 2), ("CW", 2, "v"), ("RC", 0, 1), ("NO", 0, 1, 0), ("NO", 0, 1, 1), ("RC", 0, 0),
-    ("NO", 0, 0, 0), ("NO", 0, 0, 1), ("TW", 3), ("CW", 3, "s"), ("QW", 0), ("QW", 1), ("MV", 0, 0),
-    ("CV", 0, 0, "s"), ("MV", 0, 1), ("CV", 0, 1, "v"), ("MV", 0, 2), ("CV", 0, 2, "s"), ("MV", 0, 3),
-    ("CV", 0, 3, "s"), ("MV", 0, 4), ("CV", 0, 4, "v"), ("MV", 0, 5), ("CV", 0, 5, "s"), ("QV", 0, 0), ("MV", 0, 6),
-    ("CV", 0, 6, "s"), ("MV", 0, 7), ("CV", 0, 7, "v"), ("QV", 0, 1), ("TX", 1, 0), ("CX", 1, 0, "s"), ("TX", 1, 1),
-    ("CX", 1, 1, "s"), ("TQ", 1, 0), ("CQ", 1, 0, "v"), ("TQ", 1, 1), ("CQ", 1, 1, "s"), ("QX", 1), ("SC", 1, 3, 0),
-    ("SC", 1, 3, 1), ("SC", 1, 2, 0), ("SC", 1, 2, 1), ("RM", 1, 3, 0), ("RM", 1, 3, 1), ("NM", 1, 3), ("SC", 1, 1),
-    ("EX", 1, 3, 0), ("EX", 1, 3, 1), ("RM", 1, 2, 0), ("RM", 1, 2, 1), ("NM", 1, 2), ("SC", 1, 0), ("EX", 1, 2, 0),
-    ("EX", 1, 2, 1), ("RM", 1, 1), ("NM", 1, 1), ("RC", 1, 3), ("NO", 1, 3, 0), ("NO", 1, 3, 1), ("EX", 1, 1, 0),
-    ("EX", 1, 1, 1), ("RM", 1, 0), ("NM", 1, 0), ("RC", 1, 2), ("NO", 1, 2, 0), ("NO", 1, 2, 1), ("EX", 1, 0, 0),
-    ("EX", 1, 0, 1), ("TA", 0, 0), ("CA", 0, 0, "v"), ("RC", 1, 1), ("NO", 1, 1, 0), ("NO", 1, 1, 1), ("RC", 1, 0),
-    ("NO", 1, 0, 0), ("NO", 1, 0, 1), ("TA", 0, 1), ("CA", 0, 1, "v"), ("TA", 0, 2), ("CA", 0, 2, "s"), ("QA", 0, 0),
-    ("TX", 2, 0), ("CX", 2, 0, "s"), ("TX", 2, 1), ("CX", 2, 1, "s"), ("QA", 0, 1), ("TQ", 2, 0), ("CQ", 2, 0, "v"),
-    ("TQ", 2, 1), ("CQ", 2, 1, "s"), ("QX", 2), ("MV", 1, 0), ("CV", 1, 0, "s"), ("MV", 1, 1), ("CV", 1, 1, "v"),
-    ("MV", 1, 2), ("CV", 1, 2, "s"), ("MV", 1, 3), ("CV", 1, 3, "s"), ("MV", 1, 4), ("CV", 1, 4, "v"), ("MV", 1, 5),
-    ("CV", 1, 5, "s"), ("QV", 1, 0), ("MV", 1, 6), ("CV", 1, 6, "s"), ("MV", 1, 7), ("CV", 1, 7, "v"), ("FO", 0, 0),
-    ("CO", 0, 0, "s"), ("QV", 1, 1), ("FO", 0, 1), ("CO", 0, 1, "s"), ("ST", 0, 0), ("FO", 0, 2), ("CO", 0, 2, "v"),
-    ("FO", 0, 3), ("CO", 0, 3, "s"), ("ST", 0, 1), ("SC", 2, 3, 0), ("SC", 2, 3, 1), ("SC", 2, 2, 0), ("SC", 2, 2, 1),
-    ("RM", 2, 3, 0), ("RM", 2, 3, 1), ("NM", 2, 3), ("SC", 2, 1), ("EX", 2, 3, 0), ("EX", 2, 3, 1), ("RM", 2, 2, 0),
-    ("RM", 2, 2, 1), ("NM", 2, 2), ("SC", 2, 0), ("EX", 2, 2, 0), ("EX", 2, 2, 1), ("RM", 2, 1), ("NM", 2, 1),
-    ("RC", 2, 3), ("NO", 2, 3, 0), ("NO", 2, 3, 1), ("EX", 2, 1, 0), ("EX", 2, 1, 1), ("RM", 2, 0), ("NM", 2, 0),
-    ("RC", 2, 2), ("NO", 2, 2, 0), ("NO", 2, 2, 1), ("EX", 2, 0, 0), ("EX", 2, 0, 1), ("TA", 1, 0), ("CA", 1, 0, "v"),
-    ("RC", 2, 1), ("NO", 2, 1, 0), ("NO", 2, 1, 1), ("RC", 2, 0), ("NO", 2, 0, 0), ("NO", 2, 0, 1), ("TA", 1, 1),
-    ("CA", 1, 1, "v"), ("TA", 1, 2), ("CA", 1, 2, "s"), ("QA", 1, 0), ("TX", 3, 0), ("CX", 3, 0, "s"), ("TX", 3, 1),
-    ("CX", 3, 1, "s"), ("QA", 1, 1), ("TQ", 3, 0), ("CQ", 3, 0, "v"), ("TQ", 3, 1), ("CQ", 3, 1, "s"), ("QX", 3),
-    ("MV", 2, 0), ("CV", 2, 0, "s"), ("MV", 2, 1), ("CV", 2, 1, "v"), ("MV", 2, 2), ("CV", 2, 2, "s"), ("MV", 2, 3),
-    ("CV", 2, 3, "s"), ("MV", 2, 4), ("CV", 2, 4, "v"), ("MV", 2, 5), ("CV", 2, 5, "s"), ("QV", 2, 0), ("MV", 2, 6),
-    ("CV", 2, 6, "s"), ("MV", 2, 7), ("CV", 2, 7, "v"), ("FO", 1, 0), ("CO", 1, 0, "s"), ("QV", 2, 1), ("FO", 1, 1),
-    ("CO", 1, 1, "s"), ("ST", 1, 0), ("FO", 1, 2), ("CO", 1, 2, "v"), ("FO", 1, 3), ("CO", 1, 3, "s"), ("ST", 1, 1),
-    ("SC", 3, 3, 0), ("SC", 3, 3, 1), ("SC", 3, 2, 0), ("SC", 3, 2, 1), ("RM", 3, 3, 0), ("RM", 3, 3, 1),
-    ("NM", 3, 3), ("SC", 3, 1), ("EX", 3, 3, 0), ("EX", 3, 3, 1), ("RM", 3, 2, 0), ("RM", 3, 2, 1), ("NM", 3, 2),
-    ("SC", 3, 0), ("EX", 3, 2, 0), ("EX", 3, 2, 1), ("RM", 3, 1), ("NM", 3, 1), ("RC", 3, 3), ("NO", 3, 3, 0),
-    ("NO", 3, 3, 1), ("EX", 3, 1, 0), ("EX", 3, 1, 1), ("RM", 3, 0), ("NM", 3, 0), ("RC", 3, 2), ("NO", 3, 2, 0),
-    ("NO", 3, 2, 1), ("EX", 3, 0, 0), ("EX", 3, 0, 1), ("TA", 2, 0), ("CA", 2, 0, "v"), ("RC", 3, 1), ("NO", 3, 1, 0),
-    ("NO", 3, 1, 1), ("RC", 3, 0), ("NO", 3, 0, 0), ("NO", 3, 0, 1), ("TA", 2, 1), ("CA", 2, 1, "v"), ("TA", 2, 2),
-    ("CA", 2, 2, "s"), ("QA", 2, 0), ("TX", 4, 0), ("CX", 4, 0, "s"), ("TX", 4, 1), ("CX", 4, 1, "s"), ("QA", 2, 1),
-    ("TQ", 4, 0), ("CQ", 4, 0, "v"), ("TQ", 4, 1), ("CQ", 4, 1, "s"), ("QX", 4), ("MV", 3, 0), ("CV", 3, 0, "s"),
-    ("MV", 3, 1), ("CV", 3, 1, "v"), ("MV", 3, 2), ("CV", 3, 2, "s"), ("MV", 3, 3), ("CV", 3, 3, "s"), ("MV", 3, 4),
-    ("CV", 3, 4, "v"), ("MV", 3, 5), ("CV", 3, 5, "s"), ("QV", 3, 0), ("MV", 3, 6), ("CV", 3, 6, "s"), ("MV", 3, 7),
-    ("CV", 3, 7, "v"), ("FO", 2, 0), ("CO", 2, 0, "s"), ("QV", 3, 1), ("FO", 2, 1), ("CO", 2, 1, "s"), ("ST", 2, 0),
-    ("FO", 2, 2), ("CO", 2, 2, "v"), ("FO", 2, 3), ("CO", 2, 3, "s"), ("ST", 2, 1), ("SC", 4, 3, 0), ("SC", 4, 3, 1),
-    ("SC", 4, 2, 0), ("SC", 4, 2, 1), ("RM", 4, 3, 0), ("RM", 4, 3, 1), ("NM", 4, 3), ("SC", 4, 1), ("EX", 4, 3, 0),
-    ("EX", 4, 3, 1), ("RM", 4, 2, 0), ("RM", 4, 2, 1), ("NM", 4, 2), ("SC", 4, 0), ("EX", 4, 2, 0), ("EX", 4, 2, 1),
-    ("RM", 4, 1), ("NM", 4, 1), ("RC", 4, 3), ("NO", 4, 3, 0), ("NO", 4, 3, 1), ("EX", 4, 1, 0), ("EX", 4, 1, 1),
-    ("RM", 4, 0), ("NM", 4, 0), ("RC", 4, 2), ("NO", 4, 2, 0), ("NO", 4, 2, 1), ("EX", 4, 0, 0), ("EX", 4, 0, 1),
-    ("TA", 3, 0), ("CA", 3, 0, "v"), ("RC", 4, 1), ("NO", 4, 1, 0), ("NO", 4, 1, 1), ("RC", 4, 0), ("NO", 4, 0, 0),
-    ("NO", 4, 0, 1), ("TA", 3, 1), ("CA", 3, 1, "v"), ("TA", 3, 2), ("CA", 3, 2, "s"), ("QA", 3, 0), ("TX", 5, 0),
-    ("CX", 5, 0, "s"), ("TX", 5, 1), ("CX", 5, 1, "s"), ("QA", 3, 1), ("TQ", 5, 0), ("CQ", 5, 0, "v"), ("TQ", 5, 1),
-    ("CQ", 5, 1, "s"), ("QX", 5), ("MV", 4, 0), ("CV", 4, 0, "s"), ("MV", 4, 1), ("CV", 4, 1, "v"), ("MV", 4, 2),
-    ("CV", 4, 2, "s"), ("MV", 4, 3), ("CV", 4, 3, "s"), ("MV", 4, 4), ("CV", 4, 4, "v"), ("MV", 4, 5),
-    ("CV", 4, 5, "s"), ("QV", 4, 0), ("MV", 4, 6), ("CV", 4, 6, "s"), ("MV", 4, 7), ("CV", 4, 7, "v"), ("FO", 3, 0),
-    ("CO", 3, 0, "s"), ("QV", 4, 1), ("FO", 3, 1), ("CO", 3, 1, "s"), ("ST", 3, 0), ("FO", 3, 2), ("CO", 3, 2, "v"),
-    ("FO", 3, 3), ("CO", 3, 3, "s"), ("ST", 3, 1), ("SC", 5, 3, 0), ("SC", 5, 3, 1), ("SC", 5, 2, 0), ("SC", 5, 2, 1),
-    ("RM", 5, 3, 0), ("RM", 5, 3, 1), ("NM", 5, 3), ("SC", 5, 1), ("EX", 5, 3, 0), ("EX", 5, 3, 1), ("RM", 5, 2, 0),
-    ("RM", 5, 2, 1), ("NM", 5, 2), ("SC", 5, 0), ("EX", 5, 2, 0), ("EX", 5, 2, 1), ("RM", 5, 1), ("NM", 5, 1),
-    ("RC", 5, 3), ("NO", 5, 3, 0), ("NO", 5, 3, 1), ("EX", 5, 1, 0), ("EX", 5, 1, 1), ("RM", 5, 0), ("NM", 5, 0),
-    ("RC", 5, 2), ("NO", 5, 2, 0), ("NO", 5, 2, 1), ("EX", 5, 0, 0), ("EX", 5, 0, 1), ("TA", 4, 0), ("CA", 4, 0, "v"),
-    ("RC", 5, 1), ("NO", 5, 1, 0), ("NO", 5, 1, 1), ("RC", 5, 0), ("NO", 5, 0, 0), ("NO", 5, 0, 1), ("TA", 4, 1),
-    ("CA", 4, 1, "v"), ("TA", 4, 2), ("CA", 4, 2, "s"), ("QA", 4, 0), ("TX", 6, 0), ("CX", 6, 0, "s"), ("TX", 6, 1),
-    ("CX", 6, 1, "s"), ("QA", 4, 1), ("TQ", 6, 0), ("CQ", 6, 0, "v"), ("TQ", 6, 1), ("CQ", 6, 1, "s"), ("QX", 6),
-    ("MV", 5, 0), ("CV", 5, 0, "s"), ("MV", 5, 1), ("CV", 5, 1, "v"), ("MV", 5, 2), ("CV", 5, 2, "s"), ("MV", 5, 3),
-    ("CV", 5, 3, "s"), ("MV", 5, 4), ("CV", 5, 4, "v"), ("MV", 5, 5), ("CV", 5, 5, "s"), ("QV", 5, 0), ("MV", 5, 6),
-    ("CV", 5, 6, "s"), ("MV", 5, 7), ("CV", 5, 7, "v"), ("FO", 4, 0), ("CO", 4, 0, "s"), ("QV", 5, 1), ("FO", 4, 1),
-    ("CO", 4, 1, "s"), ("ST", 4, 0), ("FO", 4, 2), ("CO", 4, 2, "v"), ("FO", 4, 3), ("CO", 4, 3, "s"), ("ST", 4, 1),
-    ("SC", 6, 3, 0), ("SC", 6, 3, 1), ("SC", 6, 2, 0), ("SC", 6, 2, 1), ("RM", 6, 3, 0), ("RM", 6, 3, 1),
-    ("NM", 6, 3), ("SC", 6, 1), ("EX", 6, 3, 0), ("EX", 6, 3, 1), ("RM", 6, 2, 0), ("RM", 6, 2, 1), ("NM", 6, 2),
-    ("SC", 6, 0), ("EX", 6, 2, 0), ("EX", 6, 2, 1), ("RM", 6, 1), ("NM", 6, 1), ("RC", 6, 3), ("NO", 6, 3, 0),
-    ("NO", 6, 3, 1), ("EX", 6, 1, 0), ("EX", 6, 1, 1), ("RM", 6, 0), ("NM", 6, 0), ("RC", 6, 2), ("NO", 6, 2, 0),
-    ("NO", 6, 2, 1), ("EX", 6, 0, 0), ("EX", 6, 0, 1), ("TA", 5, 0), ("CA", 5, 0, "v"), ("RC", 6, 1), ("NO", 6, 1, 0),
-    ("NO", 6, 1, 1), ("RC", 6, 0), ("NO", 6, 0, 0), ("NO", 6, 0, 1), ("TA", 5, 1), ("CA", 5, 1, "v"), ("TA", 5, 2),
-    ("CA", 5, 2, "s"), ("QA", 5, 0), ("TX", 7, 0), ("CX", 7, 0, "s"), ("TX", 7, 1), ("CX", 7, 1, "s"), ("QA", 5, 1),
-    ("TQ", 7, 0), ("CQ", 7, 0, "v"), ("TQ", 7, 1), ("CQ", 7, 1, "s"), ("QX", 7), ("MV", 6, 0), ("CV", 6, 0, "s"),
-    ("MV", 6, 1), ("CV", 6, 1, "v"), ("MV", 6, 2), ("CV", 6, 2, "s"), ("MV", 6, 3), ("CV", 6, 3, "s"), ("MV", 6, 4),
-    ("CV", 6, 4, "v"), ("MV", 6, 5), ("CV", 6, 5, "s"), ("QV", 6, 0), ("MV", 6, 6), ("CV", 6, 6, "s"), ("MV", 6, 7),
-    ("CV", 6, 7, "v"), ("FO", 5, 0), ("CO", 5, 0, "s"), ("QV", 6, 1), ("FO", 5, 1), ("CO", 5, 1, "s"), ("ST", 5, 0),
-    ("FO", 5, 2), ("CO", 5, 2, "v"), ("FO", 5, 3), ("CO", 5, 3, "s"), ("ST", 5, 1), ("SC", 7, 3, 0), ("SC", 7, 3, 1),
-    ("SC", 7, 2, 0), ("SC", 7, 2, 1), ("RM", 7, 3, 0), ("RM", 7, 3, 1), ("NM", 7, 3), ("SC", 7, 1), ("EX", 7, 3, 0),
-    ("EX", 7, 3, 1), ("RM", 7, 2, 0), ("RM", 7, 2, 1), ("NM", 7, 2), ("SC", 7, 0), ("EX", 7, 2, 0), ("EX", 7, 2, 1),
-    ("RM", 7, 1), ("NM", 7, 1), ("RC", 7, 3), ("NO", 7, 3, 0), ("NO", 7, 3, 1), ("EX", 7, 1, 0), ("EX", 7, 1, 1),
-    ("RM", 7, 0), ("NM", 7, 0), ("RC", 7, 2), ("NO", 7, 2, 0), ("NO", 7, 2, 1), ("EX", 7, 0, 0), ("EX", 7, 0, 1),
-    ("TA", 6, 0), ("CA", 6, 0, "v"), ("RC", 7, 1), ("NO", 7, 1, 0), ("NO", 7, 1, 1), ("RC", 7, 0), ("NO", 7, 0, 0),
-    ("NO", 7, 0, 1), ("TA", 6, 1), ("CA", 6, 1, "v"), ("TA", 6, 2), ("CA", 6, 2, "s"), ("QA", 6, 0), ("QA", 6, 1),
-    ("MV", 7, 0), ("CV", 7, 0, "s"), ("MV", 7, 1), ("CV", 7, 1, "v"), ("MV", 7, 2), ("CV", 7, 2, "s"), ("MV", 7, 3),
-    ("CV", 7, 3, "s"), ("MV", 7, 4), ("CV", 7, 4, "v"), ("MV", 7, 5), ("CV", 7, 5, "s"), ("QV", 7, 0), ("MV", 7, 6),
-    ("CV", 7, 6, "s"), ("MV", 7, 7), ("CV", 7, 7, "v"), ("QV", 7, 1), ("TA", 7, 0), ("CA", 7, 0, "v"), ("TA", 7, 1),
-    ("CA", 7, 1, "v"), ("TA", 7, 2), ("CA", 7, 2, "s"), ("QA", 7, 0), ("QA", 7, 1), ("FO", 6, 0), ("CO", 6, 0, "s"),
-    ("FO", 6, 1), ("CO", 6, 1, "s"), ("ST", 6, 0), ("FO", 6, 2), ("CO", 6, 2, "v"), ("FO", 6, 3), ("CO", 6, 3, "s"),
-    ("ST", 6, 1), ("FO", 7, 0), ("CO", 7, 0, "s"), ("FO", 7, 1), ("CO", 7, 1, "s"), ("ST", 7, 0), ("FO", 7, 2),
-    ("CO", 7, 2, "v"), ("FO", 7, 3), ("CO", 7, 3, "s"), ("ST", 7, 1),
+    ("SC", 0, 2, 1), ("SC", 0, 1), ("SC", 0, 0), ("TX", 0, 0), ("TX", 0, 1), ("RX", 0, 3, 0), ("CX", 0, 0, "s"),
+    ("RX", 0, 3, 1), ("CX", 0, 1, "s"), ("RX", 0, 2, 0), ("EX", 0, 3, 0), ("RX", 0, 2, 1), ("EX", 0, 3, 1), ("TW", 0),
+    ("TW", 1), ("TW", 2), ("TW", 3), ("RX", 0, 1, 0), ("CW", 0, "s"), ("RX", 0, 1, 1), ("CW", 1, "s"),
+    ("RX", 0, 0, 0), ("RX", 0, 0, 1), ("QX", 0), ("EX", 0, 2, 0), ("CW", 2, "v"), ("EX", 0, 2, 1), ("QW", 0),
+    ("CW", 3, "v"), ("TQ", 1, 0), ("TQ", 1, 1), ("TX", 1, 0), ("TX", 1, 1), ("RC", 0, 0), ("NO", 0, 3, 0, "g"),
+    ("NO", 0, 3, 1, "g"), ("NO", 0, 2, 0, "g"), ("NO", 0, 2, 1, "g"), ("EX", 0, 1, 0), ("EX", 0, 1, 1), ("QW", 1),
+    ("EX", 0, 0, 0), ("EX", 0, 0, 1), ("MV", 0, 0), ("MV", 0, 1), ("MV", 0, 2), ("MV", 0, 3), ("MV", 0, 4),
+    ("MV", 0, 5), ("MV", 0, 6), ("MV", 0, 7), ("CQ", 1, 0, "s"), ("CQ", 1, 1, "v"), ("RC", 0, 1),
+    ("NO", 0, 1, 0, "g"), ("NO", 0, 1, 1, "g"), ("NO", 0, 0, 0, "g"), ("NO", 0, 0, 1, "g"), ("CX", 1, 0, "s"),
+    ("CX", 1, 1, "v"), ("CV", 0, 0, "s"), ("CV", 0, 1, "v"), ("QX", 1), ("CV", 0, 2, "s"), ("CV", 0, 3, "v"),
+    ("CV", 0, 4, "s"), ("CV", 0, 5, "v"), ("QV", 0, 0), ("CV", 0, 6, "s"), ("CV", 0, 7, "v"), ("QV", 0, 1),
+    ("TX", 2, 0), ("CX", 2, 0, "s"), ("SC", 1, 3, 0), ("RX", 1, 3, 0), ("TX", 2, 1), ("CX", 2, 1, "s"),
+    ("SC", 1, 3, 1), ("RX", 1, 3, 1), ("TQ", 2, 0), ("CQ", 2, 0, "s"), ("SC", 1, 2, 0), ("RX", 1, 2, 0), ("TQ", 2, 1),
+    ("CQ", 2, 1, "s"), ("SC", 1, 2, 1), ("RX", 1, 2, 1), ("TA", 0, 1), ("CA", 0, 1, "s"), ("SC", 1, 1),
+    ("RX", 1, 1, 0), ("RX", 1, 1, 1), ("QX", 2), ("TA", 0, 2), ("CA", 0, 2, "v"), ("SC", 1, 0), ("RX", 1, 0, 0),
+    ("RX", 1, 0, 1), ("TA", 0, 0), ("CA", 0, 0, "s"), ("MV", 1, 0), ("MV", 1, 1), ("MV", 1, 2), ("MV", 1, 3),
+    ("MV", 1, 4), ("MV", 1, 5), ("MV", 1, 6), ("MV", 1, 7), ("EX", 1, 3, 0), ("CV", 1, 0, "s"), ("EX", 1, 3, 1),
+    ("CV", 1, 1, "v"), ("QA", 0, 1), ("CV", 1, 2, "v"), ("EX", 1, 2, 0), ("CV", 1, 3, "v"), ("EX", 1, 2, 1),
+    ("QA", 0, 0), ("FO", 0, 2), ("FO", 0, 3), ("FO", 0, 0), ("FO", 0, 1), ("CV", 1, 4, "s"), ("RC", 1, 0),
+    ("NO", 1, 3, 0, "g"), ("NO", 1, 3, 1, "g"), ("NO", 1, 2, 0, "g"), ("NO", 1, 2, 1, "g"), ("CV", 1, 5, "s"),
+    ("EX", 1, 1, 0), ("QV", 1, 0), ("EX", 1, 1, 1), ("CV", 1, 6, "v"), ("CV", 1, 7, "v"), ("EX", 1, 0, 0),
+    ("EX", 1, 0, 1), ("CO", 0, 2, "s"), ("CO", 0, 3, "v"), ("ST", 0, 1), ("QV", 1, 1), ("RC", 1, 1),
+    ("NO", 1, 1, 0, "g"), ("NO", 1, 1, 1, "g"), ("NO", 1, 0, 0, "g"), ("NO", 1, 0, 1, "g"), ("CO", 0, 0, "s"),
+    ("CO", 0, 1, "s"), ("ST", 0, 0), ("TX", 3, 0), ("CX", 3, 0, "s"), ("SC", 2, 3, 0), ("RX", 2, 3, 0), ("TX", 3, 1),
+    ("CX", 3, 1, "s"), ("SC", 2, 3, 1), ("RX", 2, 3, 1), ("TQ", 3, 0), ("CQ", 3, 0, "s"), ("SC", 2, 2, 0),
+    ("RX", 2, 2, 0), ("TQ", 3, 1), ("CQ", 3, 1, "s"), ("SC", 2, 2, 1), ("RX", 2, 2, 1), ("TA", 1, 1),
+    ("CA", 1, 1, "s"), ("SC", 2, 1), ("RX", 2, 1, 0), ("RX", 2, 1, 1), ("QX", 3), ("TA", 1, 2), ("CA", 1, 2, "v"),
+    ("SC", 2, 0), ("RX", 2, 0, 0), ("RX", 2, 0, 1), ("TA", 1, 0), ("CA", 1, 0, "s"), ("MV", 2, 0), ("MV", 2, 1),
+    ("MV", 2, 2), ("MV", 2, 3), ("MV", 2, 4), ("MV", 2, 5), ("MV", 2, 6), ("MV", 2, 7), ("EX", 2, 3, 0),
+    ("CV", 2, 0, "s"), ("EX", 2, 3, 1), ("CV", 2, 1, "v"), ("QA", 1, 1), ("CV", 2, 2, "v"), ("EX", 2, 2, 0),
+    ("CV", 2, 3, "v"), ("EX", 2, 2, 1), ("QA", 1, 0), ("FO", 1, 2), ("FO", 1, 3), ("FO", 1, 0), ("FO", 1, 1),
+    ("CV", 2, 4, "s"), ("RC", 2, 0), ("NO", 2, 3, 0, "g"), ("NO", 2, 3, 1, "g"), ("NO", 2, 2, 0, "g"),
+    ("NO", 2, 2, 1, "g"), ("CV", 2, 5, "s"), ("EX", 2, 1, 0), ("QV", 2, 0), ("EX", 2, 1, 1), ("CV", 2, 6, "v"),
+    ("CV", 2, 7, "v"), ("EX", 2, 0, 0), ("EX", 2, 0, 1), ("CO", 1, 2, "s"), ("CO", 1, 3, "v"), ("ST", 1, 1),
+    ("QV", 2, 1), ("RC", 2, 1), ("NO", 2, 1, 0, "g"), ("NO", 2, 1, 1, "g"), ("NO", 2, 0, 0, "g"),
+    ("NO", 2, 0, 1, "g"), ("CO", 1, 0, "s"), ("CO", 1, 1, "s"), ("ST", 1, 0), ("TX", 4, 0), ("CX", 4, 0, "s"),
+    ("SC", 3, 3, 0), ("RX", 3, 3, 0), ("TX", 4, 1), ("CX", 4, 1, "s"), ("SC", 3, 3, 1), ("RX", 3, 3, 1), ("TQ", 4, 0),
+    ("CQ", 4, 0, "s"), ("SC", 3, 2, 0), ("RX", 3, 2, 0), ("TQ", 4, 1), ("CQ", 4, 1, "s"), ("SC", 3, 2, 1),
+    ("RX", 3, 2, 1), ("TA", 2, 1), ("CA", 2, 1, "s"), ("SC", 3, 1), ("RX", 3, 1, 0), ("RX", 3, 1, 1), ("QX", 4),
+    ("TA", 2, 2), ("CA", 2, 2, "v"), ("SC", 3, 0), ("RX", 3, 0, 0), ("RX", 3, 0, 1), ("TA", 2, 0), ("CA", 2, 0, "s"),
+    ("MV", 3, 0), ("MV", 3, 1), ("MV", 3, 2), ("MV", 3, 3), ("MV", 3, 4), ("MV", 3, 5), ("MV", 3, 6), ("MV", 3, 7),
+    ("EX", 3, 3, 0), ("CV", 3, 0, "s"), ("EX", 3, 3, 1), ("CV", 3, 1, "v"), ("QA", 2, 1), ("CV", 3, 2, "v"),
+    ("EX", 3, 2, 0), ("CV", 3, 3, "v"), ("EX", 3, 2, 1), ("QA", 2, 0), ("FO", 2, 2), ("FO", 2, 3), ("FO", 2, 0),
+    ("FO", 2, 1), ("CV", 3, 4, "s"), ("RC", 3, 0), ("NO", 3, 3, 0, "g"), ("NO", 3, 3, 1, "g"), ("NO", 3, 2, 0, "g"),
+    ("NO", 3, 2, 1, "g"), ("CV", 3, 5, "s"), ("EX", 3, 1, 0), ("QV", 3, 0), ("EX", 3, 1, 1), ("CV", 3, 6, "v"),
+    ("CV", 3, 7, "v"), ("EX", 3, 0, 0), ("EX", 3, 0, 1), ("CO", 2, 2, "s"), ("CO", 2, 3, "v"), ("ST", 2, 1),
+    ("QV", 3, 1), ("RC", 3, 1), ("NO", 3, 1, 0, "g"), ("NO", 3, 1, 1, "g"), ("NO", 3, 0, 0, "g"),
+    ("NO", 3, 0, 1, "g"), ("CO", 2, 0, "s"), ("CO", 2, 1, "s"), ("ST", 2, 0), ("TX", 5, 0), ("CX", 5, 0, "s"),
+    ("SC", 4, 3, 0), ("RX", 4, 3, 0), ("TX", 5, 1), ("CX", 5, 1, "s"), ("SC", 4, 3, 1), ("RX", 4, 3, 1), ("TQ", 5, 0),
+    ("CQ", 5, 0, "s"), ("SC", 4, 2, 0), ("RX", 4, 2, 0), ("TQ", 5, 1), ("CQ", 5, 1, "s"), ("SC", 4, 2, 1),
+    ("RX", 4, 2, 1), ("TA", 3, 1), ("CA", 3, 1, "s"), ("SC", 4, 1), ("RX", 4, 1, 0), ("RX", 4, 1, 1), ("QX", 5),
+    ("TA", 3, 2), ("CA", 3, 2, "v"), ("SC", 4, 0), ("RX", 4, 0, 0), ("RX", 4, 0, 1), ("TA", 3, 0), ("CA", 3, 0, "s"),
+    ("MV", 4, 0), ("MV", 4, 1), ("MV", 4, 2), ("MV", 4, 3), ("MV", 4, 4), ("MV", 4, 5), ("MV", 4, 6), ("MV", 4, 7),
+    ("EX", 4, 3, 0), ("CV", 4, 0, "s"), ("EX", 4, 3, 1), ("CV", 4, 1, "v"), ("QA", 3, 1), ("CV", 4, 2, "v"),
+    ("EX", 4, 2, 0), ("CV", 4, 3, "v"), ("EX", 4, 2, 1), ("QA", 3, 0), ("FO", 3, 2), ("FO", 3, 3), ("FO", 3, 0),
+    ("FO", 3, 1), ("CV", 4, 4, "s"), ("RC", 4, 0), ("NO", 4, 3, 0, "g"), ("NO", 4, 3, 1, "g"), ("NO", 4, 2, 0, "g"),
+    ("NO", 4, 2, 1, "g"), ("CV", 4, 5, "s"), ("EX", 4, 1, 0), ("QV", 4, 0), ("EX", 4, 1, 1), ("CV", 4, 6, "v"),
+    ("CV", 4, 7, "v"), ("EX", 4, 0, 0), ("EX", 4, 0, 1), ("CO", 3, 2, "s"), ("CO", 3, 3, "v"), ("ST", 3, 1),
+    ("QV", 4, 1), ("RC", 4, 1), ("NO", 4, 1, 0, "g"), ("NO", 4, 1, 1, "g"), ("NO", 4, 0, 0, "g"),
+    ("NO", 4, 0, 1, "g"), ("CO", 3, 0, "s"), ("CO", 3, 1, "s"), ("ST", 3, 0), ("TX", 6, 0), ("CX", 6, 0, "s"),
+    ("SC", 5, 3, 0), ("RX", 5, 3, 0), ("TX", 6, 1), ("CX", 6, 1, "s"), ("SC", 5, 3, 1), ("RX", 5, 3, 1), ("TQ", 6, 0),
+    ("CQ", 6, 0, "s"), ("SC", 5, 2, 0), ("RX", 5, 2, 0), ("TQ", 6, 1), ("CQ", 6, 1, "s"), ("SC", 5, 2, 1),
+    ("RX", 5, 2, 1), ("TA", 4, 1), ("CA", 4, 1, "s"), ("SC", 5, 1), ("RX", 5, 1, 0), ("RX", 5, 1, 1), ("QX", 6),
+    ("TA", 4, 2), ("CA", 4, 2, "v"), ("SC", 5, 0), ("RX", 5, 0, 0), ("RX", 5, 0, 1), ("TA", 4, 0), ("CA", 4, 0, "s"),
+    ("MV", 5, 0), ("MV", 5, 1), ("MV", 5, 2), ("MV", 5, 3), ("MV", 5, 4), ("MV", 5, 5), ("MV", 5, 6), ("MV", 5, 7),
+    ("EX", 5, 3, 0), ("CV", 5, 0, "s"), ("EX", 5, 3, 1), ("CV", 5, 1, "v"), ("QA", 4, 1), ("CV", 5, 2, "v"),
+    ("EX", 5, 2, 0), ("CV", 5, 3, "v"), ("EX", 5, 2, 1), ("QA", 4, 0), ("FO", 4, 2), ("FO", 4, 3), ("FO", 4, 0),
+    ("FO", 4, 1), ("CV", 5, 4, "s"), ("RC", 5, 0), ("NO", 5, 3, 0, "g"), ("NO", 5, 3, 1, "g"), ("NO", 5, 2, 0, "g"),
+    ("NO", 5, 2, 1, "g"), ("CV", 5, 5, "s"), ("EX", 5, 1, 0), ("QV", 5, 0), ("EX", 5, 1, 1), ("CV", 5, 6, "v"),
+    ("CV", 5, 7, "v"), ("EX", 5, 0, 0), ("EX", 5, 0, 1), ("CO", 4, 2, "s"), ("CO", 4, 3, "v"), ("ST", 4, 1),
+    ("QV", 5, 1), ("RC", 5, 1), ("NO", 5, 1, 0, "g"), ("NO", 5, 1, 1, "g"), ("NO", 5, 0, 0, "g"),
+    ("NO", 5, 0, 1, "g"), ("CO", 4, 0, "s"), ("CO", 4, 1, "s"), ("ST", 4, 0), ("TX", 7, 0), ("CX", 7, 0, "s"),
+    ("SC", 6, 3, 0), ("RX", 6, 3, 0), ("TX", 7, 1), ("CX", 7, 1, "s"), ("SC", 6, 3, 1), ("RX", 6, 3, 1), ("TQ", 7, 0),
+    ("CQ", 7, 0, "s"), ("SC", 6, 2, 0), ("RX", 6, 2, 0), ("TQ", 7, 1), ("CQ", 7, 1, "s"), ("SC", 6, 2, 1),
+    ("RX", 6, 2, 1), ("TA", 5, 1), ("CA", 5, 1, "s"), ("SC", 6, 1), ("RX", 6, 1, 0), ("RX", 6, 1, 1), ("QX", 7),
+    ("TA", 5, 2), ("CA", 5, 2, "v"), ("SC", 6, 0), ("RX", 6, 0, 0), ("RX", 6, 0, 1), ("TA", 5, 0), ("CA", 5, 0, "s"),
+    ("MV", 6, 0), ("MV", 6, 1), ("MV", 6, 2), ("MV", 6, 3), ("MV", 6, 4), ("MV", 6, 5), ("MV", 6, 6), ("MV", 6, 7),
+    ("EX", 6, 3, 0), ("CV", 6, 0, "s"), ("EX", 6, 3, 1), ("CV", 6, 1, "v"), ("QA", 5, 1), ("CV", 6, 2, "v"),
+    ("EX", 6, 2, 0), ("CV", 6, 3, "v"), ("EX", 6, 2, 1), ("QA", 5, 0), ("FO", 5, 2), ("FO", 5, 3), ("FO", 5, 0),
+    ("FO", 5, 1), ("CV", 6, 4, "s"), ("RC", 6, 0), ("NO", 6, 3, 0, "g"), ("NO", 6, 3, 1, "g"), ("NO", 6, 2, 0, "g"),
+    ("NO", 6, 2, 1, "g"), ("CV", 6, 5, "s"), ("EX", 6, 1, 0), ("QV", 6, 0), ("EX", 6, 1, 1), ("CV", 6, 6, "v"),
+    ("CV", 6, 7, "v"), ("EX", 6, 0, 0), ("EX", 6, 0, 1), ("CO", 5, 2, "s"), ("CO", 5, 3, "v"), ("ST", 5, 1),
+    ("QV", 6, 1), ("RC", 6, 1), ("NO", 6, 1, 0, "g"), ("NO", 6, 1, 1, "g"), ("NO", 6, 0, 0, "g"),
+    ("NO", 6, 0, 1, "g"), ("CO", 5, 0, "s"), ("CO", 5, 1, "s"), ("ST", 5, 0), ("SC", 7, 3, 0), ("RX", 7, 3, 0),
+    ("SC", 7, 3, 1), ("RX", 7, 3, 1), ("SC", 7, 2, 0), ("RX", 7, 2, 0), ("SC", 7, 2, 1), ("RX", 7, 2, 1),
+    ("TA", 6, 1), ("CA", 6, 1, "s"), ("SC", 7, 1), ("RX", 7, 1, 0), ("RX", 7, 1, 1), ("TA", 6, 2), ("CA", 6, 2, "v"),
+    ("SC", 7, 0), ("RX", 7, 0, 0), ("RX", 7, 0, 1), ("TA", 6, 0), ("CA", 6, 0, "s"), ("MV", 7, 0), ("MV", 7, 1),
+    ("MV", 7, 2), ("MV", 7, 3), ("MV", 7, 4), ("MV", 7, 5), ("MV", 7, 6), ("MV", 7, 7), ("EX", 7, 3, 0),
+    ("CV", 7, 0, "v"), ("EX", 7, 3, 1), ("QA", 6, 1), ("CV", 7, 1, "v"), ("EX", 7, 2, 0), ("QA", 6, 0),
+    ("EX", 7, 2, 1), ("FO", 6, 2), ("FO", 6, 3), ("FO", 6, 0), ("FO", 6, 1), ("CV", 7, 2, "v"), ("EX", 7, 1, 0),
+    ("EX", 7, 1, 1), ("RC", 7, 0), ("NO", 7, 3, 0, "g"), ("NO", 7, 3, 1, "v"), ("NO", 7, 2, 0, "g"),
+    ("NO", 7, 2, 1, "v"), ("EX", 7, 0, 0), ("EX", 7, 0, 1), ("CV", 7, 3, "v"), ("CV", 7, 4, "s"), ("RC", 7, 1),
+    ("NO", 7, 1, 0, "g"), ("NO", 7, 1, 1, "v"), ("NO", 7, 0, 0, "g"), ("NO", 7, 0, 1, "v"), ("CV", 7, 5, "s"),
+    ("QV", 7, 0), ("CV", 7, 6, "s"), ("CV", 7, 7, "v"), ("TA", 7, 1), ("TA", 7, 2), ("TA", 7, 0), ("CO", 6, 2, "s"),
+    ("QV", 7, 1), ("CO", 6, 3, "v"), ("ST", 6, 1), ("CA", 7, 1, "s"), ("CA", 7, 2, "v"), ("CA", 7, 0, "s"),
+    ("QA", 7, 1), ("FO", 7, 2), ("FO", 7, 3), ("CO", 6, 0, "v"), ("QA", 7, 0), ("CO", 6, 1, "s"), ("ST", 6, 0),
+    ("FO", 7, 0), ("FO", 7, 1), ("CO", 7, 2, "v"), ("ST4", 7, 2), ("CO", 7, 3, "s"), ("ST4", 7, 3), ("CO", 7, 0, "v"),
+    ("ST4", 7, 0), ("CO", 7, 1, "s"), ("ST4", 7, 1),
 )
 
 
@@ -134,7 +138,7 @@ def tile_multiheadattention_pa_t_kernel(tc, q, k, x, Wv, mask, out):
         const = ctx.enter_context(tc.tile_pool(name="const", bufs=1))
         loads = ctx.enter_context(tc.tile_pool(name="loads", bufs=1))
         work = ctx.enter_context(tc.tile_pool(name="work", bufs=2))
-        small = ctx.enter_context(tc.tile_pool(name="small", bufs=8))
+        small = ctx.enter_context(tc.tile_pool(name="small", bufs=3))
         psum = ctx.enter_context(tc.psum_pool(name="psum", bufs=8))
         st = {}
 
@@ -148,7 +152,7 @@ def tile_multiheadattention_pa_t_kernel(tc, q, k, x, Wv, mask, out):
         q_sb = [loads.tile([P, NT * H * L], BF16, name="q_sb%d" % b) for b in range(B)]
         k_sb = [loads.tile([P, NT * H * L], BF16, name="k_sb%d" % b) for b in range(B)]
         wv_sb = loads.tile([P, 8 * D], BF16, name="wv_sb")
-        mk_i = loads.tile([P, NT * 2 * P], I32, name="mk_i")
+        mk_i = loads.tile([P, 2 * P], I32, name="mk_i")
         mask32 = mask.bitcast(I32)
         wv_view = Wv.rearrange("(r p) d -> p r d", p=P)
 
@@ -174,16 +178,12 @@ def tile_multiheadattention_pa_t_kernel(tc, q, k, x, Wv, mask, out):
             )
 
         def LM():
-            for it in range(NT):
-                nc.sync.dma_start(
-                    out=mk_i[:, it * 2 * P : (it + 1) * 2 * P],
-                    in_=mask32[0, it * P : (it + 1) * P, it * 2 * P : (it + 1) * 2 * P],
-                )
+            nc.sync.dma_start(out=mk_i[:], in_=mask32[0, 0:P, 0 : 2 * P])
 
         id_f = const.tile([P, P], F32, name="id_f")
         id_bf = const.tile([P, P], BF16, name="id_bf")
-        mk_f = const.tile([P, NT * P], F32, name="mk_f")
-        mb = const.tile([P, NT * P], BF16, name="mb")
+        mk_f = const.tile([P, P], F32, name="mk_f")
+        mb = const.tile([P, P], BF16, name="mb")
         a_sb = [[const.tile([P, H * AW[it]], BF16, name="a_sb%d_%d" % (par, it)) for it in range(NT)] for par in range(2)]
         wvg = const.tile([P, 8 * D], BF16, name="wvg", align_bytes=64)
         wvw = const.tile([P, H * D], U32, name="wvw", align_bytes=64)
@@ -266,7 +266,7 @@ def tile_multiheadattention_pa_t_kernel(tc, q, k, x, Wv, mask, out):
             if it > 0:
                 nc.tensor.matmul(out=view[:, 0 : it * P], lhsT=lhsT, rhs=kT[:, h * S : h * S + it * P], start=True, stop=True)
             nc.tensor.matmul(out=view[:, it * P : n], lhsT=lhsT, rhs=kT[:, h * S + it * P : h * S + n], start=True, stop=False)
-            nc.tensor.matmul(out=view[:, it * P : n], lhsT=id_bf[:], rhs=mb[:, it * P : (it + 1) * P], start=False, stop=True)
+            nc.tensor.matmul(out=view[:, it * P : n], lhsT=id_bf[:], rhs=mb[:], start=False, stop=True)
 
         def SC(b, it, h=0):
             n = (it + 1) * P
@@ -281,52 +281,51 @@ def tile_multiheadattention_pa_t_kernel(tc, q, k, x, Wv, mask, out):
                 sc_head(b, it, h, ps1[:])
                 st[("S", b, it, h)] = ps1[:]
 
-        def RM(b, it, h=0):
-            if ("mx", b, it) not in st:
-                mx_new = small.tile([P, H], F32, name="mx")
-                st[("mx", b, it)] = mx_new
-            mx = st[("mx", b, it)]
-            if it < 2:
-                nc.vector.tensor_reduce(out=mx[:], in_=st[("S2", b, it)][:], axis=AX.X, op=ALU.max)
-            else:
-                nc.vector.tensor_reduce(out=mx[:, h : h + 1], in_=st[("S", b, it, h)], axis=AX.X, op=ALU.max)
-
-        def NM(b, it):
-            nm = small.tile([P, H], F32, name="nm")
-            nc.vector.tensor_scalar(out=nm[:], in0=st[("mx", b, it)][:], scalar1=-SCALE, scalar2=None, op0=ALU.mult)
-            st[("nm", b, it)] = nm
+        def RX(b, it, h):
+            n = (it + 1) * P
+            if ("nm", b) not in st:
+                nm_new = small.tile([P, 2 * NT], F32, name="nm")
+                sm_new = small.tile([P, 2 * NT], F32, name="sm")
+                rc_new = small.tile([P, 2 * NT], F32, name="rc")
+                st[("nm", b)] = (nm_new, sm_new, rc_new)
+            if ("e", b, it) not in st:
+                e_new = work.tile([P, H * n], F32, name="e_sb%d" % it)
+                st[("e", b, it)] = e_new
+            c = 2 * it + h
+            nc.vector.tensor_scalar(
+                out=st[("e", b, it)][:, h * n : (h + 1) * n],
+                in0=st[("S", b, it, h)],
+                scalar1=-SCALE,
+                scalar2=None,
+                op0=ALU.mult,
+                op1=ALU.min,
+                accum_out=st[("nm", b)][0][:, c : c + 1],
+            )
 
         def EX(b, it, h):
             n = (it + 1) * P
-            if ("e", b, it) not in st:
-                e_new = work.tile([P, H * n], F32, name="e_sb%d" % it)
-                sm_new = small.tile([P, H], F32, name="sm")
-                st[("e", b, it)] = (e_new, sm_new)
-            e_sb, sm = st[("e", b, it)]
+            c = 2 * it + h
+            nm, sm, rc = st[("nm", b)]
+            e_sl = st[("e", b, it)][:, h * n : (h + 1) * n]
             nc.scalar.activation(
-                out=e_sb[:, h * n : (h + 1) * n],
-                in_=st[("S", b, it, h)],
-                func=ACT.Exp,
-                bias=st[("nm", b, it)][:, h : h + 1],
-                scale=SCALE,
-                accum_out=sm[:, h : h + 1],
+                out=e_sl, in_=e_sl, func=ACT.Exp, bias=nm[:, c : c + 1], scale=-1.0, accum_out=sm[:, c : c + 1]
             )
 
-        def RC(b, it):
-            rc = small.tile([P, H], F32, name="rc")
-            nc.vector.reciprocal(out=rc[:], in_=st[("e", b, it)][1][:])
-            st[("rc", b, it)] = rc
+        def RC(b, half):
+            nm, sm, rc = st[("nm", b)]
+            lo = 4 - 4 * half
+            nc.vector.reciprocal(out=rc[:, lo : lo + 4], in_=sm[:, lo : lo + 4])
 
-        def NO(b, it, h):
+        def NO(b, it, h, eng):
             n = (it + 1) * P
-            nc.gpsimd.tensor_scalar(
-                out=a_sb[b % 2][it][:, h * AW[it] : h * AW[it] + n],
-                in0=st[("e", b, it)][0][:, h * n : (h + 1) * n],
-                scalar1=st[("rc", b, it)][:, h : h + 1],
-                scalar2=0.0,
-                op0=ALU.mult,
-                op1=ALU.add,
-            )
+            c = 2 * it + h
+            dst = a_sb[b % 2][it][:, h * AW[it] : h * AW[it] + n]
+            src = st[("e", b, it)][:, h * n : (h + 1) * n]
+            rcol = st[("nm", b)][2][:, c : c + 1]
+            if eng == "g":
+                nc.gpsimd.tensor_scalar(out=dst, in0=src, scalar1=rcol, scalar2=0.0, op0=ALU.mult, op1=ALU.add)
+            else:
+                nc.vector.tensor_scalar(out=dst, in0=src, scalar1=rcol, scalar2=None, op0=ALU.mult)
 
         def MV(b, j):
             xw, xs = st[("xw", b)]
@@ -435,7 +434,7 @@ def tile_multiheadattention_pa_t_kernel(tc, q, k, x, Wv, mask, out):
 
         steps = {
             "LX": LX, "LQ": LQ, "LK": LK, "LW": LW, "LM": LM, "INIT": INIT, "MB": MB, "TW": TW, "CW": CW, "QW": QW,
-            "TX": TX, "CX": CX, "QX": QX, "TQ": TQ, "CQ": CQ, "SC": SC, "RM": RM, "NM": NM, "EX": EX, "RC": RC,
+            "TX": TX, "CX": CX, "QX": QX, "TQ": TQ, "CQ": CQ, "SC": SC, "RX": RX, "EX": EX, "RC": RC,
             "NO": NO, "MV": MV, "CV": CV, "QV": QV, "TA": TA, "CA": CA, "QA": QA, "FO": FO, "CO": CO, "ST": ST, "ST4": ST4,
         }
         for step in ORDER:

@@ -25,108 +25,108 @@ AW = (256, 256, 512, 512)
 SEGS = (((0, 0), (1, 0)), ((2, 0), (3, 0)), ((2, 1), (3, 1)))
 
 ORDER = (
-    ("INIT",), ("LQ", 0), ("LK", 0), ("LM",), ("LX", 0), ("LW", 0), ("LW", 1), ("LQ", 1), ("LK", 1), ("LX", 1),
-    ("LX", 2), ("LQ", 2), ("LK", 2), ("LX", 3), ("LQ", 3), ("LK", 3), ("LX", 4), ("LQ", 4), ("LK", 4), ("LX", 5),
-    ("LQ", 5), ("LK", 5), ("LX", 6), ("LQ", 6), ("LK", 6), ("LX", 7), ("LQ", 7), ("LK", 7), ("TQ", 0, 0),
-    ("CQ", 0, 0, "v"), ("TQ", 0, 1), ("CQ", 0, 1, "s"), ("MB",), ("SC", 0, 3, 0), ("SC", 0, 3, 1), ("SC", 0, 2, 0),
-    ("SC", 0, 2, 1), ("SC", 0, 1), ("SC", 0, 0), ("TX", 0, 0), ("TX", 0, 1), ("RX", 0, 3, 0), ("CX", 0, 0, "s"),
-    ("RX", 0, 3, 1), ("CX", 0, 1, "s"), ("RX", 0, 2, 0), ("EX", 0, 3, 0), ("RX", 0, 2, 1), ("EX", 0, 3, 1), ("TW", 0),
-    ("TW", 1), ("TW", 2), ("TW", 3), ("RX", 0, 1, 0), ("CW", 0, "s"), ("RX", 0, 1, 1), ("CW", 1, "s"),
-    ("RX", 0, 0, 0), ("RX", 0, 0, 1), ("QX", 0), ("EX", 0, 2, 0), ("CW", 2, "v"), ("EX", 0, 2, 1), ("QW", 0),
-    ("CW", 3, "v"), ("TQ", 1, 0), ("TQ", 1, 1), ("TX", 1, 0), ("TX", 1, 1), ("RC", 0, 0), ("NO", 0, 3, 0, "g"),
-    ("NO", 0, 3, 1, "g"), ("NO", 0, 2, 0, "g"), ("NO", 0, 2, 1, "g"), ("EX", 0, 1, 0), ("EX", 0, 1, 1), ("QW", 1),
-    ("EX", 0, 0, 0), ("EX", 0, 0, 1), ("MV", 0, 0), ("MV", 0, 1), ("MV", 0, 2), ("MV", 0, 3), ("MV", 0, 4),
-    ("MV", 0, 5), ("MV", 0, 6), ("MV", 0, 7), ("CQ", 1, 0, "s"), ("CQ", 1, 1, "v"), ("RC", 0, 1),
-    ("NO", 0, 1, 0, "g"), ("NO", 0, 1, 1, "g"), ("NO", 0, 0, 0, "g"), ("NO", 0, 0, 1, "g"), ("CX", 1, 0, "s"),
-    ("CX", 1, 1, "v"), ("CV", 0, 0, "s"), ("CV", 0, 1, "v"), ("QX", 1), ("CV", 0, 2, "s"), ("CV", 0, 3, "v"),
-    ("CV", 0, 4, "s"), ("CV", 0, 5, "v"), ("QV", 0, 0), ("CV", 0, 6, "s"), ("CV", 0, 7, "v"), ("QV", 0, 1),
-    ("TX", 2, 0), ("CX", 2, 0, "s"), ("SC", 1, 3, 0), ("RX", 1, 3, 0), ("TX", 2, 1), ("CX", 2, 1, "s"),
-    ("SC", 1, 3, 1), ("RX", 1, 3, 1), ("TQ", 2, 0), ("CQ", 2, 0, "s"), ("SC", 1, 2, 0), ("RX", 1, 2, 0), ("TQ", 2, 1),
-    ("CQ", 2, 1, "s"), ("SC", 1, 2, 1), ("RX", 1, 2, 1), ("TA", 0, 1), ("CA", 0, 1, "s"), ("SC", 1, 1),
-    ("RX", 1, 1, 0), ("RX", 1, 1, 1), ("QX", 2), ("TA", 0, 2), ("CA", 0, 2, "v"), ("SC", 1, 0), ("RX", 1, 0, 0),
-    ("RX", 1, 0, 1), ("TA", 0, 0), ("CA", 0, 0, "s"), ("MV", 1, 0), ("MV", 1, 1), ("MV", 1, 2), ("MV", 1, 3),
-    ("MV", 1, 4), ("MV", 1, 5), ("MV", 1, 6), ("MV", 1, 7), ("EX", 1, 3, 0), ("CV", 1, 0, "s"), ("EX", 1, 3, 1),
-    ("CV", 1, 1, "v"), ("QA", 0, 1), ("CV", 1, 2, "v"), ("EX", 1, 2, 0), ("CV", 1, 3, "v"), ("EX", 1, 2, 1),
-    ("QA", 0, 0), ("FO", 0, 2), ("FO", 0, 3), ("FO", 0, 0), ("FO", 0, 1), ("CV", 1, 4, "s"), ("RC", 1, 0),
-    ("NO", 1, 3, 0, "g"), ("NO", 1, 3, 1, "g"), ("NO", 1, 2, 0, "g"), ("NO", 1, 2, 1, "g"), ("CV", 1, 5, "s"),
-    ("EX", 1, 1, 0), ("QV", 1, 0), ("EX", 1, 1, 1), ("CV", 1, 6, "v"), ("CV", 1, 7, "v"), ("EX", 1, 0, 0),
-    ("EX", 1, 0, 1), ("CO", 0, 2, "s"), ("CO", 0, 3, "v"), ("ST", 0, 1), ("QV", 1, 1), ("RC", 1, 1),
-    ("NO", 1, 1, 0, "g"), ("NO", 1, 1, 1, "g"), ("NO", 1, 0, 0, "g"), ("NO", 1, 0, 1, "g"), ("CO", 0, 0, "s"),
-    ("CO", 0, 1, "s"), ("ST", 0, 0), ("TX", 3, 0), ("CX", 3, 0, "s"), ("SC", 2, 3, 0), ("RX", 2, 3, 0), ("TX", 3, 1),
-    ("CX", 3, 1, "s"), ("SC", 2, 3, 1), ("RX", 2, 3, 1), ("TQ", 3, 0), ("CQ", 3, 0, "s"), ("SC", 2, 2, 0),
-    ("RX", 2, 2, 0), ("TQ", 3, 1), ("CQ", 3, 1, "s"), ("SC", 2, 2, 1), ("RX", 2, 2, 1), ("TA", 1, 1),
-    ("CA", 1, 1, "s"), ("SC", 2, 1), ("RX", 2, 1, 0), ("RX", 2, 1, 1), ("QX", 3), ("TA", 1, 2), ("CA", 1, 2, "v"),
-    ("SC", 2, 0), ("RX", 2, 0, 0), ("RX", 2, 0, 1), ("TA", 1, 0), ("CA", 1, 0, "s"), ("MV", 2, 0), ("MV", 2, 1),
-    ("MV", 2, 2), ("MV", 2, 3), ("MV", 2, 4), ("MV", 2, 5), ("MV", 2, 6), ("MV", 2, 7), ("EX", 2, 3, 0),
-    ("CV", 2, 0, "s"), ("EX", 2, 3, 1), ("CV", 2, 1, "v"), ("QA", 1, 1), ("CV", 2, 2, "v"), ("EX", 2, 2, 0),
-    ("CV", 2, 3, "v"), ("EX", 2, 2, 1), ("QA", 1, 0), ("FO", 1, 2), ("FO", 1, 3), ("FO", 1, 0), ("FO", 1, 1),
-    ("CV", 2, 4, "s"), ("RC", 2, 0), ("NO", 2, 3, 0, "g"), ("NO", 2, 3, 1, "g"), ("NO", 2, 2, 0, "g"),
-    ("NO", 2, 2, 1, "g"), ("CV", 2, 5, "s"), ("EX", 2, 1, 0), ("QV", 2, 0), ("EX", 2, 1, 1), ("CV", 2, 6, "v"),
-    ("CV", 2, 7, "v"), ("EX", 2, 0, 0), ("EX", 2, 0, 1), ("CO", 1, 2, "s"), ("CO", 1, 3, "v"), ("ST", 1, 1),
-    ("QV", 2, 1), ("RC", 2, 1), ("NO", 2, 1, 0, "g"), ("NO", 2, 1, 1, "g"), ("NO", 2, 0, 0, "g"),
-    ("NO", 2, 0, 1, "g"), ("CO", 1, 0, "s"), ("CO", 1, 1, "s"), ("ST", 1, 0), ("TX", 4, 0), ("CX", 4, 0, "s"),
-    ("SC", 3, 3, 0), ("RX", 3, 3, 0), ("TX", 4, 1), ("CX", 4, 1, "s"), ("SC", 3, 3, 1), ("RX", 3, 3, 1), ("TQ", 4, 0),
-    ("CQ", 4, 0, "s"), ("SC", 3, 2, 0), ("RX", 3, 2, 0), ("TQ", 4, 1), ("CQ", 4, 1, "s"), ("SC", 3, 2, 1),
-    ("RX", 3, 2, 1), ("TA", 2, 1), ("CA", 2, 1, "s"), ("SC", 3, 1), ("RX", 3, 1, 0), ("RX", 3, 1, 1), ("QX", 4),
-    ("TA", 2, 2), ("CA", 2, 2, "v"), ("SC", 3, 0), ("RX", 3, 0, 0), ("RX", 3, 0, 1), ("TA", 2, 0), ("CA", 2, 0, "s"),
-    ("MV", 3, 0), ("MV", 3, 1), ("MV", 3, 2), ("MV", 3, 3), ("MV", 3, 4), ("MV", 3, 5), ("MV", 3, 6), ("MV", 3, 7),
-    ("EX", 3, 3, 0), ("CV", 3, 0, "s"), ("EX", 3, 3, 1), ("CV", 3, 1, "v"), ("QA", 2, 1), ("CV", 3, 2, "v"),
-    ("EX", 3, 2, 0), ("CV", 3, 3, "v"), ("EX", 3, 2, 1), ("QA", 2, 0), ("FO", 2, 2), ("FO", 2, 3), ("FO", 2, 0),
-    ("FO", 2, 1), ("CV", 3, 4, "s"), ("RC", 3, 0), ("NO", 3, 3, 0, "g"), ("NO", 3, 3, 1, "g"), ("NO", 3, 2, 0, "g"),
-    ("NO", 3, 2, 1, "g"), ("CV", 3, 5, "s"), ("EX", 3, 1, 0), ("QV", 3, 0), ("EX", 3, 1, 1), ("CV", 3, 6, "v"),
-    ("CV", 3, 7, "v"), ("EX", 3, 0, 0), ("EX", 3, 0, 1), ("CO", 2, 2, "s"), ("CO", 2, 3, "v"), ("ST", 2, 1),
-    ("QV", 3, 1), ("RC", 3, 1), ("NO", 3, 1, 0, "g"), ("NO", 3, 1, 1, "g"), ("NO", 3, 0, 0, "g"),
-    ("NO", 3, 0, 1, "g"), ("CO", 2, 0, "s"), ("CO", 2, 1, "s"), ("ST", 2, 0), ("TX", 5, 0), ("CX", 5, 0, "s"),
-    ("SC", 4, 3, 0), ("RX", 4, 3, 0), ("TX", 5, 1), ("CX", 5, 1, "s"), ("SC", 4, 3, 1), ("RX", 4, 3, 1), ("TQ", 5, 0),
-    ("CQ", 5, 0, "s"), ("SC", 4, 2, 0), ("RX", 4, 2, 0), ("TQ", 5, 1), ("CQ", 5, 1, "s"), ("SC", 4, 2, 1),
-    ("RX", 4, 2, 1), ("TA", 3, 1), ("CA", 3, 1, "s"), ("SC", 4, 1), ("RX", 4, 1, 0), ("RX", 4, 1, 1), ("QX", 5),
-    ("TA", 3, 2), ("CA", 3, 2, "v"), ("SC", 4, 0), ("RX", 4, 0, 0), ("RX", 4, 0, 1), ("TA", 3, 0), ("CA", 3, 0, "s"),
-    ("MV", 4, 0), ("MV", 4, 1), ("MV", 4, 2), ("MV", 4, 3), ("MV", 4, 4), ("MV", 4, 5), ("MV", 4, 6), ("MV", 4, 7),
-    ("EX", 4, 3, 0), ("CV", 4, 0, "s"), ("EX", 4, 3, 1), ("CV", 4, 1, "v"), ("QA", 3, 1), ("CV", 4, 2, "v"),
-    ("EX", 4, 2, 0), ("CV", 4, 3, "v"), ("EX", 4, 2, 1), ("QA", 3, 0), ("FO", 3, 2), ("FO", 3, 3), ("FO", 3, 0),
-    ("FO", 3, 1), ("CV", 4, 4, "s"), ("RC", 4, 0), ("NO", 4, 3, 0, "g"), ("NO", 4, 3, 1, "g"), ("NO", 4, 2, 0, "g"),
-    ("NO", 4, 2, 1, "g"), ("CV", 4, 5, "s"), ("EX", 4, 1, 0), ("QV", 4, 0), ("EX", 4, 1, 1), ("CV", 4, 6, "v"),
-    ("CV", 4, 7, "v"), ("EX", 4, 0, 0), ("EX", 4, 0, 1), ("CO", 3, 2, "s"), ("CO", 3, 3, "v"), ("ST", 3, 1),
-    ("QV", 4, 1), ("RC", 4, 1), ("NO", 4, 1, 0, "g"), ("NO", 4, 1, 1, "g"), ("NO", 4, 0, 0, "g"),
-    ("NO", 4, 0, 1, "g"), ("CO", 3, 0, "s"), ("CO", 3, 1, "s"), ("ST", 3, 0), ("TX", 6, 0), ("CX", 6, 0, "s"),
-    ("SC", 5, 3, 0), ("RX", 5, 3, 0), ("TX", 6, 1), ("CX", 6, 1, "s"), ("SC", 5, 3, 1), ("RX", 5, 3, 1), ("TQ", 6, 0),
-    ("CQ", 6, 0, "s"), ("SC", 5, 2, 0), ("RX", 5, 2, 0), ("TQ", 6, 1), ("CQ", 6, 1, "s"), ("SC", 5, 2, 1),
-    ("RX", 5, 2, 1), ("TA", 4, 1), ("CA", 4, 1, "s"), ("SC", 5, 1), ("RX", 5, 1, 0), ("RX", 5, 1, 1), ("QX", 6),
-    ("TA", 4, 2), ("CA", 4, 2, "v"), ("SC", 5, 0), ("RX", 5, 0, 0), ("RX", 5, 0, 1), ("TA", 4, 0), ("CA", 4, 0, "s"),
-    ("MV", 5, 0), ("MV", 5, 1), ("MV", 5, 2), ("MV", 5, 3), ("MV", 5, 4), ("MV", 5, 5), ("MV", 5, 6), ("MV", 5, 7),
-    ("EX", 5, 3, 0), ("CV", 5, 0, "s"), ("EX", 5, 3, 1), ("CV", 5, 1, "v"), ("QA", 4, 1), ("CV", 5, 2, "v"),
-    ("EX", 5, 2, 0), ("CV", 5, 3, "v"), ("EX", 5, 2, 1), ("QA", 4, 0), ("FO", 4, 2), ("FO", 4, 3), ("FO", 4, 0),
-    ("FO", 4, 1), ("CV", 5, 4, "s"), ("RC", 5, 0), ("NO", 5, 3, 0, "g"), ("NO", 5, 3, 1, "g"), ("NO", 5, 2, 0, "g"),
-    ("NO", 5, 2, 1, "g"), ("CV", 5, 5, "s"), ("EX", 5, 1, 0), ("QV", 5, 0), ("EX", 5, 1, 1), ("CV", 5, 6, "v"),
-    ("CV", 5, 7, "v"), ("EX", 5, 0, 0), ("EX", 5, 0, 1), ("CO", 4, 2, "s"), ("CO", 4, 3, "v"), ("ST", 4, 1),
-    ("QV", 5, 1), ("RC", 5, 1), ("NO", 5, 1, 0, "g"), ("NO", 5, 1, 1, "g"), ("NO", 5, 0, 0, "g"),
-    ("NO", 5, 0, 1, "g"), ("CO", 4, 0, "s"), ("CO", 4, 1, "s"), ("ST", 4, 0), ("TX", 7, 0), ("CX", 7, 0, "s"),
-    ("SC", 6, 3, 0), ("RX", 6, 3, 0), ("TX", 7, 1), ("CX", 7, 1, "s"), ("SC", 6, 3, 1), ("RX", 6, 3, 1), ("TQ", 7, 0),
-    ("CQ", 7, 0, "s"), ("SC", 6, 2, 0), ("RX", 6, 2, 0), ("TQ", 7, 1), ("CQ", 7, 1, "s"), ("SC", 6, 2, 1),
-    ("RX", 6, 2, 1), ("TA", 5, 1), ("CA", 5, 1, "s"), ("SC", 6, 1), ("RX", 6, 1, 0), ("RX", 6, 1, 1), ("QX", 7),
-    ("TA", 5, 2), ("CA", 5, 2, "v"), ("SC", 6, 0), ("RX", 6, 0, 0), ("RX", 6, 0, 1), ("TA", 5, 0), ("CA", 5, 0, "s"),
-    ("MV", 6, 0), ("MV", 6, 1), ("MV", 6, 2), ("MV", 6, 3), ("MV", 6, 4), ("MV", 6, 5), ("MV", 6, 6), ("MV", 6, 7),
-    ("EX", 6, 3, 0), ("CV", 6, 0, "s"), ("EX", 6, 3, 1), ("CV", 6, 1, "v"), ("QA", 5, 1), ("CV", 6, 2, "v"),
-    ("EX", 6, 2, 0), ("CV", 6, 3, "v"), ("EX", 6, 2, 1), ("QA", 5, 0), ("FO", 5, 2), ("FO", 5, 3), ("FO", 5, 0),
-    ("FO", 5, 1), ("CV", 6, 4, "s"), ("RC", 6, 0), ("NO", 6, 3, 0, "g"), ("NO", 6, 3, 1, "g"), ("NO", 6, 2, 0, "g"),
-    ("NO", 6, 2, 1, "g"), ("CV", 6, 5, "s"), ("EX", 6, 1, 0), ("QV", 6, 0), ("EX", 6, 1, 1), ("CV", 6, 6, "v"),
-    ("CV", 6, 7, "v"), ("EX", 6, 0, 0), ("EX", 6, 0, 1), ("CO", 5, 2, "s"), ("CO", 5, 3, "v"), ("ST", 5, 1),
-    ("QV", 6, 1), ("RC", 6, 1), ("NO", 6, 1, 0, "g"), ("NO", 6, 1, 1, "g"), ("NO", 6, 0, 0, "g"),
-    ("NO", 6, 0, 1, "g"), ("CO", 5, 0, "s"), ("CO", 5, 1, "s"), ("ST", 5, 0), ("SC", 7, 3, 0), ("RX", 7, 3, 0),
-    ("SC", 7, 3, 1), ("RX", 7, 3, 1), ("SC", 7, 2, 0), ("RX", 7, 2, 0), ("SC", 7, 2, 1), ("RX", 7, 2, 1),
-    ("TA", 6, 1), ("CA", 6, 1, "s"), ("SC", 7, 1), ("RX", 7, 1, 0), ("RX", 7, 1, 1), ("TA", 6, 2), ("CA", 6, 2, "v"),
-    ("SC", 7, 0), ("RX", 7, 0, 0), ("RX", 7, 0, 1), ("TA", 6, 0), ("CA", 6, 0, "s"), ("MV", 7, 0), ("MV", 7, 1),
-    ("MV", 7, 2), ("MV", 7, 3), ("MV", 7, 4), ("MV", 7, 5), ("MV", 7, 6), ("MV", 7, 7), ("EX", 7, 3, 0),
-    ("CV", 7, 0, "v"), ("EX", 7, 3, 1), ("QA", 6, 1), ("CV", 7, 1, "v"), ("EX", 7, 2, 0), ("QA", 6, 0),
-    ("EX", 7, 2, 1), ("FO", 6, 2), ("FO", 6, 3), ("FO", 6, 0), ("FO", 6, 1), ("CV", 7, 2, "v"), ("EX", 7, 1, 0),
-    ("EX", 7, 1, 1), ("RC", 7, 0), ("NO", 7, 3, 0, "g"), ("NO", 7, 3, 1, "v"), ("NO", 7, 2, 0, "g"),
-    ("NO", 7, 2, 1, "v"), ("EX", 7, 0, 0), ("EX", 7, 0, 1), ("CV", 7, 3, "v"), ("CV", 7, 4, "s"), ("RC", 7, 1),
-    ("NO", 7, 1, 0, "g"), ("NO", 7, 1, 1, "v"), ("NO", 7, 0, 0, "g"), ("NO", 7, 0, 1, "v"), ("CV", 7, 5, "s"),
-    ("QV", 7, 0), ("CV", 7, 6, "s"), ("CV", 7, 7, "v"), ("TA", 7, 1), ("TA", 7, 2), ("TA", 7, 0), ("CO", 6, 2, "s"),
-    ("QV", 7, 1), ("CO", 6, 3, "v"), ("ST", 6, 1), ("CA", 7, 1, "s"), ("CA", 7, 2, "v"), ("CA", 7, 0, "s"),
-    ("QA", 7, 1), ("FO", 7, 2), ("FO", 7, 3), ("CO", 6, 0, "v"), ("QA", 7, 0), ("CO", 6, 1, "s"), ("ST", 6, 0),
-    ("FO", 7, 0), ("FO", 7, 1), ("CO", 7, 2, "v"), ("ST4", 7, 2), ("CO", 7, 3, "s"), ("ST4", 7, 3), ("CO", 7, 0, "v"),
-    ("ST4", 7, 0), ("CO", 7, 1, "s"), ("ST4", 7, 1),
+    ("INIT",), ("LQ", 0), ("LK", 0), ("TQ", 0, 0), ("LM",), ("LX", 0), ("TQ", 0, 1), ("CQ", 0, 0, "v"), ("MB",),
+    ("CQ", 0, 1, "s"), ("LW", 0), ("SC", 0, 3, 0), ("SC", 0, 3, 1), ("LW", 1), ("SC", 0, 2, 0), ("SC", 0, 2, 1),
+    ("RX", 0, 3, 0), ("SC", 0, 1), ("RX", 0, 2, 0), ("SC", 0, 0), ("TX", 0, 0), ("LQ", 1), ("RX", 0, 3, 1),
+    ("EX", 0, 3, 0), ("TX", 0, 1), ("TW", 0), ("RX", 0, 1, 1), ("LK", 1), ("CX", 0, 0, "s"), ("TW", 1),
+    ("RX", 0, 1, 0), ("TW", 2), ("CX", 0, 1, "s"), ("RX", 0, 0, 0), ("LX", 1), ("TW", 3), ("RX", 0, 0, 1),
+    ("RX", 0, 2, 1), ("TQ", 1, 0), ("CW", 0, "s"), ("CW", 2, "v"), ("TQ", 1, 1), ("CW", 1, "s"), ("QX", 0), ("LX", 2),
+    ("EX", 0, 0, 0), ("EX", 0, 1, 0), ("TX", 1, 0), ("CW", 3, "v"), ("EX", 0, 2, 0), ("TX", 1, 1), ("QW", 1),
+    ("EX", 0, 3, 1), ("LQ", 2), ("QW", 0), ("EX", 0, 0, 1), ("EX", 0, 2, 1), ("LK", 2), ("CX", 1, 0, "v"),
+    ("EX", 0, 1, 1), ("MV", 0, 0), ("CQ", 1, 0, "v"), ("CX", 1, 1, "s"), ("LX", 3), ("MV", 0, 1), ("CQ", 1, 1, "v"),
+    ("MV", 0, 2), ("MV", 0, 3), ("RC", 0, 1), ("RC", 0, 0), ("CV", 0, 0, "v"), ("MV", 0, 4), ("CV", 0, 1, "s"),
+    ("LQ", 3), ("MV", 0, 5), ("NO", 0, 0, 1, "g"), ("QX", 1), ("CV", 0, 2, "s"), ("MV", 0, 6), ("NO", 0, 3, 1, "g"),
+    ("MV", 0, 7), ("LK", 3), ("CV", 0, 4, "s"), ("CV", 0, 3, "v"), ("TX", 2, 0), ("NO", 0, 2, 0, "g"),
+    ("CV", 0, 6, "s"), ("CV", 0, 5, "v"), ("SC", 1, 3, 0), ("LX", 4), ("TX", 2, 1), ("NO", 0, 3, 0, "g"),
+    ("CV", 0, 7, "s"), ("QV", 0, 0), ("SC", 1, 3, 1), ("TQ", 2, 0), ("CX", 2, 0, "s"), ("RX", 1, 3, 0),
+    ("NO", 0, 2, 1, "g"), ("LQ", 4), ("SC", 1, 2, 0), ("CX", 2, 1, "s"), ("RX", 1, 3, 1), ("TQ", 2, 1),
+    ("NO", 0, 1, 0, "g"), ("CQ", 2, 0, "s"), ("LK", 4), ("SC", 1, 2, 1), ("QV", 0, 1), ("NO", 0, 1, 1, "g"),
+    ("TA", 0, 1), ("EX", 1, 3, 0), ("LX", 5), ("NO", 0, 0, 0, "g"), ("RX", 1, 2, 0), ("SC", 1, 1), ("EX", 1, 3, 1),
+    ("RX", 1, 2, 1), ("TA", 0, 2), ("CA", 0, 1, "s"), ("CQ", 2, 1, "v"), ("SC", 1, 0), ("TA", 0, 0), ("LQ", 5),
+    ("RX", 1, 1, 1), ("RX", 1, 1, 0), ("MV", 1, 0), ("EX", 1, 2, 1), ("LK", 5), ("RX", 1, 0, 1), ("MV", 1, 1),
+    ("CA", 0, 2, "v"), ("EX", 1, 2, 0), ("MV", 1, 2), ("LX", 6), ("MV", 1, 3), ("CA", 0, 0, "s"), ("MV", 1, 4),
+    ("MV", 1, 5), ("CV", 1, 0, "v"), ("MV", 1, 6), ("CV", 1, 1, "s"), ("QA", 0, 1), ("LQ", 6), ("MV", 1, 7),
+    ("CV", 1, 5, "s"), ("RC", 1, 0), ("CV", 1, 2, "v"), ("LK", 6), ("CV", 1, 3, "s"), ("FO", 0, 2),
+    ("NO", 1, 2, 0, "g"), ("QA", 0, 0), ("RX", 1, 0, 0), ("EX", 1, 1, 0), ("FO", 0, 3), ("LX", 7), ("CV", 1, 4, "v"),
+    ("NO", 1, 2, 1, "g"), ("EX", 1, 0, 1), ("FO", 0, 0), ("EX", 1, 1, 1), ("CV", 1, 6, "v"), ("NO", 1, 3, 0, "g"),
+    ("FO", 0, 1), ("EX", 1, 0, 0), ("TX", 3, 0), ("CV", 1, 7, "s"), ("QX", 2), ("LQ", 7), ("SC", 2, 3, 0),
+    ("NO", 1, 3, 1, "g"), ("CO", 0, 2, "s"), ("CO", 0, 0, "v"), ("TX", 3, 1), ("LK", 7), ("SC", 2, 3, 1),
+    ("CO", 0, 1, "s"), ("RC", 1, 1), ("QV", 1, 0), ("TQ", 3, 0), ("CO", 0, 3, "s"), ("NO", 1, 0, 1, "g"),
+    ("RX", 2, 3, 0), ("SC", 2, 2, 0), ("NO", 1, 1, 1, "g"), ("CX", 3, 0, "s"), ("TQ", 3, 1), ("RX", 2, 3, 1),
+    ("NO", 1, 0, 0, "g"), ("ST", 0, 1), ("CX", 3, 1, "s"), ("SC", 2, 2, 1), ("NO", 1, 1, 0, "g"), ("QV", 1, 1),
+    ("TA", 1, 1), ("CQ", 3, 0, "s"), ("SC", 2, 1), ("RX", 2, 2, 0), ("EX", 2, 3, 0), ("TA", 1, 2), ("ST", 0, 0),
+    ("RX", 2, 2, 1), ("EX", 2, 3, 1), ("SC", 2, 0), ("CQ", 3, 1, "v"), ("TA", 1, 0), ("CA", 1, 1, "s"),
+    ("RX", 2, 1, 1), ("MV", 2, 0), ("RX", 2, 1, 0), ("MV", 2, 1), ("RX", 2, 0, 1), ("EX", 2, 2, 1), ("MV", 2, 2),
+    ("CA", 1, 2, "v"), ("MV", 2, 3), ("EX", 2, 2, 0), ("MV", 2, 4), ("MV", 2, 5), ("CA", 1, 0, "s"),
+    ("CV", 2, 0, "v"), ("MV", 2, 6), ("QA", 1, 1), ("CV", 2, 1, "s"), ("MV", 2, 7), ("RC", 2, 0), ("CV", 2, 2, "v"),
+    ("CV", 2, 5, "s"), ("FO", 1, 2), ("NO", 2, 2, 0, "g"), ("QA", 1, 0), ("CV", 2, 3, "s"), ("RX", 2, 0, 0),
+    ("FO", 1, 3), ("CV", 2, 4, "v"), ("NO", 2, 2, 1, "g"), ("EX", 2, 1, 0), ("FO", 1, 0), ("CV", 2, 6, "v"),
+    ("EX", 2, 0, 1), ("NO", 2, 3, 0, "g"), ("FO", 1, 1), ("EX", 2, 1, 1), ("TX", 4, 0), ("QX", 3), ("EX", 2, 0, 0),
+    ("CV", 2, 7, "s"), ("SC", 3, 3, 0), ("NO", 2, 3, 1, "g"), ("CO", 1, 0, "v"), ("TX", 4, 1), ("CO", 1, 2, "s"),
+    ("RC", 2, 1), ("QV", 2, 0), ("SC", 3, 3, 1), ("CO", 1, 1, "s"), ("NO", 2, 0, 1, "g"), ("RX", 3, 3, 0),
+    ("TQ", 4, 0), ("CO", 1, 3, "s"), ("NO", 2, 1, 1, "g"), ("SC", 3, 2, 0), ("RX", 3, 3, 1), ("CX", 4, 0, "s"),
+    ("NO", 2, 0, 0, "g"), ("TQ", 4, 1), ("ST", 1, 1), ("NO", 2, 1, 0, "g"), ("CX", 4, 1, "s"), ("QV", 2, 1),
+    ("SC", 3, 2, 1), ("TA", 2, 1), ("CQ", 4, 0, "s"), ("RX", 3, 2, 0), ("SC", 3, 1), ("EX", 3, 3, 0), ("RX", 3, 2, 1),
+    ("TA", 2, 2), ("ST", 1, 0), ("CQ", 4, 1, "v"), ("EX", 3, 3, 1), ("SC", 3, 0), ("RX", 3, 1, 1), ("TA", 2, 0),
+    ("CA", 2, 1, "s"), ("RX", 3, 1, 0), ("MV", 3, 0), ("RX", 3, 0, 1), ("CA", 2, 2, "v"), ("MV", 3, 1),
+    ("EX", 3, 2, 1), ("MV", 3, 2), ("MV", 3, 3), ("EX", 3, 2, 0), ("MV", 3, 4), ("CV", 3, 0, "v"), ("MV", 3, 5),
+    ("CA", 2, 0, "s"), ("MV", 3, 6), ("QA", 2, 1), ("RC", 3, 0), ("CV", 3, 2, "v"), ("CV", 3, 1, "s"),
+    ("NO", 3, 2, 0, "g"), ("MV", 3, 7), ("QA", 2, 0), ("CV", 3, 5, "s"), ("RX", 3, 0, 0), ("FO", 2, 2),
+    ("CV", 3, 4, "v"), ("NO", 3, 2, 1, "g"), ("CV", 3, 3, "s"), ("FO", 2, 3), ("CV", 3, 6, "v"), ("EX", 3, 1, 0),
+    ("NO", 3, 3, 0, "g"), ("FO", 2, 0), ("EX", 3, 0, 1), ("QX", 4), ("FO", 2, 1), ("EX", 3, 1, 1), ("TX", 5, 0),
+    ("NO", 3, 3, 1, "g"), ("EX", 3, 0, 0), ("CV", 3, 7, "s"), ("CO", 2, 0, "v"), ("SC", 4, 3, 0), ("TX", 5, 1),
+    ("CO", 2, 2, "s"), ("RC", 3, 1), ("QV", 3, 0), ("SC", 4, 3, 1), ("CO", 2, 1, "s"), ("NO", 3, 0, 1, "g"),
+    ("RX", 4, 3, 0), ("TQ", 5, 0), ("NO", 3, 1, 1, "g"), ("CO", 2, 3, "s"), ("SC", 4, 2, 0), ("RX", 4, 3, 1),
+    ("NO", 3, 0, 0, "g"), ("CX", 5, 0, "s"), ("TQ", 5, 1), ("NO", 3, 1, 0, "g"), ("QV", 3, 1), ("ST", 2, 1),
+    ("SC", 4, 2, 1), ("CX", 5, 1, "s"), ("TA", 3, 1), ("RX", 4, 2, 0), ("CQ", 5, 0, "s"), ("SC", 4, 1),
+    ("RX", 4, 2, 1), ("EX", 4, 3, 0), ("TA", 3, 2), ("ST", 2, 0), ("CQ", 5, 1, "v"), ("EX", 4, 3, 1), ("SC", 4, 0),
+    ("TA", 3, 0), ("RX", 4, 1, 1), ("CA", 3, 1, "s"), ("RX", 4, 1, 0), ("MV", 4, 0), ("RX", 4, 0, 1), ("MV", 4, 1),
+    ("CA", 3, 2, "v"), ("MV", 4, 2), ("EX", 4, 2, 1), ("MV", 4, 3), ("MV", 4, 4), ("EX", 4, 2, 0), ("CV", 4, 0, "v"),
+    ("MV", 4, 5), ("CA", 3, 0, "s"), ("MV", 4, 6), ("QA", 3, 1), ("MV", 4, 7), ("RC", 4, 0), ("CV", 4, 2, "v"),
+    ("CV", 4, 1, "s"), ("NO", 4, 2, 0, "g"), ("QA", 3, 0), ("FO", 3, 2), ("CV", 4, 5, "s"), ("RX", 4, 0, 0),
+    ("NO", 4, 2, 1, "g"), ("CV", 4, 4, "v"), ("FO", 3, 3), ("CV", 4, 3, "s"), ("CV", 4, 6, "v"), ("FO", 3, 0),
+    ("NO", 4, 3, 0, "g"), ("EX", 4, 1, 0), ("FO", 3, 1), ("EX", 4, 0, 1), ("QX", 5), ("TX", 6, 0), ("EX", 4, 1, 1),
+    ("NO", 4, 3, 1, "g"), ("EX", 4, 0, 0), ("SC", 5, 3, 0), ("CO", 3, 0, "v"), ("CV", 4, 7, "s"), ("TX", 6, 1),
+    ("RC", 4, 1), ("CO", 3, 2, "s"), ("QV", 4, 0), ("SC", 5, 3, 1), ("NO", 4, 0, 1, "g"), ("CO", 3, 1, "s"),
+    ("RX", 5, 3, 0), ("NO", 4, 1, 1, "g"), ("TQ", 6, 0), ("CO", 3, 3, "s"), ("NO", 4, 0, 0, "g"), ("RX", 5, 3, 1),
+    ("SC", 5, 2, 0), ("CX", 6, 0, "s"), ("NO", 4, 1, 0, "g"), ("TQ", 6, 1), ("QV", 4, 1), ("ST", 3, 1),
+    ("CX", 6, 1, "s"), ("SC", 5, 2, 1), ("TA", 4, 1), ("RX", 5, 2, 0), ("CQ", 6, 0, "s"), ("SC", 5, 1),
+    ("RX", 5, 2, 1), ("EX", 5, 3, 0), ("TA", 4, 2), ("ST", 3, 0), ("CQ", 6, 1, "v"), ("EX", 5, 3, 1), ("SC", 5, 0),
+    ("RX", 5, 1, 1), ("TA", 4, 0), ("CA", 4, 1, "s"), ("RX", 5, 1, 0), ("MV", 5, 0), ("RX", 5, 0, 1),
+    ("CA", 4, 2, "v"), ("MV", 5, 1), ("EX", 5, 2, 1), ("MV", 5, 2), ("MV", 5, 3), ("EX", 5, 2, 0), ("MV", 5, 4),
+    ("CV", 5, 0, "v"), ("MV", 5, 5), ("CA", 4, 0, "s"), ("MV", 5, 6), ("QA", 4, 1), ("RC", 5, 0), ("CV", 5, 2, "v"),
+    ("CV", 5, 1, "s"), ("NO", 5, 2, 0, "g"), ("MV", 5, 7), ("QA", 4, 0), ("CV", 5, 5, "s"), ("RX", 5, 0, 0),
+    ("FO", 4, 2), ("CV", 5, 4, "v"), ("NO", 5, 2, 1, "g"), ("CV", 5, 3, "s"), ("FO", 4, 3), ("CV", 5, 6, "v"),
+    ("EX", 5, 1, 0), ("NO", 5, 3, 0, "g"), ("FO", 4, 0), ("EX", 5, 0, 1), ("QX", 6), ("FO", 4, 1), ("EX", 5, 1, 1),
+    ("TX", 7, 0), ("NO", 5, 3, 1, "g"), ("EX", 5, 0, 0), ("CV", 5, 7, "s"), ("CO", 4, 0, "v"), ("SC", 6, 3, 0),
+    ("TX", 7, 1), ("CO", 4, 2, "s"), ("RC", 5, 1), ("QV", 5, 0), ("SC", 6, 3, 1), ("CO", 4, 1, "s"),
+    ("NO", 5, 0, 1, "g"), ("RX", 6, 3, 0), ("TQ", 7, 0), ("NO", 5, 1, 1, "g"), ("CO", 4, 3, "s"), ("SC", 6, 2, 0),
+    ("RX", 6, 3, 1), ("NO", 5, 0, 0, "g"), ("CX", 7, 0, "s"), ("TQ", 7, 1), ("NO", 5, 1, 0, "g"), ("QV", 5, 1),
+    ("ST", 4, 1), ("SC", 6, 2, 1), ("CX", 7, 1, "s"), ("TA", 5, 1), ("RX", 6, 2, 0), ("CQ", 7, 0, "s"), ("SC", 6, 1),
+    ("RX", 6, 2, 1), ("EX", 6, 3, 0), ("TA", 5, 2), ("ST", 4, 0), ("CQ", 7, 1, "v"), ("EX", 6, 3, 1), ("SC", 6, 0),
+    ("TA", 5, 0), ("RX", 6, 1, 1), ("CA", 5, 1, "s"), ("RX", 6, 1, 0), ("MV", 6, 0), ("RX", 6, 0, 1), ("MV", 6, 1),
+    ("CA", 5, 2, "v"), ("MV", 6, 2), ("EX", 6, 2, 1), ("MV", 6, 3), ("MV", 6, 4), ("EX", 6, 2, 0), ("CV", 6, 0, "v"),
+    ("MV", 6, 5), ("CA", 5, 0, "s"), ("MV", 6, 6), ("QA", 5, 1), ("MV", 6, 7), ("RC", 6, 0), ("CV", 6, 2, "v"),
+    ("CV", 6, 1, "s"), ("NO", 6, 2, 0, "g"), ("QA", 5, 0), ("FO", 5, 2), ("CV", 6, 5, "s"), ("RX", 6, 0, 0),
+    ("NO", 6, 2, 1, "g"), ("CV", 6, 4, "v"), ("FO", 5, 3), ("CV", 6, 3, "s"), ("CV", 6, 6, "v"), ("FO", 5, 0),
+    ("NO", 6, 3, 0, "g"), ("EX", 6, 1, 0), ("FO", 5, 1), ("EX", 6, 0, 1), ("QX", 7), ("SC", 7, 3, 0), ("EX", 6, 1, 1),
+    ("NO", 6, 3, 1, "g"), ("SC", 7, 3, 1), ("EX", 6, 0, 0), ("CO", 5, 0, "v"), ("CV", 6, 7, "s"), ("SC", 7, 2, 0),
+    ("RC", 6, 1), ("CO", 5, 2, "s"), ("RX", 7, 3, 0), ("SC", 7, 2, 1), ("NO", 6, 0, 1, "g"), ("CO", 5, 1, "s"),
+    ("RX", 7, 3, 1), ("NO", 6, 1, 1, "g"), ("TA", 6, 1), ("CO", 5, 3, "s"), ("RX", 7, 2, 0), ("NO", 6, 0, 0, "g"),
+    ("SC", 7, 1), ("EX", 7, 3, 0), ("RX", 7, 2, 1), ("NO", 6, 1, 0, "g"), ("TA", 6, 2), ("ST", 5, 1), ("EX", 7, 3, 1),
+    ("QV", 6, 1), ("SC", 7, 0), ("TA", 6, 0), ("RX", 7, 1, 1), ("EX", 7, 2, 1), ("RX", 7, 1, 0), ("MV", 7, 0),
+    ("EX", 7, 2, 0), ("RX", 7, 0, 1), ("ST", 5, 0), ("MV", 7, 1), ("CA", 6, 2, "v"), ("EX", 7, 1, 1), ("MV", 7, 2),
+    ("CA", 6, 1, "s"), ("MV", 7, 3), ("MV", 7, 4), ("RC", 7, 0), ("CV", 7, 0, "v"), ("EX", 7, 1, 0), ("MV", 7, 5),
+    ("NO", 7, 3, 0, "g"), ("RX", 7, 0, 0), ("CA", 6, 0, "s"), ("QV", 6, 0), ("MV", 7, 6), ("MV", 7, 7),
+    ("NO", 7, 2, 0, "g"), ("QA", 6, 1), ("CV", 7, 3, "s"), ("NO", 7, 3, 1, "g"), ("CV", 7, 1, "v"), ("EX", 7, 0, 0),
+    ("FO", 6, 2), ("QA", 6, 0), ("CV", 7, 4, "s"), ("NO", 7, 2, 1, "g"), ("CV", 7, 7, "v"), ("FO", 6, 3),
+    ("EX", 7, 0, 1), ("CV", 7, 2, "s"), ("FO", 6, 0), ("RC", 7, 1), ("FO", 6, 1), ("CV", 7, 6, "s"),
+    ("NO", 7, 0, 1, "v"), ("NO", 7, 1, 1, "v"), ("TA", 7, 1), ("CO", 6, 3, "v"), ("NO", 7, 0, 0, "g"),
+    ("CV", 7, 5, "s"), ("TA", 7, 2), ("NO", 7, 1, 0, "g"), ("QV", 7, 0), ("CO", 6, 2, "s"), ("QV", 7, 1),
+    ("CA", 7, 1, "s"), ("TA", 7, 0), ("ST", 6, 1), ("CA", 7, 2, "v"), ("CO", 6, 1, "s"), ("QA", 7, 1),
+    ("CA", 7, 0, "s"), ("CO", 6, 0, "v"), ("FO", 7, 2), ("QA", 7, 0), ("ST", 6, 0), ("FO", 7, 3), ("FO", 7, 0),
+    ("CO", 7, 2, "s"), ("FO", 7, 1), ("CO", 7, 3, "v"), ("CO", 7, 0, "s"), ("ST4", 7, 2), ("CO", 7, 1, "v"),
+    ("ST4", 7, 3), ("ST4", 7, 0), ("ST4", 7, 1),
 )
 
 

@@ -27,106 +27,105 @@ SEGS = (((0, 0), (1, 0)), ((2, 0), (3, 0)), ((2, 1), (3, 1)))
 ORDER = (
     ("INIT",), ("LQ", 0), ("LK", 0), ("TQ", 0, 0), ("LM",), ("LX", 0), ("TQ", 0, 1), ("CQ", 0, 0, "v"), ("MB",),
     ("CQ", 0, 1, "s"), ("LW", 0), ("SC", 0, 3, 0), ("SC", 0, 3, 1), ("LW", 1), ("SC", 0, 2, 0), ("SC", 0, 2, 1),
-    ("RX", 0, 3, 0), ("SC", 0, 1), ("RX", 0, 2, 0), ("SC", 0, 0), ("TX", 0, 0), ("LQ", 1), ("RX", 0, 3, 1),
-    ("EX", 0, 3, 0), ("TX", 0, 1), ("TW", 0), ("RX", 0, 1, 1), ("LK", 1), ("CX", 0, 0, "s"), ("TW", 1),
-    ("RX", 0, 1, 0), ("TW", 2), ("CX", 0, 1, "s"), ("RX", 0, 0, 0), ("LX", 1), ("TW", 3), ("RX", 0, 0, 1),
-    ("RX", 0, 2, 1), ("TQ", 1, 0), ("CW", 0, "s"), ("CW", 2, "v"), ("TQ", 1, 1), ("CW", 1, "s"), ("QX", 0), ("LX", 2),
-    ("EX", 0, 0, 0), ("EX", 0, 1, 0), ("TX", 1, 0), ("CW", 3, "v"), ("EX", 0, 2, 0), ("TX", 1, 1), ("QW", 1),
-    ("EX", 0, 3, 1), ("LQ", 2), ("QW", 0), ("EX", 0, 0, 1), ("EX", 0, 2, 1), ("LK", 2), ("CX", 1, 0, "v"),
-    ("EX", 0, 1, 1), ("MV", 0, 0), ("CQ", 1, 0, "v"), ("CX", 1, 1, "s"), ("LX", 3), ("MV", 0, 1), ("CQ", 1, 1, "v"),
-    ("MV", 0, 2), ("MV", 0, 3), ("RC", 0, 1), ("RC", 0, 0), ("CV", 0, 0, "v"), ("MV", 0, 4), ("CV", 0, 1, "s"),
-    ("LQ", 3), ("MV", 0, 5), ("NO", 0, 0, 1, "g"), ("QX", 1), ("CV", 0, 2, "s"), ("MV", 0, 6), ("NO", 0, 3, 1, "g"),
-    ("MV", 0, 7), ("LK", 3), ("CV", 0, 4, "s"), ("CV", 0, 3, "v"), ("TX", 2, 0), ("NO", 0, 2, 0, "g"),
-    ("CV", 0, 6, "s"), ("CV", 0, 5, "v"), ("SC", 1, 3, 0), ("LX", 4), ("TX", 2, 1), ("NO", 0, 3, 0, "g"),
-    ("CV", 0, 7, "s"), ("QV", 0, 0), ("SC", 1, 3, 1), ("TQ", 2, 0), ("CX", 2, 0, "s"), ("RX", 1, 3, 0),
-    ("NO", 0, 2, 1, "g"), ("LQ", 4), ("SC", 1, 2, 0), ("CX", 2, 1, "s"), ("RX", 1, 3, 1), ("TQ", 2, 1),
-    ("NO", 0, 1, 0, "g"), ("CQ", 2, 0, "s"), ("LK", 4), ("SC", 1, 2, 1), ("QV", 0, 1), ("NO", 0, 1, 1, "g"),
-    ("TA", 0, 1), ("EX", 1, 3, 0), ("LX", 5), ("NO", 0, 0, 0, "g"), ("RX", 1, 2, 0), ("SC", 1, 1), ("EX", 1, 3, 1),
-    ("RX", 1, 2, 1), ("TA", 0, 2), ("CA", 0, 1, "s"), ("CQ", 2, 1, "v"), ("SC", 1, 0), ("TA", 0, 0), ("LQ", 5),
-    ("RX", 1, 1, 1), ("RX", 1, 1, 0), ("MV", 1, 0), ("EX", 1, 2, 1), ("LK", 5), ("RX", 1, 0, 1), ("MV", 1, 1),
-    ("CA", 0, 2, "v"), ("EX", 1, 2, 0), ("MV", 1, 2), ("LX", 6), ("MV", 1, 3), ("CA", 0, 0, "s"), ("MV", 1, 4),
-    ("MV", 1, 5), ("CV", 1, 0, "v"), ("MV", 1, 6), ("CV", 1, 1, "s"), ("QA", 0, 1), ("LQ", 6), ("MV", 1, 7),
-    ("CV", 1, 5, "s"), ("RC", 1, 0), ("CV", 1, 2, "v"), ("LK", 6), ("CV", 1, 3, "s"), ("FO", 0, 2),
-    ("NO", 1, 2, 0, "g"), ("QA", 0, 0), ("RX", 1, 0, 0), ("EX", 1, 1, 0), ("FO", 0, 3), ("LX", 7), ("CV", 1, 4, "v"),
-    ("NO", 1, 2, 1, "g"), ("EX", 1, 0, 1), ("FO", 0, 0), ("EX", 1, 1, 1), ("CV", 1, 6, "v"), ("NO", 1, 3, 0, "g"),
-    ("FO", 0, 1), ("EX", 1, 0, 0), ("TX", 3, 0), ("CV", 1, 7, "s"), ("QX", 2), ("LQ", 7), ("SC", 2, 3, 0),
-    ("NO", 1, 3, 1, "g"), ("CO", 0, 2, "s"), ("CO", 0, 0, "v"), ("TX", 3, 1), ("LK", 7), ("SC", 2, 3, 1),
-    ("CO", 0, 1, "s"), ("RC", 1, 1), ("QV", 1, 0), ("TQ", 3, 0), ("CO", 0, 3, "s"), ("NO", 1, 0, 1, "g"),
-    ("RX", 2, 3, 0), ("SC", 2, 2, 0), ("NO", 1, 1, 1, "g"), ("CX", 3, 0, "s"), ("TQ", 3, 1), ("RX", 2, 3, 1),
-    ("NO", 1, 0, 0, "g"), ("ST", 0, 1), ("CX", 3, 1, "s"), ("SC", 2, 2, 1), ("NO", 1, 1, 0, "g"), ("QV", 1, 1),
-    ("TA", 1, 1), ("CQ", 3, 0, "s"), ("SC", 2, 1), ("RX", 2, 2, 0), ("EX", 2, 3, 0), ("TA", 1, 2), ("ST", 0, 0),
-    ("RX", 2, 2, 1), ("EX", 2, 3, 1), ("SC", 2, 0), ("CQ", 3, 1, "v"), ("TA", 1, 0), ("CA", 1, 1, "s"),
-    ("RX", 2, 1, 1), ("MV", 2, 0), ("RX", 2, 1, 0), ("MV", 2, 1), ("RX", 2, 0, 1), ("EX", 2, 2, 1), ("MV", 2, 2),
-    ("CA", 1, 2, "v"), ("MV", 2, 3), ("EX", 2, 2, 0), ("MV", 2, 4), ("MV", 2, 5), ("CA", 1, 0, "s"),
-    ("CV", 2, 0, "v"), ("MV", 2, 6), ("QA", 1, 1), ("CV", 2, 1, "s"), ("MV", 2, 7), ("RC", 2, 0), ("CV", 2, 2, "v"),
-    ("CV", 2, 5, "s"), ("FO", 1, 2), ("NO", 2, 2, 0, "g"), ("QA", 1, 0), ("CV", 2, 3, "s"), ("RX", 2, 0, 0),
-    ("FO", 1, 3), ("CV", 2, 4, "v"), ("NO", 2, 2, 1, "g"), ("EX", 2, 1, 0), ("FO", 1, 0), ("CV", 2, 6, "v"),
-    ("EX", 2, 0, 1), ("NO", 2, 3, 0, "g"), ("FO", 1, 1), ("EX", 2, 1, 1), ("TX", 4, 0), ("QX", 3), ("EX", 2, 0, 0),
-    ("CV", 2, 7, "s"), ("SC", 3, 3, 0), ("NO", 2, 3, 1, "g"), ("CO", 1, 0, "v"), ("TX", 4, 1), ("CO", 1, 2, "s"),
-    ("RC", 2, 1), ("QV", 2, 0), ("SC", 3, 3, 1), ("CO", 1, 1, "s"), ("NO", 2, 0, 1, "g"), ("RX", 3, 3, 0),
-    ("TQ", 4, 0), ("CO", 1, 3, "s"), ("NO", 2, 1, 1, "g"), ("SC", 3, 2, 0), ("RX", 3, 3, 1), ("CX", 4, 0, "s"),
-    ("NO", 2, 0, 0, "g"), ("TQ", 4, 1), ("ST", 1, 1), ("NO", 2, 1, 0, "g"), ("CX", 4, 1, "s"), ("QV", 2, 1),
-    ("SC", 3, 2, 1), ("TA", 2, 1), ("CQ", 4, 0, "s"), ("RX", 3, 2, 0), ("SC", 3, 1), ("EX", 3, 3, 0), ("RX", 3, 2, 1),
-    ("TA", 2, 2), ("ST", 1, 0), ("CQ", 4, 1, "v"), ("EX", 3, 3, 1), ("SC", 3, 0), ("RX", 3, 1, 1), ("TA", 2, 0),
-    ("CA", 2, 1, "s"), ("RX", 3, 1, 0), ("MV", 3, 0), ("RX", 3, 0, 1), ("CA", 2, 2, "v"), ("MV", 3, 1),
-    ("EX", 3, 2, 1), ("MV", 3, 2), ("MV", 3, 3), ("EX", 3, 2, 0), ("MV", 3, 4), ("CV", 3, 0, "v"), ("MV", 3, 5),
-    ("CA", 2, 0, "s"), ("MV", 3, 6), ("QA", 2, 1), ("RC", 3, 0), ("CV", 3, 2, "v"), ("CV", 3, 1, "s"),
-    ("NO", 3, 2, 0, "g"), ("MV", 3, 7), ("QA", 2, 0), ("CV", 3, 5, "s"), ("RX", 3, 0, 0), ("FO", 2, 2),
-    ("CV", 3, 4, "v"), ("NO", 3, 2, 1, "g"), ("CV", 3, 3, "s"), ("FO", 2, 3), ("CV", 3, 6, "v"), ("EX", 3, 1, 0),
-    ("NO", 3, 3, 0, "g"), ("FO", 2, 0), ("EX", 3, 0, 1), ("QX", 4), ("FO", 2, 1), ("EX", 3, 1, 1), ("TX", 5, 0),
-    ("NO", 3, 3, 1, "g"), ("EX", 3, 0, 0), ("CV", 3, 7, "s"), ("CO", 2, 0, "v"), ("SC", 4, 3, 0), ("TX", 5, 1),
-    ("CO", 2, 2, "s"), ("RC", 3, 1), ("QV", 3, 0), ("SC", 4, 3, 1), ("CO", 2, 1, "s"), ("NO", 3, 0, 1, "g"),
-    ("RX", 4, 3, 0), ("TQ", 5, 0), ("NO", 3, 1, 1, "g"), ("CO", 2, 3, "s"), ("SC", 4, 2, 0), ("RX", 4, 3, 1),
-    ("NO", 3, 0, 0, "g"), ("CX", 5, 0, "s"), ("TQ", 5, 1), ("NO", 3, 1, 0, "g"), ("QV", 3, 1), ("ST", 2, 1),
-    ("SC", 4, 2, 1), ("CX", 5, 1, "s"), ("TA", 3, 1), ("RX", 4, 2, 0), ("CQ", 5, 0, "s"), ("SC", 4, 1),
-    ("RX", 4, 2, 1), ("EX", 4, 3, 0), ("TA", 3, 2), ("ST", 2, 0), ("CQ", 5, 1, "v"), ("EX", 4, 3, 1), ("SC", 4, 0),
-    ("TA", 3, 0), ("RX", 4, 1, 1), ("CA", 3, 1, "s"), ("RX", 4, 1, 0), ("MV", 4, 0), ("RX", 4, 0, 1), ("MV", 4, 1),
-    ("CA", 3, 2, "v"), ("MV", 4, 2), ("EX", 4, 2, 1), ("MV", 4, 3), ("MV", 4, 4), ("EX", 4, 2, 0), ("CV", 4, 0, "v"),
-    ("MV", 4, 5), ("CA", 3, 0, "s"), ("MV", 4, 6), ("QA", 3, 1), ("MV", 4, 7), ("RC", 4, 0), ("CV", 4, 2, "v"),
-    ("CV", 4, 1, "s"), ("NO", 4, 2, 0, "g"), ("QA", 3, 0), ("FO", 3, 2), ("CV", 4, 5, "s"), ("RX", 4, 0, 0),
-    ("NO", 4, 2, 1, "g"), ("CV", 4, 4, "v"), ("FO", 3, 3), ("CV", 4, 3, "s"), ("CV", 4, 6, "v"), ("FO", 3, 0),
-    ("NO", 4, 3, 0, "g"), ("EX", 4, 1, 0), ("FO", 3, 1), ("EX", 4, 0, 1), ("QX", 5), ("TX", 6, 0), ("EX", 4, 1, 1),
-    ("NO", 4, 3, 1, "g"), ("EX", 4, 0, 0), ("SC", 5, 3, 0), ("CO", 3, 0, "v"), ("CV", 4, 7, "s"), ("TX", 6, 1),
-    ("RC", 4, 1), ("CO", 3, 2, "s"), ("QV", 4, 0), ("SC", 5, 3, 1), ("NO", 4, 0, 1, "g"), ("CO", 3, 1, "s"),
-    ("RX", 5, 3, 0), ("NO", 4, 1, 1, "g"), ("TQ", 6, 0), ("CO", 3, 3, "s"), ("NO", 4, 0, 0, "g"), ("RX", 5, 3, 1),
-    ("SC", 5, 2, 0), ("CX", 6, 0, "s"), ("NO", 4, 1, 0, "g"), ("TQ", 6, 1), ("QV", 4, 1), ("ST", 3, 1),
-    ("CX", 6, 1, "s"), ("SC", 5, 2, 1), ("TA", 4, 1), ("RX", 5, 2, 0), ("CQ", 6, 0, "s"), ("SC", 5, 1),
-    ("RX", 5, 2, 1), ("EX", 5, 3, 0), ("TA", 4, 2), ("ST", 3, 0), ("CQ", 6, 1, "v"), ("EX", 5, 3, 1), ("SC", 5, 0),
-    ("RX", 5, 1, 1), ("TA", 4, 0), ("CA", 4, 1, "s"), ("RX", 5, 1, 0), ("MV", 5, 0), ("RX", 5, 0, 1),
-    ("CA", 4, 2, "v"), ("MV", 5, 1), ("EX", 5, 2, 1), ("MV", 5, 2), ("MV", 5, 3), ("EX", 5, 2, 0), ("MV", 5, 4),
-    ("CV", 5, 0, "v"), ("MV", 5, 5), ("CA", 4, 0, "s"), ("MV", 5, 6), ("QA", 4, 1), ("RC", 5, 0), ("CV", 5, 2, "v"),
-    ("CV", 5, 1, "s"), ("NO", 5, 2, 0, "g"), ("MV", 5, 7), ("QA", 4, 0), ("CV", 5, 5, "s"), ("RX", 5, 0, 0),
-    ("FO", 4, 2), ("CV", 5, 4, "v"), ("NO", 5, 2, 1, "g"), ("CV", 5, 3, "s"), ("FO", 4, 3), ("CV", 5, 6, "v"),
-    ("EX", 5, 1, 0), ("NO", 5, 3, 0, "g"), ("FO", 4, 0), ("EX", 5, 0, 1), ("QX", 6), ("FO", 4, 1), ("EX", 5, 1, 1),
-    ("TX", 7, 0), ("NO", 5, 3, 1, "g"), ("EX", 5, 0, 0), ("CV", 5, 7, "s"), ("CO", 4, 0, "v"), ("SC", 6, 3, 0),
-    ("TX", 7, 1), ("CO", 4, 2, "s"), ("RC", 5, 1), ("QV", 5, 0), ("SC", 6, 3, 1), ("CO", 4, 1, "s"),
-    ("NO", 5, 0, 1, "g"), ("RX", 6, 3, 0), ("TQ", 7, 0), ("NO", 5, 1, 1, "g"), ("CO", 4, 3, "s"), ("SC", 6, 2, 0),
-    ("RX", 6, 3, 1), ("NO", 5, 0, 0, "g"), ("CX", 7, 0, "s"), ("TQ", 7, 1), ("NO", 5, 1, 0, "g"), ("QV", 5, 1),
-    ("ST", 4, 1), ("SC", 6, 2, 1), ("CX", 7, 1, "s"), ("TA", 5, 1), ("RX", 6, 2, 0), ("CQ", 7, 0, "s"), ("SC", 6, 1),
-    ("RX", 6, 2, 1), ("EX", 6, 3, 0), ("TA", 5, 2), ("ST", 4, 0), ("CQ", 7, 1, "v"), ("EX", 6, 3, 1), ("SC", 6, 0),
-    ("TA", 5, 0), ("RX", 6, 1, 1), ("CA", 5, 1, "s"), ("RX", 6, 1, 0), ("MV", 6, 0), ("RX", 6, 0, 1), ("MV", 6, 1),
-    ("CA", 5, 2, "v"), ("MV", 6, 2), ("EX", 6, 2, 1), ("MV", 6, 3), ("MV", 6, 4), ("EX", 6, 2, 0), ("CV", 6, 0, "v"),
-    ("MV", 6, 5), ("CA", 5, 0, "s"), ("MV", 6, 6), ("QA", 5, 1), ("MV", 6, 7), ("RC", 6, 0), ("CV", 6, 2, "v"),
-    ("CV", 6, 1, "s"), ("NO", 6, 2, 0, "g"), ("QA", 5, 0), ("FO", 5, 2), ("CV", 6, 5, "s"), ("RX", 6, 0, 0),
-    ("NO", 6, 2, 1, "g"), ("CV", 6, 4, "v"), ("FO", 5, 3), ("CV", 6, 3, "s"), ("CV", 6, 6, "v"), ("FO", 5, 0),
-    ("NO", 6, 3, 0, "g"), ("EX", 6, 1, 0), ("FO", 5, 1), ("EX", 6, 0, 1), ("QX", 7), ("SC", 7, 3, 0), ("EX", 6, 1, 1),
-    ("NO", 6, 3, 1, "g"), ("SC", 7, 3, 1), ("EX", 6, 0, 0), ("CO", 5, 0, "v"), ("CV", 6, 7, "s"), ("SC", 7, 2, 0),
-    ("RC", 6, 1), ("CO", 5, 2, "s"), ("RX", 7, 3, 0), ("SC", 7, 2, 1), ("NO", 6, 0, 1, "g"), ("CO", 5, 1, "s"),
-    ("RX", 7, 3, 1), ("NO", 6, 1, 1, "g"), ("TA", 6, 1), ("CO", 5, 3, "s"), ("RX", 7, 2, 0), ("NO", 6, 0, 0, "g"),
-    ("SC", 7, 1), ("EX", 7, 3, 0), ("RX", 7, 2, 1), ("NO", 6, 1, 0, "g"), ("TA", 6, 2), ("ST", 5, 1), ("EX", 7, 3, 1),
-    ("QV", 6, 1), ("SC", 7, 0), ("TA", 6, 0), ("RX", 7, 1, 1), ("EX", 7, 2, 1), ("RX", 7, 1, 0), ("MV", 7, 0),
-    ("EX", 7, 2, 0), ("RX", 7, 0, 1), ("ST", 5, 0), ("MV", 7, 1), ("CA", 6, 2, "v"), ("EX", 7, 1, 1), ("MV", 7, 2),
-    ("CA", 6, 1, "s"), ("MV", 7, 3), ("MV", 7, 4), ("RC", 7, 0), ("CV", 7, 0, "v"), ("EX", 7, 1, 0), ("MV", 7, 5),
-    ("NO", 7, 3, 0, "g"), ("RX", 7, 0, 0), ("CA", 6, 0, "s"), ("QV", 6, 0), ("MV", 7, 6), ("MV", 7, 7),
-    ("NO", 7, 2, 0, "g"), ("QA", 6, 1), ("CV", 7, 3, "s"), ("NO", 7, 3, 1, "g"), ("CV", 7, 1, "v"), ("EX", 7, 0, 0),
-    ("FO", 6, 2), ("QA", 6, 0), ("CV", 7, 4, "s"), ("NO", 7, 2, 1, "g"), ("CV", 7, 7, "v"), ("FO", 6, 3),
-    ("EX", 7, 0, 1), ("CV", 7, 2, "s"), ("FO", 6, 0), ("RC", 7, 1), ("FO", 6, 1), ("CV", 7, 6, "s"),
-    ("NO", 7, 0, 1, "v"), ("NO", 7, 1, 1, "v"), ("TA", 7, 1), ("CO", 6, 3, "v"), ("NO", 7, 0, 0, "g"),
-    ("CV", 7, 5, "s"), ("TA", 7, 2), ("NO", 7, 1, 0, "g"), ("QV", 7, 0), ("CO", 6, 2, "s"), ("QV", 7, 1),
-    ("CA", 7, 1, "s"), ("TA", 7, 0), ("ST", 6, 1), ("CA", 7, 2, "v"), ("CO", 6, 1, "s"), ("QA", 7, 1),
-    ("CA", 7, 0, "s"), ("CO", 6, 0, "v"), ("FO", 7, 2), ("QA", 7, 0), ("ST", 6, 0), ("FO", 7, 3), ("FO", 7, 0),
-    ("CO", 7, 2, "s"), ("FO", 7, 1), ("CO", 7, 3, "v"), ("CO", 7, 0, "s"), ("ST4", 7, 2), ("CO", 7, 1, "v"),
-    ("ST4", 7, 3), ("ST4", 7, 0), ("ST4", 7, 1),
+    ("RX", 0, 3, 0), ("SC", 0, 1), ("RX", 0, 2, 0), ("SC", 0, 0), ("TX", 0, 0), ("LQ", 1), ("RX", 0, 2, 1),
+    ("EX", 0, 3, 0), ("TX", 0, 1), ("RX", 0, 3, 1), ("TW", 0), ("LK", 1), ("CX", 0, 0, "s"), ("TW", 1),
+    ("RX", 0, 1, 0), ("TW", 2), ("CX", 0, 1, "s"), ("LX", 1), ("RX", 0, 1, 1), ("TW", 3), ("RX", 0, 0, 0),
+    ("CW", 0, "s"), ("TQ", 1, 0), ("RX", 0, 0, 1), ("CW", 2, "v"), ("CW", 1, "s"), ("TQ", 1, 1), ("QX", 0), ("LX", 2),
+    ("EX", 0, 3, 1), ("TX", 1, 0), ("CW", 3, "v"), ("EX", 0, 2, 0), ("TX", 1, 1), ("QW", 0), ("EX", 0, 2, 1),
+    ("LQ", 2), ("QW", 1), ("EX", 0, 1, 0), ("EX", 0, 1, 1), ("LK", 2), ("CQ", 1, 0, "v"), ("EX", 0, 0, 0),
+    ("EX", 0, 0, 1), ("MV", 0, 0), ("CQ", 1, 1, "v"), ("CX", 1, 1, "s"), ("LX", 3), ("MV", 0, 1), ("RC", 0, 0),
+    ("CX", 1, 0, "v"), ("MV", 0, 2), ("MV", 0, 3), ("NO", 0, 2, 1, "g"), ("MV", 0, 4), ("CV", 0, 1, "s"), ("LQ", 3),
+    ("MV", 0, 5), ("RC", 0, 1), ("CV", 0, 0, "v"), ("NO", 0, 2, 0, "g"), ("CV", 0, 2, "s"), ("MV", 0, 6),
+    ("MV", 0, 7), ("LK", 3), ("CV", 0, 4, "s"), ("QX", 1), ("TX", 2, 0), ("CV", 0, 6, "s"), ("SC", 1, 3, 0),
+    ("LX", 4), ("CV", 0, 3, "v"), ("NO", 0, 3, 0, "g"), ("TX", 2, 1), ("CV", 0, 7, "s"), ("CV", 0, 5, "v"),
+    ("SC", 1, 3, 1), ("NO", 0, 3, 1, "g"), ("TQ", 2, 0), ("CX", 2, 0, "s"), ("RX", 1, 3, 0), ("LQ", 4),
+    ("SC", 1, 2, 0), ("CX", 2, 1, "s"), ("NO", 0, 1, 0, "g"), ("TQ", 2, 1), ("RX", 1, 3, 1), ("NO", 0, 1, 1, "g"),
+    ("CQ", 2, 0, "s"), ("LK", 4), ("SC", 1, 2, 1), ("RX", 1, 2, 0), ("TA", 0, 1), ("NO", 0, 0, 0, "g"),
+    ("EX", 1, 3, 0), ("LX", 5), ("NO", 0, 0, 1, "g"), ("SC", 1, 1), ("RX", 1, 2, 1), ("EX", 1, 3, 1), ("TA", 0, 2),
+    ("CQ", 2, 1, "v"), ("CA", 0, 1, "s"), ("SC", 1, 0), ("RX", 1, 1, 0), ("TA", 0, 0), ("LQ", 5), ("RX", 1, 1, 1),
+    ("MV", 1, 0), ("RX", 1, 0, 0), ("EX", 1, 2, 0), ("LK", 5), ("RX", 1, 0, 1), ("MV", 1, 1), ("CA", 0, 2, "v"),
+    ("EX", 1, 2, 1), ("MV", 1, 2), ("LX", 6), ("MV", 1, 3), ("CA", 0, 0, "s"), ("MV", 1, 4), ("MV", 1, 5),
+    ("QV", 0, 0), ("MV", 1, 6), ("CV", 1, 1, "s"), ("QV", 0, 1), ("LQ", 6), ("MV", 1, 7), ("CV", 1, 3, "s"),
+    ("QA", 0, 1), ("LK", 6), ("CV", 1, 5, "s"), ("QA", 0, 0), ("RC", 1, 0), ("CV", 1, 0, "v"), ("EX", 1, 1, 0),
+    ("LX", 7), ("FO", 0, 2), ("EX", 1, 1, 1), ("NO", 1, 3, 0, "g"), ("CV", 1, 2, "v"), ("FO", 0, 3), ("EX", 1, 0, 0),
+    ("EX", 1, 0, 1), ("CV", 1, 4, "v"), ("CV", 1, 7, "s"), ("FO", 0, 0), ("NO", 1, 3, 1, "g"), ("FO", 0, 1),
+    ("LQ", 7), ("CV", 1, 6, "v"), ("CO", 0, 2, "s"), ("TX", 3, 0), ("NO", 1, 2, 0, "g"), ("SC", 2, 3, 0),
+    ("CO", 0, 0, "v"), ("LK", 7), ("CO", 0, 3, "s"), ("TX", 3, 1), ("NO", 1, 2, 1, "g"), ("CO", 0, 1, "s"),
+    ("SC", 2, 3, 1), ("TQ", 3, 0), ("QX", 2), ("ST", 0, 1), ("CX", 3, 0, "s"), ("SC", 2, 2, 0), ("RC", 1, 1),
+    ("CX", 3, 1, "s"), ("RX", 2, 3, 0), ("TQ", 3, 1), ("NO", 1, 1, 0, "g"), ("CQ", 3, 0, "s"), ("SC", 2, 2, 1),
+    ("RX", 2, 3, 1), ("ST", 0, 0), ("TA", 1, 1), ("NO", 1, 1, 1, "g"), ("EX", 2, 3, 0), ("RX", 2, 2, 0), ("SC", 2, 1),
+    ("NO", 1, 0, 0, "g"), ("RX", 2, 2, 1), ("EX", 2, 3, 1), ("TA", 1, 2), ("NO", 1, 0, 1, "g"), ("CQ", 3, 1, "v"),
+    ("SC", 2, 0), ("CA", 1, 1, "s"), ("TA", 1, 0), ("RX", 2, 1, 0), ("RX", 2, 1, 1), ("MV", 2, 0), ("EX", 2, 2, 0),
+    ("RX", 2, 0, 0), ("MV", 2, 1), ("RX", 2, 0, 1), ("EX", 2, 2, 1), ("CA", 1, 2, "v"), ("MV", 2, 2), ("MV", 2, 3),
+    ("CA", 1, 0, "s"), ("MV", 2, 4), ("MV", 2, 5), ("QV", 1, 0), ("CV", 2, 1, "s"), ("MV", 2, 6), ("QV", 1, 1),
+    ("MV", 2, 7), ("CV", 2, 3, "s"), ("QA", 1, 1), ("CV", 2, 5, "s"), ("QA", 1, 0), ("RC", 2, 0), ("EX", 2, 1, 0),
+    ("CV", 2, 0, "v"), ("FO", 1, 2), ("EX", 2, 1, 1), ("NO", 2, 3, 0, "g"), ("CV", 2, 2, "v"), ("FO", 1, 3),
+    ("EX", 2, 0, 0), ("EX", 2, 0, 1), ("CV", 2, 4, "v"), ("CV", 2, 7, "s"), ("FO", 1, 0), ("NO", 2, 3, 1, "g"),
+    ("FO", 1, 1), ("CO", 1, 2, "s"), ("CV", 2, 6, "v"), ("TX", 4, 0), ("NO", 2, 2, 0, "g"), ("CO", 1, 3, "s"),
+    ("SC", 3, 3, 0), ("CO", 1, 0, "v"), ("TX", 4, 1), ("NO", 2, 2, 1, "g"), ("CO", 1, 1, "s"), ("SC", 3, 3, 1),
+    ("TQ", 4, 0), ("ST", 1, 1), ("CX", 4, 0, "s"), ("QX", 3), ("SC", 3, 2, 0), ("CX", 4, 1, "s"), ("RC", 2, 1),
+    ("RX", 3, 3, 0), ("TQ", 4, 1), ("CQ", 4, 0, "s"), ("NO", 2, 1, 0, "g"), ("SC", 3, 2, 1), ("RX", 3, 3, 1),
+    ("ST", 1, 0), ("TA", 2, 1), ("NO", 2, 1, 1, "g"), ("EX", 3, 3, 0), ("RX", 3, 2, 0), ("SC", 3, 1),
+    ("NO", 2, 0, 0, "g"), ("RX", 3, 2, 1), ("EX", 3, 3, 1), ("TA", 2, 2), ("NO", 2, 0, 1, "g"), ("CQ", 4, 1, "v"),
+    ("SC", 3, 0), ("CA", 2, 1, "s"), ("TA", 2, 0), ("RX", 3, 1, 0), ("RX", 3, 1, 1), ("MV", 3, 0), ("EX", 3, 2, 0),
+    ("RX", 3, 0, 0), ("MV", 3, 1), ("RX", 3, 0, 1), ("EX", 3, 2, 1), ("CA", 2, 2, "v"), ("MV", 3, 2), ("MV", 3, 3),
+    ("CA", 2, 0, "s"), ("MV", 3, 4), ("MV", 3, 5), ("QV", 2, 0), ("CV", 3, 1, "s"), ("MV", 3, 6), ("QV", 2, 1),
+    ("MV", 3, 7), ("CV", 3, 3, "s"), ("QA", 2, 1), ("CV", 3, 5, "s"), ("QA", 2, 0), ("RC", 3, 0), ("EX", 3, 1, 0),
+    ("CV", 3, 0, "v"), ("FO", 2, 2), ("EX", 3, 1, 1), ("NO", 3, 3, 0, "g"), ("CV", 3, 2, "v"), ("FO", 2, 3),
+    ("EX", 3, 0, 0), ("EX", 3, 0, 1), ("CV", 3, 4, "v"), ("CV", 3, 7, "s"), ("FO", 2, 0), ("NO", 3, 3, 1, "g"),
+    ("FO", 2, 1), ("CO", 2, 2, "s"), ("CV", 3, 6, "v"), ("TX", 5, 0), ("NO", 3, 2, 0, "g"), ("CO", 2, 3, "s"),
+    ("SC", 4, 3, 0), ("CO", 2, 0, "v"), ("TX", 5, 1), ("NO", 3, 2, 1, "g"), ("CO", 2, 1, "s"), ("SC", 4, 3, 1),
+    ("TQ", 5, 0), ("ST", 2, 1), ("CX", 5, 0, "s"), ("QX", 4), ("SC", 4, 2, 0), ("CX", 5, 1, "s"), ("RC", 3, 1),
+    ("RX", 4, 3, 0), ("TQ", 5, 1), ("CQ", 5, 0, "s"), ("NO", 3, 1, 0, "g"), ("SC", 4, 2, 1), ("RX", 4, 3, 1),
+    ("ST", 2, 0), ("TA", 3, 1), ("NO", 3, 1, 1, "g"), ("EX", 4, 3, 0), ("RX", 4, 2, 0), ("SC", 4, 1),
+    ("NO", 3, 0, 0, "g"), ("RX", 4, 2, 1), ("EX", 4, 3, 1), ("TA", 3, 2), ("NO", 3, 0, 1, "g"), ("CQ", 5, 1, "v"),
+    ("SC", 4, 0), ("CA", 3, 1, "s"), ("TA", 3, 0), ("RX", 4, 1, 0), ("RX", 4, 1, 1), ("MV", 4, 0), ("EX", 4, 2, 0),
+    ("RX", 4, 0, 0), ("MV", 4, 1), ("RX", 4, 0, 1), ("EX", 4, 2, 1), ("CA", 3, 2, "v"), ("MV", 4, 2), ("MV", 4, 3),
+    ("CA", 3, 0, "s"), ("MV", 4, 4), ("MV", 4, 5), ("QV", 3, 0), ("CV", 4, 1, "s"), ("MV", 4, 6), ("QV", 3, 1),
+    ("MV", 4, 7), ("CV", 4, 3, "s"), ("QA", 3, 1), ("CV", 4, 5, "s"), ("QA", 3, 0), ("RC", 4, 0), ("EX", 4, 1, 0),
+    ("CV", 4, 0, "v"), ("FO", 3, 2), ("EX", 4, 1, 1), ("NO", 4, 3, 0, "g"), ("CV", 4, 2, "v"), ("FO", 3, 3),
+    ("EX", 4, 0, 0), ("EX", 4, 0, 1), ("CV", 4, 4, "v"), ("CV", 4, 7, "s"), ("FO", 3, 0), ("NO", 4, 3, 1, "g"),
+    ("FO", 3, 1), ("CO", 3, 2, "s"), ("CV", 4, 6, "v"), ("TX", 6, 0), ("NO", 4, 2, 0, "g"), ("CO", 3, 3, "s"),
+    ("SC", 5, 3, 0), ("CO", 3, 0, "v"), ("TX", 6, 1), ("NO", 4, 2, 1, "g"), ("CO", 3, 1, "s"), ("SC", 5, 3, 1),
+    ("TQ", 6, 0), ("ST", 3, 1), ("CX", 6, 0, "s"), ("QX", 5), ("SC", 5, 2, 0), ("CX", 6, 1, "s"), ("RC", 4, 1),
+    ("RX", 5, 3, 0), ("TQ", 6, 1), ("CQ", 6, 0, "s"), ("NO", 4, 1, 0, "g"), ("SC", 5, 2, 1), ("RX", 5, 3, 1),
+    ("ST", 3, 0), ("TA", 4, 1), ("NO", 4, 1, 1, "g"), ("EX", 5, 3, 0), ("RX", 5, 2, 0), ("SC", 5, 1),
+    ("NO", 4, 0, 0, "g"), ("RX", 5, 2, 1), ("EX", 5, 3, 1), ("TA", 4, 2), ("NO", 4, 0, 1, "g"), ("CQ", 6, 1, "v"),
+    ("SC", 5, 0), ("CA", 4, 1, "s"), ("TA", 4, 0), ("RX", 5, 1, 0), ("RX", 5, 1, 1), ("MV", 5, 0), ("EX", 5, 2, 0),
+    ("RX", 5, 0, 0), ("MV", 5, 1), ("RX", 5, 0, 1), ("EX", 5, 2, 1), ("CA", 4, 2, "v"), ("MV", 5, 2), ("MV", 5, 3),
+    ("CA", 4, 0, "s"), ("MV", 5, 4), ("MV", 5, 5), ("QV", 4, 0), ("CV", 5, 1, "s"), ("MV", 5, 6), ("QV", 4, 1),
+    ("MV", 5, 7), ("CV", 5, 3, "s"), ("QA", 4, 1), ("CV", 5, 5, "s"), ("QA", 4, 0), ("RC", 5, 0), ("EX", 5, 1, 0),
+    ("CV", 5, 0, "v"), ("FO", 4, 2), ("EX", 5, 1, 1), ("NO", 5, 3, 0, "g"), ("CV", 5, 2, "v"), ("FO", 4, 3),
+    ("EX", 5, 0, 0), ("EX", 5, 0, 1), ("CV", 5, 4, "v"), ("CV", 5, 7, "s"), ("FO", 4, 0), ("NO", 5, 3, 1, "g"),
+    ("FO", 4, 1), ("CO", 4, 2, "s"), ("CV", 5, 6, "v"), ("TX", 7, 0), ("NO", 5, 2, 0, "g"), ("CO", 4, 3, "s"),
+    ("SC", 6, 3, 0), ("CO", 4, 0, "v"), ("TX", 7, 1), ("NO", 5, 2, 1, "g"), ("CO", 4, 1, "s"), ("SC", 6, 3, 1),
+    ("TQ", 7, 0), ("ST", 4, 1), ("CX", 7, 0, "s"), ("QX", 6), ("SC", 6, 2, 0), ("CX", 7, 1, "s"), ("RC", 5, 1),
+    ("RX", 6, 3, 0), ("TQ", 7, 1), ("CQ", 7, 0, "s"), ("NO", 5, 1, 0, "g"), ("SC", 6, 2, 1), ("RX", 6, 3, 1),
+    ("ST", 4, 0), ("TA", 5, 1), ("NO", 5, 1, 1, "g"), ("EX", 6, 3, 0), ("RX", 6, 2, 0), ("SC", 6, 1),
+    ("NO", 5, 0, 0, "g"), ("RX", 6, 2, 1), ("EX", 6, 3, 1), ("TA", 5, 2), ("NO", 5, 0, 1, "g"), ("CQ", 7, 1, "v"),
+    ("SC", 6, 0), ("CA", 5, 1, "s"), ("TA", 5, 0), ("RX", 6, 1, 0), ("RX", 6, 1, 1), ("MV", 6, 0), ("EX", 6, 2, 0),
+    ("RX", 6, 0, 0), ("MV", 6, 1), ("RX", 6, 0, 1), ("EX", 6, 2, 1), ("CA", 5, 2, "v"), ("MV", 6, 2), ("MV", 6, 3),
+    ("CA", 5, 0, "s"), ("MV", 6, 4), ("MV", 6, 5), ("QV", 5, 0), ("CV", 6, 1, "s"), ("MV", 6, 6), ("QV", 5, 1),
+    ("MV", 6, 7), ("CV", 6, 3, "s"), ("QA", 5, 1), ("CV", 6, 5, "s"), ("QA", 5, 0), ("RC", 6, 0), ("EX", 6, 1, 0),
+    ("CV", 6, 0, "v"), ("FO", 5, 2), ("EX", 6, 1, 1), ("NO", 6, 3, 0, "g"), ("CV", 6, 2, "v"), ("FO", 5, 3),
+    ("EX", 6, 0, 0), ("EX", 6, 0, 1), ("CV", 6, 4, "v"), ("CV", 6, 7, "s"), ("FO", 5, 0), ("NO", 6, 3, 1, "g"),
+    ("FO", 5, 1), ("CO", 5, 2, "s"), ("CV", 6, 6, "v"), ("SC", 7, 3, 0), ("NO", 6, 2, 0, "g"), ("SC", 7, 3, 1),
+    ("CO", 5, 3, "s"), ("CO", 5, 0, "v"), ("SC", 7, 2, 0), ("NO", 6, 2, 1, "g"), ("CO", 5, 1, "s"), ("SC", 7, 2, 1),
+    ("ST", 5, 1), ("QX", 7), ("TA", 6, 1), ("RC", 6, 1), ("RX", 7, 3, 0), ("SC", 7, 1), ("NO", 6, 1, 0, "g"),
+    ("RX", 7, 3, 1), ("ST", 5, 0), ("TA", 6, 2), ("NO", 6, 1, 1, "g"), ("EX", 7, 3, 0), ("RX", 7, 2, 0), ("SC", 7, 0),
+    ("NO", 6, 0, 0, "g"), ("RX", 7, 2, 1), ("EX", 7, 3, 1), ("NO", 6, 0, 1, "g"), ("QV", 6, 0), ("EX", 7, 2, 0),
+    ("TA", 6, 0), ("CA", 6, 2, "v"), ("EX", 7, 2, 1), ("MV", 7, 0), ("CA", 6, 1, "s"), ("MV", 7, 1), ("RC", 7, 0),
+    ("RX", 7, 0, 1), ("MV", 7, 2), ("QV", 6, 1), ("CA", 6, 0, "s"), ("MV", 7, 3), ("MV", 7, 4), ("RX", 7, 1, 1),
+    ("NO", 7, 3, 0, "g"), ("MV", 7, 5), ("RX", 7, 1, 0), ("CV", 7, 3, "s"), ("QA", 6, 1), ("MV", 7, 6), ("MV", 7, 7),
+    ("EX", 7, 0, 1), ("RX", 7, 0, 0), ("NO", 7, 3, 1, "g"), ("EX", 7, 1, 1), ("CV", 7, 1, "v"), ("EX", 7, 1, 0),
+    ("FO", 6, 2), ("NO", 7, 2, 0, "g"), ("CV", 7, 0, "v"), ("EX", 7, 0, 0), ("CV", 7, 4, "s"), ("FO", 6, 3),
+    ("QA", 6, 0), ("CV", 7, 2, "s"), ("RC", 7, 1), ("NO", 7, 0, 1, "v"), ("CV", 7, 7, "v"), ("NO", 7, 2, 1, "g"),
+    ("CV", 7, 5, "s"), ("FO", 6, 0), ("CO", 6, 3, "v"), ("FO", 6, 1), ("NO", 7, 1, 0, "g"), ("CV", 7, 6, "s"),
+    ("TA", 7, 1), ("QV", 7, 0), ("CO", 6, 2, "s"), ("NO", 7, 1, 1, "v"), ("TA", 7, 2), ("QV", 7, 1), ("ST", 6, 1),
+    ("CA", 7, 1, "s"), ("NO", 7, 0, 0, "g"), ("CA", 7, 2, "v"), ("TA", 7, 0), ("CO", 6, 1, "s"), ("QA", 7, 1),
+    ("CA", 7, 0, "s"), ("CO", 6, 0, "v"), ("FO", 7, 2), ("ST", 6, 0), ("FO", 7, 3), ("QA", 7, 0), ("CO", 7, 2, "s"),
+    ("FO", 7, 0), ("CO", 7, 3, "v"), ("FO", 7, 1), ("ST4", 7, 2), ("CO", 7, 0, "s"), ("CO", 7, 1, "v"), ("ST4", 7, 3),
+    ("ST4", 7, 0), ("ST4", 7, 1),
 )
 
 

@@ -12,137 +12,33 @@ U8 = mybir.dt.uint8
 FP8X4 = mybir.dt.float8_e4m3fn_x4
 ALU = mybir.AluOpType
 ACT = mybir.ActivationFunctionType
-AX = mybir.AxisListType
 
 B, S, D, H, L = 8, 512, 512, 2, 128
 P = 128
+PACK = 4
 NT = S // P
 FLOPS = 2 * B * S * D * H * D + 2 * B * H * S * S * L + 2 * B * S * H * S * D
 SCALE = 1.0 / math.sqrt(L)
-BIG = float(2 ** 100)
-MANUAL = True
-AW = (256, 256, 512, 512)
-SEGS = (((0, 0), (1, 0)), ((2, 0), (3, 0)), ((2, 1), (3, 1)))
-
-ORDER = (
-    ("INIT",), ("LQ", 0), ("LK", 0), ("TQ", 0, 0), ("LM",), ("LX", 0), ("TQ", 0, 1), ("CQ", 0, 0, "v"), ("MB",),
-    ("CQ", 0, 1, "s"), ("LW", 0), ("SC", 0, 3, 0), ("SC", 0, 3, 1), ("LW", 1), ("SC", 0, 2, 0), ("SC", 0, 2, 1),
-    ("RX", 0, 3, 0), ("SC", 0, 1), ("RX", 0, 2, 0), ("SC", 0, 0), ("TX", 0, 0), ("LQ", 1), ("RX", 0, 2, 1),
-    ("EX", 0, 3, 0), ("TX", 0, 1), ("RX", 0, 3, 1), ("TW", 0), ("LK", 1), ("CX", 0, 0, "s"), ("TW", 1),
-    ("RX", 0, 1, 0), ("TW", 2), ("CX", 0, 1, "s"), ("LX", 1), ("RX", 0, 1, 1), ("TW", 3), ("RX", 0, 0, 0),
-    ("CW", 0, "s"), ("TQ", 1, 0), ("RX", 0, 0, 1), ("CW", 2, "v"), ("CW", 1, "s"), ("TQ", 1, 1), ("QX", 0), ("LX", 2),
-    ("EX", 0, 3, 1), ("TX", 1, 0), ("CW", 3, "v"), ("EX", 0, 2, 0), ("TX", 1, 1), ("QW", 0), ("EX", 0, 2, 1),
-    ("LQ", 2), ("QW", 1), ("EX", 0, 1, 0), ("EX", 0, 1, 1), ("LK", 2), ("CQ", 1, 0, "v"), ("EX", 0, 0, 0),
-    ("EX", 0, 0, 1), ("MV", 0, 0), ("CQ", 1, 1, "v"), ("CX", 1, 1, "s"), ("LX", 3), ("MV", 0, 1), ("RC", 0, 0),
-    ("CX", 1, 0, "v"), ("MV", 0, 2), ("MV", 0, 3), ("NO", 0, 2, 1, "g"), ("MV", 0, 4), ("CV", 0, 1, "s"), ("LQ", 3),
-    ("MV", 0, 5), ("RC", 0, 1), ("CV", 0, 0, "v"), ("NO", 0, 2, 0, "g"), ("CV", 0, 2, "s"), ("MV", 0, 6),
-    ("MV", 0, 7), ("LK", 3), ("CV", 0, 4, "s"), ("QX", 1), ("TX", 2, 0), ("CV", 0, 6, "s"), ("SC", 1, 3, 0),
-    ("LX", 4), ("CV", 0, 3, "v"), ("NO", 0, 3, 0, "g"), ("TX", 2, 1), ("CV", 0, 7, "s"), ("CV", 0, 5, "v"),
-    ("SC", 1, 3, 1), ("NO", 0, 3, 1, "g"), ("TQ", 2, 0), ("CX", 2, 0, "s"), ("RX", 1, 3, 0), ("LQ", 4),
-    ("SC", 1, 2, 0), ("CX", 2, 1, "s"), ("NO", 0, 1, 0, "g"), ("TQ", 2, 1), ("RX", 1, 3, 1), ("NO", 0, 1, 1, "g"),
-    ("CQ", 2, 0, "s"), ("LK", 4), ("SC", 1, 2, 1), ("RX", 1, 2, 0), ("TA", 0, 1), ("NO", 0, 0, 0, "g"),
-    ("EX", 1, 3, 0), ("LX", 5), ("NO", 0, 0, 1, "g"), ("SC", 1, 1), ("RX", 1, 2, 1), ("EX", 1, 3, 1), ("TA", 0, 2),
-    ("CQ", 2, 1, "v"), ("CA", 0, 1, "s"), ("SC", 1, 0), ("RX", 1, 1, 0), ("TA", 0, 0), ("LQ", 5), ("RX", 1, 1, 1),
-    ("MV", 1, 0), ("RX", 1, 0, 0), ("EX", 1, 2, 0), ("LK", 5), ("RX", 1, 0, 1), ("MV", 1, 1), ("CA", 0, 2, "v"),
-    ("EX", 1, 2, 1), ("MV", 1, 2), ("LX", 6), ("MV", 1, 3), ("CA", 0, 0, "s"), ("MV", 1, 4), ("MV", 1, 5),
-    ("QV", 0, 0), ("MV", 1, 6), ("CV", 1, 1, "s"), ("QV", 0, 1), ("LQ", 6), ("MV", 1, 7), ("CV", 1, 3, "s"),
-    ("QA", 0, 1), ("LK", 6), ("CV", 1, 5, "s"), ("QA", 0, 0), ("RC", 1, 0), ("CV", 1, 0, "v"), ("EX", 1, 1, 0),
-    ("LX", 7), ("FO", 0, 2), ("EX", 1, 1, 1), ("NO", 1, 3, 0, "g"), ("CV", 1, 2, "v"), ("FO", 0, 3), ("EX", 1, 0, 0),
-    ("EX", 1, 0, 1), ("CV", 1, 4, "v"), ("CV", 1, 7, "s"), ("FO", 0, 0), ("NO", 1, 3, 1, "g"), ("FO", 0, 1),
-    ("LQ", 7), ("CV", 1, 6, "v"), ("CO", 0, 2, "s"), ("TX", 3, 0), ("NO", 1, 2, 0, "g"), ("SC", 2, 3, 0),
-    ("CO", 0, 0, "v"), ("LK", 7), ("CO", 0, 3, "s"), ("TX", 3, 1), ("NO", 1, 2, 1, "g"), ("CO", 0, 1, "s"),
-    ("SC", 2, 3, 1), ("TQ", 3, 0), ("QX", 2), ("ST", 0, 1), ("CX", 3, 0, "s"), ("SC", 2, 2, 0), ("RC", 1, 1),
-    ("CX", 3, 1, "s"), ("RX", 2, 3, 0), ("TQ", 3, 1), ("NO", 1, 1, 0, "g"), ("CQ", 3, 0, "s"), ("SC", 2, 2, 1),
-    ("RX", 2, 3, 1), ("ST", 0, 0), ("TA", 1, 1), ("NO", 1, 1, 1, "g"), ("EX", 2, 3, 0), ("RX", 2, 2, 0), ("SC", 2, 1),
-    ("NO", 1, 0, 0, "g"), ("RX", 2, 2, 1), ("EX", 2, 3, 1), ("TA", 1, 2), ("NO", 1, 0, 1, "g"), ("CQ", 3, 1, "v"),
-    ("SC", 2, 0), ("CA", 1, 1, "s"), ("TA", 1, 0), ("RX", 2, 1, 0), ("RX", 2, 1, 1), ("MV", 2, 0), ("EX", 2, 2, 0),
-    ("RX", 2, 0, 0), ("MV", 2, 1), ("RX", 2, 0, 1), ("EX", 2, 2, 1), ("CA", 1, 2, "v"), ("MV", 2, 2), ("MV", 2, 3),
-    ("CA", 1, 0, "s"), ("MV", 2, 4), ("MV", 2, 5), ("QV", 1, 0), ("CV", 2, 1, "s"), ("MV", 2, 6), ("QV", 1, 1),
-    ("MV", 2, 7), ("CV", 2, 3, "s"), ("QA", 1, 1), ("CV", 2, 5, "s"), ("QA", 1, 0), ("RC", 2, 0), ("EX", 2, 1, 0),
-    ("CV", 2, 0, "v"), ("FO", 1, 2), ("EX", 2, 1, 1), ("NO", 2, 3, 0, "g"), ("CV", 2, 2, "v"), ("FO", 1, 3),
-    ("EX", 2, 0, 0), ("EX", 2, 0, 1), ("CV", 2, 4, "v"), ("CV", 2, 7, "s"), ("FO", 1, 0), ("NO", 2, 3, 1, "g"),
-    ("FO", 1, 1), ("CO", 1, 2, "s"), ("CV", 2, 6, "v"), ("TX", 4, 0), ("NO", 2, 2, 0, "g"), ("CO", 1, 3, "s"),
-    ("SC", 3, 3, 0), ("CO", 1, 0, "v"), ("TX", 4, 1), ("NO", 2, 2, 1, "g"), ("CO", 1, 1, "s"), ("SC", 3, 3, 1),
-    ("TQ", 4, 0), ("ST", 1, 1), ("CX", 4, 0, "s"), ("QX", 3), ("SC", 3, 2, 0), ("CX", 4, 1, "s"), ("RC", 2, 1),
-    ("RX", 3, 3, 0), ("TQ", 4, 1), ("CQ", 4, 0, "s"), ("NO", 2, 1, 0, "g"), ("SC", 3, 2, 1), ("RX", 3, 3, 1),
-    ("ST", 1, 0), ("TA", 2, 1), ("NO", 2, 1, 1, "g"), ("EX", 3, 3, 0), ("RX", 3, 2, 0), ("SC", 3, 1),
-    ("NO", 2, 0, 0, "g"), ("RX", 3, 2, 1), ("EX", 3, 3, 1), ("TA", 2, 2), ("NO", 2, 0, 1, "g"), ("CQ", 4, 1, "v"),
-    ("SC", 3, 0), ("CA", 2, 1, "s"), ("TA", 2, 0), ("RX", 3, 1, 0), ("RX", 3, 1, 1), ("MV", 3, 0), ("EX", 3, 2, 0),
-    ("RX", 3, 0, 0), ("MV", 3, 1), ("RX", 3, 0, 1), ("EX", 3, 2, 1), ("CA", 2, 2, "v"), ("MV", 3, 2), ("MV", 3, 3),
-    ("CA", 2, 0, "s"), ("MV", 3, 4), ("MV", 3, 5), ("QV", 2, 0), ("CV", 3, 1, "s"), ("MV", 3, 6), ("QV", 2, 1),
-    ("MV", 3, 7), ("CV", 3, 3, "s"), ("QA", 2, 1), ("CV", 3, 5, "s"), ("QA", 2, 0), ("RC", 3, 0), ("EX", 3, 1, 0),
-    ("CV", 3, 0, "v"), ("FO", 2, 2), ("EX", 3, 1, 1), ("NO", 3, 3, 0, "g"), ("CV", 3, 2, "v"), ("FO", 2, 3),
-    ("EX", 3, 0, 0), ("EX", 3, 0, 1), ("CV", 3, 4, "v"), ("CV", 3, 7, "s"), ("FO", 2, 0), ("NO", 3, 3, 1, "g"),
-    ("FO", 2, 1), ("CO", 2, 2, "s"), ("CV", 3, 6, "v"), ("TX", 5, 0), ("NO", 3, 2, 0, "g"), ("CO", 2, 3, "s"),
-    ("SC", 4, 3, 0), ("CO", 2, 0, "v"), ("TX", 5, 1), ("NO", 3, 2, 1, "g"), ("CO", 2, 1, "s"), ("SC", 4, 3, 1),
-    ("TQ", 5, 0), ("ST", 2, 1), ("CX", 5, 0, "s"), ("QX", 4), ("SC", 4, 2, 0), ("CX", 5, 1, "s"), ("RC", 3, 1),
-    ("RX", 4, 3, 0), ("TQ", 5, 1), ("CQ", 5, 0, "s"), ("NO", 3, 1, 0, "g"), ("SC", 4, 2, 1), ("RX", 4, 3, 1),
-    ("ST", 2, 0), ("TA", 3, 1), ("NO", 3, 1, 1, "g"), ("EX", 4, 3, 0), ("RX", 4, 2, 0), ("SC", 4, 1),
-    ("NO", 3, 0, 0, "g"), ("RX", 4, 2, 1), ("EX", 4, 3, 1), ("TA", 3, 2), ("NO", 3, 0, 1, "g"), ("CQ", 5, 1, "v"),
-    ("SC", 4, 0), ("CA", 3, 1, "s"), ("TA", 3, 0), ("RX", 4, 1, 0), ("RX", 4, 1, 1), ("MV", 4, 0), ("EX", 4, 2, 0),
-    ("RX", 4, 0, 0), ("MV", 4, 1), ("RX", 4, 0, 1), ("EX", 4, 2, 1), ("CA", 3, 2, "v"), ("MV", 4, 2), ("MV", 4, 3),
-    ("CA", 3, 0, "s"), ("MV", 4, 4), ("MV", 4, 5), ("QV", 3, 0), ("CV", 4, 1, "s"), ("MV", 4, 6), ("QV", 3, 1),
-    ("MV", 4, 7), ("CV", 4, 3, "s"), ("QA", 3, 1), ("CV", 4, 5, "s"), ("QA", 3, 0), ("RC", 4, 0), ("EX", 4, 1, 0),
-    ("CV", 4, 0, "v"), ("FO", 3, 2), ("EX", 4, 1, 1), ("NO", 4, 3, 0, "g"), ("CV", 4, 2, "v"), ("FO", 3, 3),
-    ("EX", 4, 0, 0), ("EX", 4, 0, 1), ("CV", 4, 4, "v"), ("CV", 4, 7, "s"), ("FO", 3, 0), ("NO", 4, 3, 1, "g"),
-    ("FO", 3, 1), ("CO", 3, 2, "s"), ("CV", 4, 6, "v"), ("TX", 6, 0), ("NO", 4, 2, 0, "g"), ("CO", 3, 3, "s"),
-    ("SC", 5, 3, 0), ("CO", 3, 0, "v"), ("TX", 6, 1), ("NO", 4, 2, 1, "g"), ("CO", 3, 1, "s"), ("SC", 5, 3, 1),
-    ("TQ", 6, 0), ("ST", 3, 1), ("CX", 6, 0, "s"), ("QX", 5), ("SC", 5, 2, 0), ("CX", 6, 1, "s"), ("RC", 4, 1),
-    ("RX", 5, 3, 0), ("TQ", 6, 1), ("CQ", 6, 0, "s"), ("NO", 4, 1, 0, "g"), ("SC", 5, 2, 1), ("RX", 5, 3, 1),
-    ("ST", 3, 0), ("TA", 4, 1), ("NO", 4, 1, 1, "g"), ("EX", 5, 3, 0), ("RX", 5, 2, 0), ("SC", 5, 1),
-    ("NO", 4, 0, 0, "g"), ("RX", 5, 2, 1), ("EX", 5, 3, 1), ("TA", 4, 2), ("NO", 4, 0, 1, "g"), ("CQ", 6, 1, "v"),
-    ("SC", 5, 0), ("CA", 4, 1, "s"), ("TA", 4, 0), ("RX", 5, 1, 0), ("RX", 5, 1, 1), ("MV", 5, 0), ("EX", 5, 2, 0),
-    ("RX", 5, 0, 0), ("MV", 5, 1), ("RX", 5, 0, 1), ("EX", 5, 2, 1), ("CA", 4, 2, "v"), ("MV", 5, 2), ("MV", 5, 3),
-    ("CA", 4, 0, "s"), ("MV", 5, 4), ("MV", 5, 5), ("QV", 4, 0), ("CV", 5, 1, "s"), ("MV", 5, 6), ("QV", 4, 1),
-    ("MV", 5, 7), ("CV", 5, 3, "s"), ("QA", 4, 1), ("CV", 5, 5, "s"), ("QA", 4, 0), ("RC", 5, 0), ("EX", 5, 1, 0),
-    ("CV", 5, 0, "v"), ("FO", 4, 2), ("EX", 5, 1, 1), ("NO", 5, 3, 0, "g"), ("CV", 5, 2, "v"), ("FO", 4, 3),
-    ("EX", 5, 0, 0), ("EX", 5, 0, 1), ("CV", 5, 4, "v"), ("CV", 5, 7, "s"), ("FO", 4, 0), ("NO", 5, 3, 1, "g"),
-    ("FO", 4, 1), ("CO", 4, 2, "s"), ("CV", 5, 6, "v"), ("TX", 7, 0), ("NO", 5, 2, 0, "g"), ("CO", 4, 3, "s"),
-    ("SC", 6, 3, 0), ("CO", 4, 0, "v"), ("TX", 7, 1), ("NO", 5, 2, 1, "g"), ("CO", 4, 1, "s"), ("SC", 6, 3, 1),
-    ("TQ", 7, 0), ("ST", 4, 1), ("CX", 7, 0, "s"), ("QX", 6), ("SC", 6, 2, 0), ("CX", 7, 1, "s"), ("RC", 5, 1),
-    ("RX", 6, 3, 0), ("TQ", 7, 1), ("CQ", 7, 0, "s"), ("NO", 5, 1, 0, "g"), ("SC", 6, 2, 1), ("RX", 6, 3, 1),
-    ("ST", 4, 0), ("TA", 5, 1), ("NO", 5, 1, 1, "g"), ("EX", 6, 3, 0), ("RX", 6, 2, 0), ("SC", 6, 1),
-    ("NO", 5, 0, 0, "g"), ("RX", 6, 2, 1), ("EX", 6, 3, 1), ("TA", 5, 2), ("NO", 5, 0, 1, "g"), ("CQ", 7, 1, "v"),
-    ("SC", 6, 0), ("CA", 5, 1, "s"), ("TA", 5, 0), ("RX", 6, 1, 0), ("RX", 6, 1, 1), ("MV", 6, 0), ("EX", 6, 2, 0),
-    ("RX", 6, 0, 0), ("MV", 6, 1), ("RX", 6, 0, 1), ("EX", 6, 2, 1), ("CA", 5, 2, "v"), ("MV", 6, 2), ("MV", 6, 3),
-    ("CA", 5, 0, "s"), ("MV", 6, 4), ("MV", 6, 5), ("QV", 5, 0), ("CV", 6, 1, "s"), ("MV", 6, 6), ("QV", 5, 1),
-    ("MV", 6, 7), ("CV", 6, 3, "s"), ("QA", 5, 1), ("CV", 6, 5, "s"), ("QA", 5, 0), ("RC", 6, 0), ("EX", 6, 1, 0),
-    ("CV", 6, 0, "v"), ("FO", 5, 2), ("EX", 6, 1, 1), ("NO", 6, 3, 0, "g"), ("CV", 6, 2, "v"), ("FO", 5, 3),
-    ("EX", 6, 0, 0), ("EX", 6, 0, 1), ("CV", 6, 4, "v"), ("CV", 6, 7, "s"), ("FO", 5, 0), ("NO", 6, 3, 1, "g"),
-    ("FO", 5, 1), ("CO", 5, 2, "s"), ("CV", 6, 6, "v"), ("SC", 7, 3, 0), ("NO", 6, 2, 0, "g"), ("SC", 7, 3, 1),
-    ("CO", 5, 3, "s"), ("CO", 5, 0, "v"), ("SC", 7, 2, 0), ("NO", 6, 2, 1, "g"), ("CO", 5, 1, "s"), ("SC", 7, 2, 1),
-    ("ST", 5, 1), ("QX", 7), ("TA", 6, 1), ("RC", 6, 1), ("RX", 7, 3, 0), ("SC", 7, 1), ("NO", 6, 1, 0, "g"),
-    ("RX", 7, 3, 1), ("ST", 5, 0), ("TA", 6, 2), ("NO", 6, 1, 1, "g"), ("EX", 7, 3, 0), ("RX", 7, 2, 0), ("SC", 7, 0),
-    ("NO", 6, 0, 0, "g"), ("RX", 7, 2, 1), ("EX", 7, 3, 1), ("NO", 6, 0, 1, "g"), ("QV", 6, 0), ("EX", 7, 2, 0),
-    ("TA", 6, 0), ("CA", 6, 2, "v"), ("EX", 7, 2, 1), ("MV", 7, 0), ("CA", 6, 1, "s"), ("MV", 7, 1), ("RC", 7, 0),
-    ("RX", 7, 0, 1), ("MV", 7, 2), ("QV", 6, 1), ("CA", 6, 0, "s"), ("MV", 7, 3), ("MV", 7, 4), ("RX", 7, 1, 1),
-    ("NO", 7, 3, 0, "g"), ("MV", 7, 5), ("RX", 7, 1, 0), ("CV", 7, 3, "s"), ("QA", 6, 1), ("MV", 7, 6), ("MV", 7, 7),
-    ("EX", 7, 0, 1), ("RX", 7, 0, 0), ("NO", 7, 3, 1, "g"), ("EX", 7, 1, 1), ("CV", 7, 1, "v"), ("EX", 7, 1, 0),
-    ("FO", 6, 2), ("NO", 7, 2, 0, "g"), ("CV", 7, 0, "v"), ("EX", 7, 0, 0), ("CV", 7, 4, "s"), ("FO", 6, 3),
-    ("QA", 6, 0), ("CV", 7, 2, "s"), ("RC", 7, 1), ("NO", 7, 0, 1, "v"), ("CV", 7, 7, "v"), ("NO", 7, 2, 1, "g"),
-    ("CV", 7, 5, "s"), ("FO", 6, 0), ("CO", 6, 3, "v"), ("FO", 6, 1), ("NO", 7, 1, 0, "g"), ("CV", 7, 6, "s"),
-    ("TA", 7, 1), ("QV", 7, 0), ("CO", 6, 2, "s"), ("NO", 7, 1, 1, "v"), ("TA", 7, 2), ("QV", 7, 1), ("ST", 6, 1),
-    ("CA", 7, 1, "s"), ("NO", 7, 0, 0, "g"), ("CA", 7, 2, "v"), ("TA", 7, 0), ("CO", 6, 1, "s"), ("QA", 7, 1),
-    ("CA", 7, 0, "s"), ("CO", 6, 0, "v"), ("FO", 7, 2), ("ST", 6, 0), ("FO", 7, 3), ("QA", 7, 0), ("CO", 7, 2, "s"),
-    ("FO", 7, 0), ("CO", 7, 3, "v"), ("FO", 7, 1), ("ST4", 7, 2), ("CO", 7, 0, "s"), ("CO", 7, 1, "v"), ("ST4", 7, 3),
-    ("ST4", 7, 0), ("ST4", 7, 1),
-)
+MASKED = float(2 ** 100)
+KEYS_READ = (256, 256, 512, 512)
+ATTN_BANKS = (((0, 0), (1, 0)), ((2, 0), (3, 0)), ((2, 1), (3, 1)))
+VECTOR, SCALAR, GPSIMD = "vector", "scalar", "gpsimd"
+LARGE_FIRST = ((3, 0), (3, 1), (2, 0), (2, 1), (1, 0), (1, 1), (0, 0), (0, 1))
 
 
 def tile_multiheadattention_pa_t_kernel(tc, q, k, x, Wv, mask, out):
     nc = tc.nc
     with ExitStack() as ctx:
-        if MANUAL:
-            ctx.enter_context(tc.manual_schedule())
+        ctx.enter_context(tc.manual_schedule())
         const = ctx.enter_context(tc.tile_pool(name="const", bufs=1))
         loads = ctx.enter_context(tc.tile_pool(name="loads", bufs=1))
         work = ctx.enter_context(tc.tile_pool(name="work", bufs=2))
-        small = ctx.enter_context(tc.tile_pool(name="small", bufs=3))
+        stats = ctx.enter_context(tc.tile_pool(name="stats", bufs=3))
         psum = ctx.enter_context(tc.psum_pool(name="psum", bufs=8))
-        st = {}
+        live = {}
 
-        def copy(eng, dst, src):
-            if eng == "v":
+        def copy(engine, dst, src):
+            if engine == VECTOR:
                 nc.vector.tensor_copy(out=dst, in_=src)
             else:
                 nc.scalar.copy(out=dst, in_=src)
@@ -150,291 +46,472 @@ def tile_multiheadattention_pa_t_kernel(tc, q, k, x, Wv, mask, out):
         x_sb = [loads.tile([P, NT * D], BF16, name="x_sb%d" % b) for b in range(B)]
         q_sb = [loads.tile([P, NT * H * L], BF16, name="q_sb%d" % b) for b in range(B)]
         k_sb = [loads.tile([P, NT * H * L], BF16, name="k_sb%d" % b) for b in range(B)]
-        wv_sb = loads.tile([P, 8 * D], BF16, name="wv_sb")
-        mk_i = loads.tile([P, 2 * P], I32, name="mk_i")
-        mask32 = mask.bitcast(I32)
-        wv_view = Wv.rearrange("(r p) d -> p r d", p=P)
+        wv_sb = loads.tile([P, 2 * NT * D], BF16, name="wv_sb")
+        mask_sb = loads.tile([P, 2 * P], I32, name="mask_sb")
 
-        def LX(b):
+        def load_rows(dst, rows):
+            nc.sync.dma_start(out=dst[:].rearrange("p (a c) -> p a c", a=NT), in_=rows.rearrange("(a p) c -> p a c", p=P))
+
+        def load_x(b):
+            load_rows(x_sb[b], x[b])
+
+        def load_qk(b):
+            load_rows(q_sb[b], q[b].rearrange("s h l -> s (h l)"))
+            load_rows(k_sb[b], k[b].rearrange("s h l -> s (h l)"))
+
+        def load_wv(h):
             nc.sync.dma_start(
-                out=x_sb[b][:].rearrange("p (a d) -> p a d", a=NT), in_=x[b].rearrange("(a p) d -> p a d", p=P)
+                out=wv_sb[:, h * NT * D : (h + 1) * NT * D].rearrange("p (a c) -> p a c", a=NT),
+                in_=Wv[h * D : (h + 1) * D, :].rearrange("(a p) c -> p a c", p=P),
             )
 
-        def LQ(b):
-            nc.sync.dma_start(
-                out=q_sb[b][:].rearrange("p (a c) -> p a c", a=NT), in_=q[b].rearrange("(a p) h l -> p a (h l)", p=P)
-            )
+        identity_f32 = const.tile([P, P], F32, name="identity_f32")
+        identity_bf16 = const.tile([P, P], BF16, name="identity_bf16")
+        mask_f32 = const.tile([P, P], F32, name="mask_f32")
+        mask_bias = const.tile([P, P], BF16, name="mask_bias")
+        attn_sb = [
+            [const.tile([P, H * KEYS_READ[it]], BF16, name="attn_sb%d_%d" % (parity, it)) for it in range(NT)]
+            for parity in range(2)
+        ]
+        wv_grouped = const.tile([P, 2 * NT * D], BF16, name="wv_grouped", align_bytes=64)
+        wv_words = const.tile([P, H * D], U32, name="wv_words", align_bytes=64)
+        wv_scales = const.tile([P, H * D], U8, name="wv_scales", align_bytes=64)
 
-        def LK(b):
-            nc.sync.dma_start(
-                out=k_sb[b][:].rearrange("p (a c) -> p a c", a=NT), in_=k[b].rearrange("(a p) h l -> p a (h l)", p=P)
-            )
-
-        def LW(half):
-            nc.sync.dma_start(
-                out=wv_sb[:, half * 4 * D : (half + 1) * 4 * D].rearrange("p (r d) -> p r d", r=4),
-                in_=wv_view[:, half * 4 : (half + 1) * 4, :],
-            )
-
-        def LM():
-            nc.sync.dma_start(out=mk_i[:], in_=mask32[0, 0:P, 0 : 2 * P])
-
-        id_f = const.tile([P, P], F32, name="id_f")
-        id_bf = const.tile([P, P], BF16, name="id_bf")
-        mk_f = const.tile([P, P], F32, name="mk_f")
-        mb = const.tile([P, P], BF16, name="mb")
-        a_sb = [[const.tile([P, H * AW[it]], BF16, name="a_sb%d_%d" % (par, it)) for it in range(NT)] for par in range(2)]
-        wvg = const.tile([P, 8 * D], BF16, name="wvg", align_bytes=64)
-        wvw = const.tile([P, H * D], U32, name="wvw", align_bytes=64)
-        wvs = const.tile([P, H * D], U8, name="wvs", align_bytes=64)
-
-        def INIT():
-            make_identity(nc, id_bf[:])
-            make_identity(nc, id_f[:])
-            for par in range(2):
+        def make_constants():
+            make_identity(nc, identity_bf16[:])
+            make_identity(nc, identity_f32[:])
+            for parity in range(2):
                 for it in range(NT):
-                    n = (it + 1) * P
-                    if n < AW[it]:
-                        nc.gpsimd.memset(a_sb[par][it][:].rearrange("p (h j) -> p h j", h=H)[:, :, n:], 0.0)
+                    keys = (it + 1) * P
+                    if keys < KEYS_READ[it]:
+                        by_head = attn_sb[parity][it][:].rearrange("p (h key) -> p h key", h=H)
+                        nc.gpsimd.memset(by_head[:, :, keys:], 0.0)
 
-        def MB():
-            nc.vector.tensor_copy(out=mk_f[:], in_=mk_i[:].rearrange("p (j w) -> p j w", w=2)[:, :, 0])
-            nc.vector.tensor_scalar(out=mb[:], in0=mk_f[:], scalar1=1.0, scalar2=BIG, op0=ALU.subtract, op1=ALU.mult)
-
-        def TW(g):
-            src = wv_sb[:].bitcast(F32)
-            ps = psum.tile([P, 2, 2, P], F32, name="ps_wv", tag="bank")
-            for rr in range(2):
-                for u in range(2):
-                    o = (2 * g + rr) * 256 + u * P
-                    nc.tensor.transpose(ps[:, rr, u, :], src[:, o : o + P], id_f[:])
-            st[("TW", g)] = ps
-
-        def CW(g, eng):
-            dst = wvg[:].bitcast(F32).rearrange("w (r c u) -> w r c u", r=8, u=2)
-            copy(eng, dst[:, 2 * g : 2 * g + 2, :, :], st[("TW", g)][:].rearrange("w r u c -> w r c u"))
-
-        def QW(h):
-            nc.vector.quantize_mx(
-                out=wvw[:, h * D : (h + 1) * D].bitcast(FP8X4),
-                scales=wvs[:, h * D : (h + 1) * D],
-                in_=wvg[:, h * 4 * D : (h + 1) * 4 * D],
+        def make_mask_bias():
+            nc.vector.tensor_copy(out=mask_f32[:], in_=mask_sb[:].rearrange("p (key word) -> p key word", word=2)[:, :, 0])
+            nc.vector.tensor_scalar(
+                out=mask_bias[:], in0=mask_f32[:], scalar1=1.0, scalar2=MASKED, op0=ALU.subtract, op1=ALU.mult
             )
 
-        def TX(b, g):
-            src = x_sb[b][:].bitcast(F32)
-            ps = psum.tile([P, 2, 2, P], F32, name="ps_x", tag="bank")
-            for a2 in range(2):
-                for u in range(2):
-                    o = (2 * g + a2) * 256 + u * P
-                    nc.tensor.transpose(ps[:, a2, u, :], src[:, o : o + P], id_f[:])
-            st[("TX", b, g)] = ps
+        def transpose_words(src, pair):
+            words = src[:].bitcast(F32)
+            bank = psum.tile([P, 2, 2, P], F32, name="bank_words", tag="bank")
+            for a in range(2):
+                for m in range(2):
+                    first = (2 * pair + a) * (D // 2) + m * P
+                    nc.tensor.transpose(bank[:, a, m, :], words[:, first : first + P], identity_f32[:])
+            return bank
 
-        def CX(b, g, eng):
-            if ("xg", b) not in st:
-                xg_new = work.tile([P, NT * D], BF16, name="xg", align_bytes=64)
-                st[("xg", b)] = xg_new
-            dst = st[("xg", b)][:].bitcast(F32).rearrange("w (a p u) -> w a p u", a=NT, u=2)
-            copy(eng, dst[:, 2 * g : 2 * g + 2, :, :], st[("TX", b, g)][:].rearrange("w a u p -> w a p u"))
+        def copy_words(engine, grouped, row_tiles, pair, bank):
+            dst = grouped[:].bitcast(F32).rearrange("w (a r m) -> w a r m", a=row_tiles, m=2)
+            copy(engine, dst[:, 2 * pair : 2 * pair + 2, :, :], bank[:].rearrange("w a m r -> w a r m"))
 
-        def QX(b):
-            xw = work.tile([P, S], U32, name="xw", align_bytes=64)
-            xs = work.tile([P, S], U8, name="xs", align_bytes=64)
-            nc.vector.quantize_mx(out=xw[:].bitcast(FP8X4), scales=xs[:], in_=st[("xg", b)][:])
-            st[("xw", b)] = (xw, xs)
+        def transpose_wv(pair):
+            live[("wv bank", pair)] = transpose_words(wv_sb, pair)
 
-        def TQ(b, i):
-            src = (q_sb[b], k_sb[b])[i]
-            ps = psum.tile([P, H, NT, P], BF16, name="ps_qk", tag="bank")
+        def copy_wv(pair, engine):
+            copy_words(engine, wv_grouped, 2 * NT, pair, live[("wv bank", pair)])
+
+        def quantise_wv(h):
+            nc.vector.quantize_mx(
+                out=wv_words[:, h * D : (h + 1) * D].bitcast(FP8X4),
+                scales=wv_scales[:, h * D : (h + 1) * D],
+                in_=wv_grouped[:, h * PACK * D : (h + 1) * PACK * D],
+            )
+
+        def transpose_x(b, pair):
+            live[("x bank", b, pair)] = transpose_words(x_sb[b], pair)
+
+        def copy_x(b, pair, engine):
+            if pair == 0:
+                x_grouped = work.tile([P, NT * D], BF16, name="x_grouped", align_bytes=64)
+                live[("x grouped", b)] = x_grouped
+            copy_words(engine, live[("x grouped", b)], NT, pair, live[("x bank", b, pair)])
+
+        def quantise_x(b):
+            x_words = work.tile([P, S], U32, name="x_words", align_bytes=64)
+            x_scales = work.tile([P, S], U8, name="x_scales", align_bytes=64)
+            nc.vector.quantize_mx(out=x_words[:].bitcast(FP8X4), scales=x_scales[:], in_=live[("x grouped", b)][:])
+            live[("x", b)] = (x_words, x_scales)
+
+        def values(b, bank_no):
+            x_words, x_scales = live[("x", b)]
+            u, c = bank_no // NT, bank_no % NT
+            bank = psum.tile([P, PACK, P], F32, name="bank_v", tag="bank")
+            for h in range(H):
+                for tile_in_pass in range(2):
+                    rows = slice((2 * u + tile_in_pass) * P, (2 * u + tile_in_pass + 1) * P)
+                    cols = slice(h * D + c * P, h * D + (c + 1) * P)
+                    nc.tensor.matmul_mx(
+                        out=bank[:, 2 * h + tile_in_pass, :],
+                        lhsT=x_words[:, rows].bitcast(FP8X4),
+                        lhsT_scale=x_scales[:, rows],
+                        rhs=wv_words[:, cols].bitcast(FP8X4),
+                        rhs_scale=wv_scales[:, cols],
+                        start=True,
+                        stop=True,
+                    )
+            live[("v bank", b, bank_no)] = bank
+
+        def copy_values(b, bank_no, engine):
+            if bank_no == 0:
+                v_grouped = work.tile([P, 2 * PACK * D], BF16, name="v_grouped", align_bytes=64)
+                live[("v grouped", b)] = v_grouped
+            dst = live[("v grouped", b)][:, bank_no * PACK * P : (bank_no + 1) * PACK * P]
+            copy(engine, dst.rearrange("p (d t) -> p d t", t=PACK), live[("v bank", b, bank_no)][:].rearrange("p t d -> p d t"))
+
+        def quantise_values(b):
+            v_words = work.tile([P, 2 * D], U32, name="v_words", align_bytes=64)
+            v_scales = work.tile([P, 2 * D], U8, name="v_scales", align_bytes=64)
+            nc.vector.quantize_mx(out=v_words[:].bitcast(FP8X4), scales=v_scales[:], in_=live[("v grouped", b)][:])
+            live[("v", b)] = (v_words, v_scales)
+
+        def transpose_qk(b, which):
+            src = (q_sb[b], k_sb[b])[which]
+            bank = psum.tile([P, H, NT, P], BF16, name="bank_qk", tag="bank")
             for h in range(H):
                 for a in range(NT):
-                    o = a * H * L + h * L
-                    nc.tensor.transpose(ps[:, h, a, :], src[:, o : o + L], id_bf[:])
-            st[("TQ", b, i)] = ps
+                    first = (a * H + h) * L
+                    nc.tensor.transpose(bank[:, h, a, :], src[:, first : first + L], identity_bf16[:])
+            live[("qk bank", b, which)] = bank
 
-        def CQ(b, i, eng):
-            dst = work.tile([P, H * S], BF16, name="qkT%d" % i)
-            copy(eng, dst[:], st[("TQ", b, i)][:].rearrange("l h a p -> l (h a p)"))
-            st[("qk", b, i)] = dst
+        def copy_qk(b, which, engine):
+            transposed = work.tile([P, H * S], BF16, name="qk_transposed%d" % which)
+            copy(engine, transposed[:], live[("qk bank", b, which)][:].rearrange("l h a s -> l (h a s)"))
+            live[("qk", b, which)] = transposed
 
-        def sc_head(b, it, h, view):
-            qT = st[("qk", b, 0)]
-            kT = st[("qk", b, 1)]
-            n = (it + 1) * P
-            lhsT = qT[:, h * S + it * P : h * S + (it + 1) * P]
+        def scores_of_head(b, it, h, dst):
+            q_t, k_t = live[("qk", b, 0)], live[("qk", b, 1)]
+            queries = q_t[:, h * S + it * P : h * S + (it + 1) * P]
+            diagonal = slice(it * P, (it + 1) * P)
             if it > 0:
-                nc.tensor.matmul(out=view[:, 0 : it * P], lhsT=lhsT, rhs=kT[:, h * S : h * S + it * P], start=True, stop=True)
-            nc.tensor.matmul(out=view[:, it * P : n], lhsT=lhsT, rhs=kT[:, h * S + it * P : h * S + n], start=True, stop=False)
-            nc.tensor.matmul(out=view[:, it * P : n], lhsT=id_bf[:], rhs=mb[:], start=False, stop=True)
+                nc.tensor.matmul(out=dst[:, 0 : it * P], lhsT=queries, rhs=k_t[:, h * S : h * S + it * P], start=True, stop=True)
+            nc.tensor.matmul(
+                out=dst[:, diagonal], lhsT=queries, rhs=k_t[:, h * S + it * P : h * S + (it + 1) * P], start=True, stop=False
+            )
+            nc.tensor.matmul(out=dst[:, diagonal], lhsT=identity_bf16[:], rhs=mask_bias[:], start=False, stop=True)
 
-        def SC(b, it, h=0):
-            n = (it + 1) * P
-            if it < 2:
-                ps = psum.tile([P, H, n], F32, name="ps_s", tag="bank")
-                for hh in range(H):
-                    sc_head(b, it, hh, ps[:, hh, :])
-                    st[("S", b, it, hh)] = ps[:, hh, :]
-                st[("S2", b, it)] = ps
+        def scores(b, it, h=None):
+            keys = (it + 1) * P
+            if h is None:
+                bank = psum.tile([P, H, keys], F32, name="bank_scores2", tag="bank")
+                for head in range(H):
+                    scores_of_head(b, it, head, bank[:, head, :])
+                    live[("scores", b, it, head)] = bank[:, head, :]
             else:
-                ps1 = psum.tile([P, n], F32, name="ps_s1", tag="bank")
-                sc_head(b, it, h, ps1[:])
-                st[("S", b, it, h)] = ps1[:]
+                bank1 = psum.tile([P, keys], F32, name="bank_scores1", tag="bank")
+                scores_of_head(b, it, h, bank1[:])
+                live[("scores", b, it, h)] = bank1[:]
 
-        def RX(b, it, h):
-            n = (it + 1) * P
-            if ("nm", b) not in st:
-                nm_new = small.tile([P, 2 * NT], F32, name="nm")
-                sm_new = small.tile([P, 2 * NT], F32, name="sm")
-                rc_new = small.tile([P, 2 * NT], F32, name="rc")
-                st[("nm", b)] = (nm_new, sm_new, rc_new)
-            if ("e", b, it) not in st:
-                e_new = work.tile([P, H * n], F32, name="e_sb%d" % it)
-                st[("e", b, it)] = e_new
-            c = 2 * it + h
+        def scale_and_minimum(b, it, h):
+            keys = (it + 1) * P
+            if ("stats", b) not in live:
+                bias = stats.tile([P, H * NT], F32, name="bias")
+                sums = stats.tile([P, H * NT], F32, name="sums")
+                inverse = stats.tile([P, H * NT], F32, name="inverse")
+                live[("stats", b)] = (bias, sums, inverse)
+            if h == 0:
+                e_sb = work.tile([P, H * keys], F32, name="e_sb%d" % it)
+                live[("e", b, it)] = e_sb
+            col = H * it + h
             nc.vector.tensor_scalar(
-                out=st[("e", b, it)][:, h * n : (h + 1) * n],
-                in0=st[("S", b, it, h)],
+                out=live[("e", b, it)][:, h * keys : (h + 1) * keys],
+                in0=live[("scores", b, it, h)],
                 scalar1=-SCALE,
                 scalar2=None,
                 op0=ALU.mult,
                 op1=ALU.min,
-                accum_out=st[("nm", b)][0][:, c : c + 1],
+                accum_out=live[("stats", b)][0][:, col : col + 1],
             )
 
-        def EX(b, it, h):
-            n = (it + 1) * P
-            c = 2 * it + h
-            nm, sm, rc = st[("nm", b)]
-            e_sl = st[("e", b, it)][:, h * n : (h + 1) * n]
+        def exponential(b, it, h):
+            keys = (it + 1) * P
+            col = H * it + h
+            bias, sums = live[("stats", b)][:2]
+            e_part = live[("e", b, it)][:, h * keys : (h + 1) * keys]
             nc.scalar.activation(
-                out=e_sl, in_=e_sl, func=ACT.Exp, bias=nm[:, c : c + 1], scale=-1.0, accum_out=sm[:, c : c + 1]
+                out=e_part, in_=e_part, func=ACT.Exp, bias=bias[:, col : col + 1], scale=-1.0, accum_out=sums[:, col : col + 1]
             )
 
-        def RC(b, half):
-            nm, sm, rc = st[("nm", b)]
-            lo = 4 - 4 * half
-            nc.vector.reciprocal(out=rc[:, lo : lo + 4], in_=sm[:, lo : lo + 4])
+        def reciprocals(b, first_tile):
+            sums, inverse = live[("stats", b)][1:]
+            pair_cols = slice(H * first_tile, H * (first_tile + 2))
+            nc.vector.reciprocal(out=inverse[:, pair_cols], in_=sums[:, pair_cols])
 
-        def NO(b, it, h, eng):
-            n = (it + 1) * P
-            c = 2 * it + h
-            dst = a_sb[b % 2][it][:, h * AW[it] : h * AW[it] + n]
-            src = st[("e", b, it)][:, h * n : (h + 1) * n]
-            rcol = st[("nm", b)][2][:, c : c + 1]
-            if eng == "g":
-                nc.gpsimd.tensor_scalar(out=dst, in0=src, scalar1=rcol, scalar2=0.0, op0=ALU.mult, op1=ALU.add)
+        def normalise(b, it, h, engine):
+            keys = (it + 1) * P
+            col = H * it + h
+            dst = attn_sb[b % 2][it][:, h * KEYS_READ[it] : h * KEYS_READ[it] + keys]
+            src = live[("e", b, it)][:, h * keys : (h + 1) * keys]
+            factor = live[("stats", b)][2][:, col : col + 1]
+            if engine == GPSIMD:
+                nc.gpsimd.tensor_scalar(out=dst, in0=src, scalar1=factor, scalar2=0.0, op0=ALU.mult, op1=ALU.add)
             else:
-                nc.vector.tensor_scalar(out=dst, in0=src, scalar1=rcol, scalar2=None, op0=ALU.mult)
+                nc.vector.tensor_scalar(out=dst, in0=src, scalar1=factor, scalar2=None, op0=ALU.mult)
 
-        def MV(b, j):
-            xw, xs = st[("xw", b)]
-            U = j // 4
-            c = j % 4
-            ps = psum.tile([P, 4, P], F32, name="ps_v", tag="bank")
-            for h in range(H):
-                for blk in range(2):
-                    a = 2 * U + blk
-                    col = h * D + c * P
-                    nc.tensor.matmul_mx(
-                        out=ps[:, 2 * h + blk, :],
-                        lhsT=xw[:, a * P : (a + 1) * P].bitcast(FP8X4),
-                        lhsT_scale=xs[:, a * P : (a + 1) * P],
-                        rhs=wvw[:, col : col + P].bitcast(FP8X4),
-                        rhs_scale=wvs[:, col : col + P],
-                        start=True,
-                        stop=True,
-                    )
-            st[("MV", b, j)] = ps
+        def normalise_large(b):
+            reciprocals(b, 2)
+            for it, h in LARGE_FIRST[:4]:
+                normalise(b, it, h, GPSIMD)
 
-        def CV(b, j, eng):
-            if ("vg", b) not in st:
-                vg_new = work.tile([P, 2 * 4 * D], BF16, name="vg", align_bytes=64)
-                st[("vg", b)] = vg_new
-            o = j * 4 * P
-            copy(
-                eng,
-                st[("vg", b)][:, o : o + 4 * P].rearrange("p (d t) -> p d t", t=4),
-                st[("MV", b, j)][:].rearrange("p t d -> p d t"),
-            )
+        def normalise_small(b):
+            reciprocals(b, 0)
+            for it, h in LARGE_FIRST[4:]:
+                normalise(b, it, h, GPSIMD)
 
-        def QV(b, U):
-            if ("vw", b) not in st:
-                vw_new = work.tile([P, 2 * D], U32, name="vw", align_bytes=64)
-                vs_new = work.tile([P, 2 * D], U8, name="vs", align_bytes=64)
-                st[("vw", b)] = (vw_new, vs_new)
-            vw, vs = st[("vw", b)]
-            nc.vector.quantize_mx(
-                out=vw[:, U * D : (U + 1) * D].bitcast(FP8X4),
-                scales=vs[:, U * D : (U + 1) * D],
-                in_=st[("vg", b)][:, U * 4 * D : (U + 1) * 4 * D],
-            )
-
-        def TA(b, g):
-            ps = psum.tile([P, 2, 4, P], BF16, name="ps_a", tag="bank")
-            for gi in range(2):
-                it, U = SEGS[g][gi]
-                at = a_sb[b % 2][it]
+        def transpose_attn(b, bank_no):
+            bank = psum.tile([P, 2, PACK, P], BF16, name="bank_attn", tag="bank")
+            for place in range(2):
+                it, u = ATTN_BANKS[bank_no][place]
                 for h in range(H):
-                    for blk in range(2):
-                        o = h * AW[it] + (2 * U + blk) * P
-                        nc.tensor.transpose(ps[:, gi, 2 * h + blk, :], at[:, o : o + P], id_bf[:])
-            st[("TA", b, g)] = ps
+                    for tile_in_pass in range(2):
+                        first = h * KEYS_READ[it] + (2 * u + tile_in_pass) * P
+                        nc.tensor.transpose(
+                            bank[:, place, 2 * h + tile_in_pass, :], attn_sb[b % 2][it][:, first : first + P], identity_bf16[:]
+                        )
+            live[("attn bank", b, bank_no)] = bank
 
-        def CA(b, g, eng):
-            if ("ag", b) not in st:
-                ag_new = work.tile([P, 6 * 4 * P], BF16, name="ag", align_bytes=64)
-                st[("ag", b)] = ag_new
+        def copy_attn(b, bank_no, engine):
+            if ("attn grouped", b) not in live:
+                attn_grouped = work.tile([P, 6 * PACK * P], BF16, name="attn_grouped", align_bytes=64)
+                live[("attn grouped", b)] = attn_grouped
+            dst = live[("attn grouped", b)][:, bank_no * 2 * PACK * P : (bank_no + 1) * 2 * PACK * P]
             copy(
-                eng,
-                st[("ag", b)][:, g * 1024 : (g + 1) * 1024].rearrange("p (g i t) -> p g i t", g=2, t=4),
-                st[("TA", b, g)][:].rearrange("p g t i -> p g i t"),
+                engine,
+                dst.rearrange("p (place i t) -> p place i t", place=2, t=PACK),
+                live[("attn bank", b, bank_no)][:].rearrange("p place t i -> p place i t"),
             )
 
-        def QA(b, part):
-            if ("aw", b) not in st:
-                aw_new = work.tile([P, 6 * P], U32, name="aw", align_bytes=64)
-                as_new = work.tile([P, 6 * P], U8, name="asc", align_bytes=64)
-                st[("aw", b)] = (aw_new, as_new)
-            aw, asc = st[("aw", b)]
-            lo, hi = ((0, 256), (256, 768))[part]
-            nc.vector.quantize_mx(out=aw[:, lo:hi].bitcast(FP8X4), scales=asc[:, lo:hi], in_=st[("ag", b)][:, 4 * lo : 4 * hi])
+        def quantise_attn(b, first_bank, last_bank):
+            if ("attn", b) not in live:
+                attn_words = work.tile([P, 6 * P], U32, name="attn_words", align_bytes=64)
+                attn_scales = work.tile([P, 6 * P], U8, name="attn_scales", align_bytes=64)
+                live[("attn", b)] = (attn_words, attn_scales)
+            attn_words, attn_scales = live[("attn", b)]
+            first, end = first_bank * 2 * P, (last_bank + 1) * 2 * P
+            nc.vector.quantize_mx(
+                out=attn_words[:, first:end].bitcast(FP8X4),
+                scales=attn_scales[:, first:end],
+                in_=live[("attn grouped", b)][:, PACK * first : PACK * end],
+            )
 
-        def FO(b, it):
-            aw, asc = st[("aw", b)]
-            vw, vs = st[("vw", b)]
-            po = psum.tile([P, D], F32, name="po", tag="bank")
-            passes = [(it, 0)] + ([(it + 2, 1)] if it >= 2 else [])
-            for i, (seg, U) in enumerate(passes):
+        def product(b, it):
+            attn_words, attn_scales = live[("attn", b)]
+            v_words, v_scales = live[("v", b)]
+            bank = psum.tile([P, D], F32, name="bank_out", tag="bank")
+            passes = 1 if it < 2 else 2
+            for u in range(passes):
+                segment = it if u == 0 else it + 2
+                rows = slice(segment * P, (segment + 1) * P)
                 nc.tensor.matmul_mx(
-                    out=po[:],
-                    lhsT=aw[:, seg * P : (seg + 1) * P].bitcast(FP8X4),
-                    lhsT_scale=asc[:, seg * P : (seg + 1) * P],
-                    rhs=vw[:, U * D : (U + 1) * D].bitcast(FP8X4),
-                    rhs_scale=vs[:, U * D : (U + 1) * D],
-                    start=(i == 0),
-                    stop=(i == len(passes) - 1),
+                    out=bank[:],
+                    lhsT=attn_words[:, rows].bitcast(FP8X4),
+                    lhsT_scale=attn_scales[:, rows],
+                    rhs=v_words[:, u * D : (u + 1) * D].bitcast(FP8X4),
+                    rhs_scale=v_scales[:, u * D : (u + 1) * D],
+                    start=(u == 0),
+                    stop=(u == passes - 1),
                 )
-            st[("FO", b, it)] = po
+            live[("out bank", b, it)] = bank
 
-        def CO(b, it, eng):
-            if ("o", b) not in st:
-                o_new = work.tile([P, NT * D], F32, name="o_sb")
-                st[("o", b)] = o_new
-            copy(eng, st[("o", b)][:, it * D : (it + 1) * D], st[("FO", b, it)][:])
+        def copy_out(b, it, engine):
+            if ("out", b) not in live:
+                out_sb = work.tile([P, NT * D], F32, name="out_sb")
+                live[("out", b)] = out_sb
+            copy(engine, live[("out", b)][:, it * D : (it + 1) * D], live[("out bank", b, it)][:])
 
-        def ST(b, pr):
+        def store(b, it, count):
             nc.sync.dma_start(
-                out=out[b, 2 * pr * P : (2 * pr + 2) * P, :].rearrange("(a p) d -> p a d", p=P),
-                in_=st[("o", b)][:, 2 * pr * D : (2 * pr + 2) * D].rearrange("p (a d) -> p a d", a=2),
+                out=out[b, it * P : (it + count) * P, :].rearrange("(a p) d -> p a d", p=P),
+                in_=live[("out", b)][:, it * D : (it + count) * D].rearrange("p (a d) -> p a d", a=count),
             )
 
-        def ST4(b, it):
-            nc.sync.dma_start(out=out[b, it * P : (it + 1) * P, :], in_=st[("o", b)][:, it * D : (it + 1) * D])
+        def phase_plain(j):
+            transpose_x(j + 2, 0)
+            copy_x(j + 2, 0, SCALAR)
+            scores(j + 1, 3, 0)
+            scale_and_minimum(j + 1, 3, 0)
+            transpose_x(j + 2, 1)
+            copy_x(j + 2, 1, SCALAR)
+            scores(j + 1, 3, 1)
+            scale_and_minimum(j + 1, 3, 1)
+            transpose_qk(j + 2, 0)
+            copy_qk(j + 2, 0, SCALAR)
+            scores(j + 1, 2, 0)
+            scale_and_minimum(j + 1, 2, 0)
+            exponential(j + 1, 3, 0)
+            exponential(j + 1, 3, 1)
+            transpose_qk(j + 2, 1)
+            scores(j + 1, 2, 1)
+            scale_and_minimum(j + 1, 2, 1)
+            copy_qk(j + 2, 1, VECTOR)
+            transpose_attn(j, 1)
+            copy_attn(j, 1, SCALAR)
+            scores(j + 1, 1)
+            scale_and_minimum(j + 1, 1, 0)
+            scale_and_minimum(j + 1, 1, 1)
+            exponential(j + 1, 2, 0)
+            exponential(j + 1, 2, 1)
+            transpose_attn(j, 2)
+            scores(j + 1, 0)
+            scale_and_minimum(j + 1, 0, 0)
+            scale_and_minimum(j + 1, 0, 1)
+            copy_attn(j, 2, VECTOR)
+            transpose_attn(j, 0)
+            copy_attn(j, 0, SCALAR)
 
-        steps = {
-            "LX": LX, "LQ": LQ, "LK": LK, "LW": LW, "LM": LM, "INIT": INIT, "MB": MB, "TW": TW, "CW": CW, "QW": QW,
-            "TX": TX, "CX": CX, "QX": QX, "TQ": TQ, "CQ": CQ, "SC": SC, "RX": RX, "EX": EX, "RC": RC,
-            "NO": NO, "MV": MV, "CV": CV, "QV": QV, "TA": TA, "CA": CA, "QA": QA, "FO": FO, "CO": CO, "ST": ST, "ST4": ST4,
-        }
-        for step in ORDER:
-            steps[step[0]](*step[1:])
+        def phase_mx(j):
+            for bank_no in range(2 * NT):
+                values(j + 1, bank_no)
+            quantise_values(j)
+            quantise_attn(j, 1, 2)
+            quantise_attn(j, 0, 0)
+            normalise_large(j + 1)
+            for it in (2, 3, 0, 1):
+                product(j, it)
+            for bank_no in range(7):
+                copy_values(j + 1, bank_no, (VECTOR, SCALAR)[bank_no % 2])
+            for it, h in LARGE_FIRST[4:]:
+                exponential(j + 1, it, h)
+            copy_values(j + 1, 7, SCALAR)
+            copy_out(j, 0, VECTOR)
+            copy_out(j, 2, SCALAR)
+            copy_out(j, 3, SCALAR)
+            store(j, 2, 2)
+            copy_out(j, 1, SCALAR)
+            store(j, 0, 2)
+            quantise_x(j + 2)
+            normalise_small(j + 1)
+
+        make_constants()
+        load_qk(0)
+        nc.sync.dma_start(out=mask_sb[:], in_=mask.bitcast(I32)[0, 0:P, 0 : 2 * P])
+        load_x(0)
+        load_wv(0)
+        load_wv(1)
+        load_qk(1)
+        load_x(1)
+        for b in range(2, B):
+            load_x(b)
+            load_qk(b)
+
+        transpose_qk(0, 0)
+        copy_qk(0, 0, VECTOR)
+        transpose_qk(0, 1)
+        copy_qk(0, 1, SCALAR)
+        make_mask_bias()
+        for it, h in LARGE_FIRST[:4]:
+            scores(0, it, h)
+        scores(0, 1)
+        scores(0, 0)
+        transpose_x(0, 0)
+        transpose_x(0, 1)
+        scale_and_minimum(0, 3, 0)
+        exponential(0, 3, 0)
+        copy_x(0, 0, SCALAR)
+        copy_x(0, 1, SCALAR)
+        for it, h in LARGE_FIRST[1:]:
+            scale_and_minimum(0, it, h)
+        for pair in range(4):
+            transpose_wv(pair)
+        copy_wv(0, SCALAR)
+        copy_wv(1, SCALAR)
+        for it, h in LARGE_FIRST[1:]:
+            exponential(0, it, h)
+        copy_wv(2, VECTOR)
+        quantise_x(0)
+        copy_wv(3, VECTOR)
+        quantise_wv(0)
+        quantise_wv(1)
+        transpose_qk(1, 0)
+        transpose_qk(1, 1)
+        transpose_x(1, 0)
+        transpose_x(1, 1)
+        for bank_no in range(2 * NT):
+            values(0, bank_no)
+        copy_qk(1, 0, VECTOR)
+        copy_qk(1, 1, VECTOR)
+        normalise_large(0)
+        copy_x(1, 0, VECTOR)
+        normalise_small(0)
+        copy_x(1, 1, SCALAR)
+        copy_values(0, 0, VECTOR)
+        copy_values(0, 1, SCALAR)
+        copy_values(0, 2, SCALAR)
+        quantise_x(1)
+        copy_values(0, 3, VECTOR)
+        copy_values(0, 4, SCALAR)
+        copy_values(0, 5, VECTOR)
+        copy_values(0, 6, SCALAR)
+        copy_values(0, 7, SCALAR)
+
+        for j in range(B - 2):
+            phase_plain(j)
+            phase_mx(j)
+
+        j, last = B - 2, B - 1
+        scores(last, 3, 0)
+        scale_and_minimum(last, 3, 0)
+        scores(last, 3, 1)
+        scale_and_minimum(last, 3, 1)
+        exponential(last, 3, 0)
+        scores(last, 2, 0)
+        scale_and_minimum(last, 2, 0)
+        exponential(last, 3, 1)
+        scores(last, 2, 1)
+        scale_and_minimum(last, 2, 1)
+        exponential(last, 2, 0)
+        exponential(last, 2, 1)
+        quantise_values(j)
+        transpose_attn(j, 1)
+        copy_attn(j, 1, SCALAR)
+        scores(last, 1)
+        transpose_attn(j, 2)
+        copy_attn(j, 2, VECTOR)
+        normalise_large(last)
+        scale_and_minimum(last, 1, 0)
+        scale_and_minimum(last, 1, 1)
+        scores(last, 0)
+        scale_and_minimum(last, 0, 0)
+        scale_and_minimum(last, 0, 1)
+        transpose_attn(j, 0)
+        copy_attn(j, 0, SCALAR)
+        for bank_no in range(2 * NT):
+            values(last, bank_no)
+        quantise_attn(j, 1, 2)
+        copy_values(last, 0, VECTOR)
+        copy_values(last, 1, VECTOR)
+        quantise_attn(j, 0, 0)
+        copy_values(last, 2, SCALAR)
+        for it, h in LARGE_FIRST[4:]:
+            exponential(last, it, h)
+        reciprocals(last, 0)
+        normalise(last, 1, 0, GPSIMD)
+        normalise(last, 1, 1, VECTOR)
+        normalise(last, 0, 0, GPSIMD)
+        normalise(last, 0, 1, VECTOR)
+        for it in (2, 3, 0, 1):
+            product(j, it)
+        for bank_no in range(3, 7):
+            copy_values(last, bank_no, SCALAR)
+        copy_values(last, 7, VECTOR)
+        transpose_attn(last, 1)
+        transpose_attn(last, 2)
+        transpose_attn(last, 0)
+        copy_out(j, 3, VECTOR)
+        copy_out(j, 2, SCALAR)
+        store(j, 2, 2)
+        quantise_values(last)
+        copy_attn(last, 1, SCALAR)
+        copy_attn(last, 2, VECTOR)
+        quantise_attn(last, 1, 2)
+        copy_out(j, 1, SCALAR)
+        copy_out(j, 0, VECTOR)
+        store(j, 0, 2)
+        copy_attn(last, 0, SCALAR)
+        quantise_attn(last, 0, 0)
+        for it in (2, 3, 0, 1):
+            product(last, it)
+        for it, engine in ((2, SCALAR), (3, VECTOR), (0, SCALAR), (1, VECTOR)):
+            copy_out(last, it, engine)
+            store(last, it, 1)

@@ -29,7 +29,6 @@ LARGE_FIRST = ((3, 0), (3, 1), (2, 0), (2, 1), (1, 0), (1, 1), (0, 0), (0, 1))
 def tile_multiheadattention_pa_t_kernel(tc, q, k, x, Wv, mask, out):
     nc = tc.nc
     with ExitStack() as ctx:
-        ctx.enter_context(tc.manual_schedule())
         const = ctx.enter_context(tc.tile_pool(name="const", bufs=1))
         loads = ctx.enter_context(tc.tile_pool(name="loads", bufs=1))
         work = ctx.enter_context(tc.tile_pool(name="work", bufs=2))

@@ -12,32 +12,98 @@ U8 = mybir.dt.uint8
 FP8X4 = mybir.dt.float8_e4m3fn_x4
 ALU = mybir.AluOpType
 ACT = mybir.ActivationFunctionType
+AX = mybir.AxisListType
 
 B, S, D, H, L = 8, 512, 512, 2, 128
 P = 128
-PACK = 4
 NT = S // P
 FLOPS = 2 * B * S * D * H * D + 2 * B * H * S * S * L + 2 * B * S * H * S * D
 SCALE = 1.0 / math.sqrt(L)
-MASKED = float(2 ** 100)
-KEYS_READ = (256, 256, 512, 512)
-ATTN_BANKS = (((0, 0), (1, 0)), ((2, 0), (3, 0)), ((2, 1), (3, 1)))
-VECTOR, SCALAR, GPSIMD = "vector", "scalar", "gpsimd"
-LARGE_FIRST = ((3, 0), (3, 1), (2, 0), (2, 1), (1, 0), (1, 1), (0, 0), (0, 1))
+BIG = float(2 ** 100)
+AW = (256, 256, 512, 512)
+SEGS = (((0, 0), (1, 0)), ((2, 0), (3, 0)), ((2, 1), (3, 1)))
+
+PERIOD = (
+    ("SC", 0, 3, 0), ("FO", -2, 2), ("MV", -1, 2), ("FO", -2, 3),
+    ("SC", 0, 3, 1), ("MV", -1, 3), ("MV", -1, 4), ("MV", -1, 5),
+    ("SC", 0, 2, 0), ("TA", -1, 0), ("TA", -1, 1), ("TA", -1, 2), ("TX", 0, 0), ("TX", 0, 1),
+    ("SC", 0, 2, 1), ("MV", -1, 6), ("MV", -1, 7),
+    ("SC", 0, 1), ("TQ", 1, 0), ("TQ", 1, 1),
+    ("SC", 0, 0), ("FO", -1, 0), ("MV", 0, 0), ("FO", -1, 1), ("MV", 0, 1),
+)
+LAG_COPY = 3.0
+LAG_MAX = 3.0
+LAG_EXP = 5.5
+LAG_QUANT = 3.0
+LAG_QUANT_A = 5.0
+LAG_SUM = 0.05
+LAG_STORE = 6.0
+COPY_OF = {"TX": "CX", "TQ": "CQ", "TA": "CA", "MV": "CV", "FO": "CO"}
+ENGINES = {"CX": "vs", "CQ": "ss", "CA": "svs", "CV": "vvsssvvs", "CO": "sssv", "CW": "svvs"}
+
+
+def order():
+    items = []
+    at = {}
+
+    def add(slot, step):
+        items.append((slot, len(items), step))
+
+    for period in range(-1, B + 2):
+        for i, entry in enumerate(PERIOD):
+            name, b = entry[0], period + entry[1]
+            arg = entry[2:]
+            slot = period * len(PERIOD) + i
+            if not 0 <= b < B:
+                continue
+            add(slot, (name, b) + arg)
+            if name == "SC":
+                it = arg[0]
+                for h in range(H) if it < 2 else (arg[1],):
+                    add(slot + LAG_MAX + 0.01 * h, ("RX", b, it, h))
+                    at[("EX", b, it, h)] = slot + LAG_MAX + LAG_EXP + 0.01 * h
+                    add(at[("EX", b, it, h)], ("EX", b, it, h))
+            else:
+                copy = COPY_OF[name]
+                at[(copy, b) + arg] = slot + LAG_COPY
+                add(slot + LAG_COPY, (copy, b) + arg + (ENGINES[copy][arg[0]],))
+    for b in range(B):
+        add(max(at[("CX", b, g)] for g in range(2)) + LAG_QUANT, ("QX", b))
+        for u in range(2):
+            add(max(at[("CV", b, 4 * u + c)] for c in range(4)) + LAG_QUANT, ("QV", b, u))
+        add(at[("CA", b, 0)] + LAG_QUANT_A, ("QA", b, 0))
+        add(max(at[("CA", b, g)] for g in (1, 2)) + LAG_QUANT_A, ("QA", b, 1))
+        for half, tiles in enumerate(((3, 2), (1, 0))):
+            slot = max(at[("EX", b, it, h)] for it in tiles for h in range(H)) + LAG_SUM
+            add(slot, ("RC", b, half))
+            for j, it in enumerate(tiles):
+                for h in range(H):
+                    add(slot + LAG_SUM + 0.001 * (2 * j + h), ("NO", b, it, h, "g"))
+        for pr in range(2):
+            add(max(at[("CO", b, 2 * pr + i)] for i in range(2)) + LAG_STORE, ("ST", b, pr))
+    add(-1, ("MB",))
+    for i, g in enumerate((0, 2, 1, 3)):
+        slot = 5 + 2 * i
+        add(slot, ("TW", g))
+        add(slot + LAG_COPY, ("CW", g, ENGINES["CW"][g]))
+        if i % 2:
+            add(slot + LAG_COPY + LAG_QUANT, ("QW", i // 2))
+    return [item[2] for item in sorted(items)]
 
 
 def tile_multiheadattention_pa_t_kernel(tc, q, k, x, Wv, mask, out):
     nc = tc.nc
     with ExitStack() as ctx:
+        ctx.enter_context(tc.manual_schedule())
         const = ctx.enter_context(tc.tile_pool(name="const", bufs=1))
         loads = ctx.enter_context(tc.tile_pool(name="loads", bufs=1))
         work = ctx.enter_context(tc.tile_pool(name="work", bufs=2))
-        stats = ctx.enter_context(tc.tile_pool(name="stats", bufs=3))
+        small = ctx.enter_context(tc.tile_pool(name="small", bufs=3))
         psum = ctx.enter_context(tc.psum_pool(name="psum", bufs=8))
-        live = {}
+        st = {}
 
-        def copy(engine, dst, src):
-            if engine == VECTOR:
+        def copy(eng, dst, src):
+            if eng == "v":
                 nc.vector.tensor_copy(out=dst, in_=src)
             else:
                 nc.scalar.copy(out=dst, in_=src)
@@ -45,472 +111,299 @@ def tile_multiheadattention_pa_t_kernel(tc, q, k, x, Wv, mask, out):
         x_sb = [loads.tile([P, NT * D], BF16, name="x_sb%d" % b) for b in range(B)]
         q_sb = [loads.tile([P, NT * H * L], BF16, name="q_sb%d" % b) for b in range(B)]
         k_sb = [loads.tile([P, NT * H * L], BF16, name="k_sb%d" % b) for b in range(B)]
-        wv_sb = loads.tile([P, 2 * NT * D], BF16, name="wv_sb")
-        mask_sb = loads.tile([P, 2 * P], I32, name="mask_sb")
+        wv_sb = loads.tile([P, 8 * D], BF16, name="wv_sb")
+        mk_i = loads.tile([P, 2 * P], I32, name="mk_i")
+        mask32 = mask.bitcast(I32)
+        wv_view = Wv.rearrange("(r p) d -> p r d", p=P)
 
-        def load_rows(dst, rows):
-            nc.sync.dma_start(out=dst[:].rearrange("p (a c) -> p a c", a=NT), in_=rows.rearrange("(a p) c -> p a c", p=P))
-
-        def load_x(b):
-            load_rows(x_sb[b], x[b])
-
-        def load_qk(b):
-            load_rows(q_sb[b], q[b].rearrange("s h l -> s (h l)"))
-            load_rows(k_sb[b], k[b].rearrange("s h l -> s (h l)"))
-
-        def load_wv(h):
+        def LX(b):
             nc.sync.dma_start(
-                out=wv_sb[:, h * NT * D : (h + 1) * NT * D].rearrange("p (a c) -> p a c", a=NT),
-                in_=Wv[h * D : (h + 1) * D, :].rearrange("(a p) c -> p a c", p=P),
+                out=x_sb[b][:].rearrange("p (u c) -> p u c", u=2), in_=x[b].rearrange("(u p e) d -> p u (e d)", u=2, e=2)
             )
 
-        identity_f32 = const.tile([P, P], F32, name="identity_f32")
-        identity_bf16 = const.tile([P, P], BF16, name="identity_bf16")
-        mask_f32 = const.tile([P, P], F32, name="mask_f32")
-        mask_bias = const.tile([P, P], BF16, name="mask_bias")
-        attn_sb = [
-            [const.tile([P, H * KEYS_READ[it]], BF16, name="attn_sb%d_%d" % (parity, it)) for it in range(NT)]
-            for parity in range(2)
-        ]
-        wv_grouped = const.tile([P, 2 * NT * D], BF16, name="wv_grouped", align_bytes=64)
-        wv_words = const.tile([P, H * D], U32, name="wv_words", align_bytes=64)
-        wv_scales = const.tile([P, H * D], U8, name="wv_scales", align_bytes=64)
+        def LQ(b):
+            nc.sync.dma_start(
+                out=q_sb[b][:].rearrange("p (a c) -> p a c", a=NT), in_=q[b].rearrange("(a p) h l -> p a (h l)", p=P)
+            )
 
-        def make_constants():
-            make_identity(nc, identity_bf16[:])
-            make_identity(nc, identity_f32[:])
-            for parity in range(2):
+        def LK(b):
+            nc.sync.dma_start(
+                out=k_sb[b][:].rearrange("p (a c) -> p a c", a=NT), in_=k[b].rearrange("(a p) h l -> p a (h l)", p=P)
+            )
+
+        def LW(half):
+            nc.sync.dma_start(
+                out=wv_sb[:, half * 4 * D : (half + 1) * 4 * D].rearrange("p (r d) -> p r d", r=4),
+                in_=wv_view[:, half * 4 : (half + 1) * 4, :],
+            )
+
+        def LM():
+            nc.sync.dma_start(out=mk_i[:], in_=mask32[0, 0:P, 0 : 2 * P])
+
+        id_f = const.tile([P, P], F32, name="id_f")
+        id_bf = const.tile([P, P], BF16, name="id_bf")
+        mk_f = const.tile([P, P], F32, name="mk_f")
+        mb = const.tile([P, P], BF16, name="mb")
+        a_sb = [[const.tile([P, H * AW[it]], BF16, name="a_sb%d_%d" % (par, it)) for it in range(NT)] for par in range(2)]
+        wvg = const.tile([P, 8 * D], BF16, name="wvg", align_bytes=64)
+        wvw = const.tile([P, H * D], U32, name="wvw", align_bytes=64)
+        wvs = const.tile([P, H * D], U8, name="wvs", align_bytes=64)
+
+        def INIT():
+            make_identity(nc, id_bf[:])
+            make_identity(nc, id_f[:])
+            for par in range(2):
                 for it in range(NT):
-                    keys = (it + 1) * P
-                    if keys < KEYS_READ[it]:
-                        by_head = attn_sb[parity][it][:].rearrange("p (h key) -> p h key", h=H)
-                        nc.gpsimd.memset(by_head[:, :, keys:], 0.0)
+                    n = (it + 1) * P
+                    if n < AW[it]:
+                        nc.gpsimd.memset(a_sb[par][it][:].rearrange("p (h j) -> p h j", h=H)[:, :, n:], 0.0)
 
-        def make_mask_bias():
-            nc.vector.tensor_copy(out=mask_f32[:], in_=mask_sb[:].rearrange("p (key word) -> p key word", word=2)[:, :, 0])
-            nc.vector.tensor_scalar(
-                out=mask_bias[:], in0=mask_f32[:], scalar1=1.0, scalar2=MASKED, op0=ALU.subtract, op1=ALU.mult
-            )
+        def MB():
+            nc.vector.tensor_copy(out=mk_f[:], in_=mk_i[:].rearrange("p (j w) -> p j w", w=2)[:, :, 0])
+            nc.vector.tensor_scalar(out=mb[:], in0=mk_f[:], scalar1=1.0, scalar2=BIG, op0=ALU.subtract, op1=ALU.mult)
 
-        def transpose_words(src, pair):
-            words = src[:].bitcast(F32)
-            bank = psum.tile([P, 2, 2, P], F32, name="bank_words", tag="bank")
-            for a in range(2):
-                for m in range(2):
-                    first = (2 * pair + a) * (D // 2) + m * P
-                    nc.tensor.transpose(bank[:, a, m, :], words[:, first : first + P], identity_f32[:])
-            return bank
+        def TW(g):
+            src = wv_sb[:].bitcast(F32)
+            ps = psum.tile([P, 2, 2, P], F32, name="ps_wv", tag="bank")
+            for rr in range(2):
+                for u in range(2):
+                    o = (2 * g + rr) * 256 + u * P
+                    nc.tensor.transpose(ps[:, rr, u, :], src[:, o : o + P], id_f[:])
+            st[("TW", g)] = ps
 
-        def copy_words(engine, grouped, row_tiles, pair, bank):
-            dst = grouped[:].bitcast(F32).rearrange("w (a r m) -> w a r m", a=row_tiles, m=2)
-            copy(engine, dst[:, 2 * pair : 2 * pair + 2, :, :], bank[:].rearrange("w a m r -> w a r m"))
+        def CW(g, eng):
+            dst = wvg[:].bitcast(F32).rearrange("w (r h c u) -> w h r c u", r=4, h=H, u=2)
+            r0 = 2 * g % 4
+            copy(eng, dst[:, g // 2, r0 : r0 + 2, :, :], st[("TW", g)][:].rearrange("w r u c -> w r c u"))
 
-        def transpose_wv(pair):
-            live[("wv bank", pair)] = transpose_words(wv_sb, pair)
-
-        def copy_wv(pair, engine):
-            copy_words(engine, wv_grouped, 2 * NT, pair, live[("wv bank", pair)])
-
-        def quantise_wv(h):
+        def QW(h):
             nc.vector.quantize_mx(
-                out=wv_words[:, h * D : (h + 1) * D].bitcast(FP8X4),
-                scales=wv_scales[:, h * D : (h + 1) * D],
-                in_=wv_grouped[:, h * PACK * D : (h + 1) * PACK * D],
+                out=wvw[:, h * D : (h + 1) * D].bitcast(FP8X4),
+                scales=wvs[:, h * D : (h + 1) * D],
+                in_=wvg[:, h * 4 * D : (h + 1) * 4 * D],
             )
 
-        def transpose_x(b, pair):
-            live[("x bank", b, pair)] = transpose_words(x_sb[b], pair)
+        def TX(b, g):
+            src = x_sb[b][:].bitcast(F32)
+            ps = psum.tile([P, 2, 2, P], F32, name="ps_x", tag="bank")
+            for a2 in range(2):
+                for u in range(2):
+                    o = (2 * g + a2) * 256 + u * P
+                    nc.tensor.transpose(ps[:, a2, u, :], src[:, o : o + P], id_f[:])
+            st[("TX", b, g)] = ps
 
-        def copy_x(b, pair, engine):
-            if pair == 0:
-                x_grouped = work.tile([P, NT * D], BF16, name="x_grouped", align_bytes=64)
-                live[("x grouped", b)] = x_grouped
-            copy_words(engine, live[("x grouped", b)], NT, pair, live[("x bank", b, pair)])
+        def CX(b, g, eng):
+            if ("xg", b) not in st:
+                xg_new = work.tile([P, NT * D], BF16, name="xg", align_bytes=64)
+                st[("xg", b)] = xg_new
+            dst = st[("xg", b)][:].bitcast(F32).rearrange("w (a p u) -> w a p u", a=NT, u=2)
+            copy(eng, dst[:, 2 * g : 2 * g + 2, :, :], st[("TX", b, g)][:].rearrange("w a u p -> w a p u"))
 
-        def quantise_x(b):
-            x_words = work.tile([P, S], U32, name="x_words", align_bytes=64)
-            x_scales = work.tile([P, S], U8, name="x_scales", align_bytes=64)
-            nc.vector.quantize_mx(out=x_words[:].bitcast(FP8X4), scales=x_scales[:], in_=live[("x grouped", b)][:])
-            live[("x", b)] = (x_words, x_scales)
+        def QX(b):
+            xw = work.tile([P, S], U32, name="xw", align_bytes=64)
+            xs = work.tile([P, S], U8, name="xs", align_bytes=64)
+            nc.vector.quantize_mx(out=xw[:].bitcast(FP8X4), scales=xs[:], in_=st[("xg", b)][:])
+            st[("xw", b)] = (xw, xs)
 
-        def values(b, bank_no):
-            x_words, x_scales = live[("x", b)]
-            u, c = bank_no // NT, bank_no % NT
-            bank = psum.tile([P, PACK, P], F32, name="bank_v", tag="bank")
-            for h in range(H):
-                for tile_in_pass in range(2):
-                    rows = slice((2 * u + tile_in_pass) * P, (2 * u + tile_in_pass + 1) * P)
-                    cols = slice(h * D + c * P, h * D + (c + 1) * P)
-                    nc.tensor.matmul_mx(
-                        out=bank[:, 2 * h + tile_in_pass, :],
-                        lhsT=x_words[:, rows].bitcast(FP8X4),
-                        lhsT_scale=x_scales[:, rows],
-                        rhs=wv_words[:, cols].bitcast(FP8X4),
-                        rhs_scale=wv_scales[:, cols],
-                        start=True,
-                        stop=True,
-                    )
-            live[("v bank", b, bank_no)] = bank
-
-        def copy_values(b, bank_no, engine):
-            if bank_no == 0:
-                v_grouped = work.tile([P, 2 * PACK * D], BF16, name="v_grouped", align_bytes=64)
-                live[("v grouped", b)] = v_grouped
-            dst = live[("v grouped", b)][:, bank_no * PACK * P : (bank_no + 1) * PACK * P]
-            copy(engine, dst.rearrange("p (d t) -> p d t", t=PACK), live[("v bank", b, bank_no)][:].rearrange("p t d -> p d t"))
-
-        def quantise_values(b):
-            v_words = work.tile([P, 2 * D], U32, name="v_words", align_bytes=64)
-            v_scales = work.tile([P, 2 * D], U8, name="v_scales", align_bytes=64)
-            nc.vector.quantize_mx(out=v_words[:].bitcast(FP8X4), scales=v_scales[:], in_=live[("v grouped", b)][:])
-            live[("v", b)] = (v_words, v_scales)
-
-        def transpose_qk(b, which):
-            src = (q_sb[b], k_sb[b])[which]
-            bank = psum.tile([P, H, NT, P], BF16, name="bank_qk", tag="bank")
+        def TQ(b, i):
+            src = (q_sb[b], k_sb[b])[i]
+            ps = psum.tile([P, H, NT, P], BF16, name="ps_qk", tag="bank")
             for h in range(H):
                 for a in range(NT):
-                    first = (a * H + h) * L
-                    nc.tensor.transpose(bank[:, h, a, :], src[:, first : first + L], identity_bf16[:])
-            live[("qk bank", b, which)] = bank
+                    o = a * H * L + h * L
+                    nc.tensor.transpose(ps[:, h, a, :], src[:, o : o + L], id_bf[:])
+            st[("TQ", b, i)] = ps
 
-        def copy_qk(b, which, engine):
-            transposed = work.tile([P, H * S], BF16, name="qk_transposed%d" % which)
-            copy(engine, transposed[:], live[("qk bank", b, which)][:].rearrange("l h a s -> l (h a s)"))
-            live[("qk", b, which)] = transposed
+        def CQ(b, i, eng):
+            dst = work.tile([P, H * S], BF16, name="qkT%d" % i)
+            copy(eng, dst[:], st[("TQ", b, i)][:].rearrange("l h a p -> l (h a p)"))
+            st[("qk", b, i)] = dst
 
-        def scores_of_head(b, it, h, dst):
-            q_t, k_t = live[("qk", b, 0)], live[("qk", b, 1)]
-            queries = q_t[:, h * S + it * P : h * S + (it + 1) * P]
-            diagonal = slice(it * P, (it + 1) * P)
-            if it > 0:
-                nc.tensor.matmul(out=dst[:, 0 : it * P], lhsT=queries, rhs=k_t[:, h * S : h * S + it * P], start=True, stop=True)
-            nc.tensor.matmul(
-                out=dst[:, diagonal], lhsT=queries, rhs=k_t[:, h * S + it * P : h * S + (it + 1) * P], start=True, stop=False
-            )
-            nc.tensor.matmul(out=dst[:, diagonal], lhsT=identity_bf16[:], rhs=mask_bias[:], start=False, stop=True)
+        def sc_head(b, it, h, view):
+            qT = st[("qk", b, 0)]
+            kT = st[("qk", b, 1)]
+            n = (it + 1) * P
+            lhsT = qT[:, h * S + it * P : h * S + (it + 1) * P]
+            nc.tensor.matmul(out=view[:, 0:n], lhsT=lhsT, rhs=kT[:, h * S : h * S + n], start=True, stop=False)
+            nc.tensor.matmul(out=view[:, it * P : n], lhsT=id_bf[:], rhs=mb[:], start=False, stop=True)
 
-        def scores(b, it, h=None):
-            keys = (it + 1) * P
-            if h is None:
-                bank = psum.tile([P, H, keys], F32, name="bank_scores2", tag="bank")
-                for head in range(H):
-                    scores_of_head(b, it, head, bank[:, head, :])
-                    live[("scores", b, it, head)] = bank[:, head, :]
+        def SC(b, it, h=0):
+            n = (it + 1) * P
+            if it < 2:
+                ps = psum.tile([P, H, n], F32, name="ps_s", tag="bank")
+                for hh in range(H):
+                    sc_head(b, it, hh, ps[:, hh, :])
+                    st[("S", b, it, hh)] = ps[:, hh, :]
+                st[("S2", b, it)] = ps
             else:
-                bank1 = psum.tile([P, keys], F32, name="bank_scores1", tag="bank")
-                scores_of_head(b, it, h, bank1[:])
-                live[("scores", b, it, h)] = bank1[:]
+                ps1 = psum.tile([P, n], F32, name="ps_s1", tag="bank")
+                sc_head(b, it, h, ps1[:])
+                st[("S", b, it, h)] = ps1[:]
 
-        def scale_and_minimum(b, it, h):
-            keys = (it + 1) * P
-            if ("stats", b) not in live:
-                bias = stats.tile([P, H * NT], F32, name="bias")
-                sums = stats.tile([P, H * NT], F32, name="sums")
-                inverse = stats.tile([P, H * NT], F32, name="inverse")
-                live[("stats", b)] = (bias, sums, inverse)
-            if h == 0:
-                e_sb = work.tile([P, H * keys], F32, name="e_sb%d" % it)
-                live[("e", b, it)] = e_sb
-            col = H * it + h
+        def RX(b, it, h):
+            n = (it + 1) * P
+            if ("nm", b) not in st:
+                nm_new = small.tile([P, 2 * NT], F32, name="nm")
+                sm_new = small.tile([P, 2 * NT], F32, name="sm")
+                rc_new = small.tile([P, 2 * NT], F32, name="rc")
+                st[("nm", b)] = (nm_new, sm_new, rc_new)
+            if ("e", b, it) not in st:
+                e_new = work.tile([P, H * n], F32, name="e_sb%d" % it)
+                st[("e", b, it)] = e_new
+            c = 2 * it + h
             nc.vector.tensor_scalar(
-                out=live[("e", b, it)][:, h * keys : (h + 1) * keys],
-                in0=live[("scores", b, it, h)],
+                out=st[("e", b, it)][:, h * n : (h + 1) * n],
+                in0=st[("S", b, it, h)],
                 scalar1=-SCALE,
                 scalar2=None,
                 op0=ALU.mult,
                 op1=ALU.min,
-                accum_out=live[("stats", b)][0][:, col : col + 1],
+                accum_out=st[("nm", b)][0][:, c : c + 1],
             )
 
-        def exponential(b, it, h):
-            keys = (it + 1) * P
-            col = H * it + h
-            bias, sums = live[("stats", b)][:2]
-            e_part = live[("e", b, it)][:, h * keys : (h + 1) * keys]
+        def EX(b, it, h):
+            n = (it + 1) * P
+            c = 2 * it + h
+            nm, sm, rc = st[("nm", b)]
+            e_sl = st[("e", b, it)][:, h * n : (h + 1) * n]
             nc.scalar.activation(
-                out=e_part, in_=e_part, func=ACT.Exp, bias=bias[:, col : col + 1], scale=-1.0, accum_out=sums[:, col : col + 1]
+                out=e_sl, in_=e_sl, func=ACT.Exp, bias=nm[:, c : c + 1], scale=-1.0, accum_out=sm[:, c : c + 1]
             )
 
-        def reciprocals(b, first_tile):
-            sums, inverse = live[("stats", b)][1:]
-            pair_cols = slice(H * first_tile, H * (first_tile + 2))
-            nc.vector.reciprocal(out=inverse[:, pair_cols], in_=sums[:, pair_cols])
+        def RC(b, half):
+            nm, sm, rc = st[("nm", b)]
+            lo = 4 - 4 * half
+            nc.vector.reciprocal(out=rc[:, lo : lo + 4], in_=sm[:, lo : lo + 4])
 
-        def normalise(b, it, h, engine):
-            keys = (it + 1) * P
-            col = H * it + h
-            dst = attn_sb[b % 2][it][:, h * KEYS_READ[it] : h * KEYS_READ[it] + keys]
-            src = live[("e", b, it)][:, h * keys : (h + 1) * keys]
-            factor = live[("stats", b)][2][:, col : col + 1]
-            if engine == GPSIMD:
-                nc.gpsimd.tensor_scalar(out=dst, in0=src, scalar1=factor, scalar2=0.0, op0=ALU.mult, op1=ALU.add)
+        def NO(b, it, h, eng):
+            n = (it + 1) * P
+            c = 2 * it + h
+            dst = a_sb[b % 2][it][:, h * AW[it] : h * AW[it] + n]
+            src = st[("e", b, it)][:, h * n : (h + 1) * n]
+            rcol = st[("nm", b)][2][:, c : c + 1]
+            if eng == "g":
+                nc.gpsimd.tensor_scalar(out=dst, in0=src, scalar1=rcol, scalar2=0.0, op0=ALU.mult, op1=ALU.add)
             else:
-                nc.vector.tensor_scalar(out=dst, in0=src, scalar1=factor, scalar2=None, op0=ALU.mult)
+                nc.vector.tensor_scalar(out=dst, in0=src, scalar1=rcol, scalar2=None, op0=ALU.mult)
 
-        def normalise_large(b):
-            reciprocals(b, 2)
-            for it, h in LARGE_FIRST[:4]:
-                normalise(b, it, h, GPSIMD)
-
-        def normalise_small(b):
-            reciprocals(b, 0)
-            for it, h in LARGE_FIRST[4:]:
-                normalise(b, it, h, GPSIMD)
-
-        def transpose_attn(b, bank_no):
-            bank = psum.tile([P, 2, PACK, P], BF16, name="bank_attn", tag="bank")
-            for place in range(2):
-                it, u = ATTN_BANKS[bank_no][place]
-                for h in range(H):
-                    for tile_in_pass in range(2):
-                        first = h * KEYS_READ[it] + (2 * u + tile_in_pass) * P
-                        nc.tensor.transpose(
-                            bank[:, place, 2 * h + tile_in_pass, :], attn_sb[b % 2][it][:, first : first + P], identity_bf16[:]
-                        )
-            live[("attn bank", b, bank_no)] = bank
-
-        def copy_attn(b, bank_no, engine):
-            if ("attn grouped", b) not in live:
-                attn_grouped = work.tile([P, 6 * PACK * P], BF16, name="attn_grouped", align_bytes=64)
-                live[("attn grouped", b)] = attn_grouped
-            dst = live[("attn grouped", b)][:, bank_no * 2 * PACK * P : (bank_no + 1) * 2 * PACK * P]
-            copy(
-                engine,
-                dst.rearrange("p (place i t) -> p place i t", place=2, t=PACK),
-                live[("attn bank", b, bank_no)][:].rearrange("p place t i -> p place i t"),
-            )
-
-        def quantise_attn(b, first_bank, last_bank):
-            if ("attn", b) not in live:
-                attn_words = work.tile([P, 6 * P], U32, name="attn_words", align_bytes=64)
-                attn_scales = work.tile([P, 6 * P], U8, name="attn_scales", align_bytes=64)
-                live[("attn", b)] = (attn_words, attn_scales)
-            attn_words, attn_scales = live[("attn", b)]
-            first, end = first_bank * 2 * P, (last_bank + 1) * 2 * P
-            nc.vector.quantize_mx(
-                out=attn_words[:, first:end].bitcast(FP8X4),
-                scales=attn_scales[:, first:end],
-                in_=live[("attn grouped", b)][:, PACK * first : PACK * end],
-            )
-
-        def product(b, it):
-            attn_words, attn_scales = live[("attn", b)]
-            v_words, v_scales = live[("v", b)]
-            bank = psum.tile([P, D], F32, name="bank_out", tag="bank")
-            passes = 1 if it < 2 else 2
-            for u in range(passes):
-                segment = it if u == 0 else it + 2
-                rows = slice(segment * P, (segment + 1) * P)
+        def MV(b, j):
+            xw, xs = st[("xw", b)]
+            U = j // 4
+            c = j % 4
+            ps = psum.tile([P, 2, H * P], F32, name="ps_v", tag="bank")
+            col = c * H * P
+            for e in range(2):
+                a = 2 * U + e
                 nc.tensor.matmul_mx(
-                    out=bank[:],
-                    lhsT=attn_words[:, rows].bitcast(FP8X4),
-                    lhsT_scale=attn_scales[:, rows],
-                    rhs=v_words[:, u * D : (u + 1) * D].bitcast(FP8X4),
-                    rhs_scale=v_scales[:, u * D : (u + 1) * D],
-                    start=(u == 0),
-                    stop=(u == passes - 1),
+                    out=ps[:, e, :],
+                    lhsT=xw[:, a * P : (a + 1) * P].bitcast(FP8X4),
+                    lhsT_scale=xs[:, a * P : (a + 1) * P],
+                    rhs=wvw[:, col : col + H * P].bitcast(FP8X4),
+                    rhs_scale=wvs[:, col : col + H * P],
+                    start=True,
+                    stop=True,
                 )
-            live[("out bank", b, it)] = bank
+            st[("MV", b, j)] = ps
 
-        def copy_out(b, it, engine):
-            if ("out", b) not in live:
-                out_sb = work.tile([P, NT * D], F32, name="out_sb")
-                live[("out", b)] = out_sb
-            copy(engine, live[("out", b)][:, it * D : (it + 1) * D], live[("out bank", b, it)][:])
-
-        def store(b, it, count):
-            nc.sync.dma_start(
-                out=out[b, it * P : (it + count) * P, :].rearrange("(a p) d -> p a d", p=P),
-                in_=live[("out", b)][:, it * D : (it + count) * D].rearrange("p (a d) -> p a d", a=count),
+        def CV(b, j, eng):
+            if ("vg", b) not in st:
+                vg_new = work.tile([P, 2 * 4 * D], BF16, name="vg", align_bytes=64)
+                st[("vg", b)] = vg_new
+            o = j * 4 * P
+            copy(
+                eng,
+                st[("vg", b)][:, o : o + 4 * P].rearrange("p (d h e) -> p d h e", h=H, e=2),
+                st[("MV", b, j)][:].rearrange("p e (h d) -> p d h e", h=H),
             )
 
-        def phase_plain(j):
-            transpose_x(j + 2, 0)
-            copy_x(j + 2, 0, SCALAR)
-            scores(j + 1, 3, 0)
-            scale_and_minimum(j + 1, 3, 0)
-            transpose_x(j + 2, 1)
-            copy_x(j + 2, 1, SCALAR)
-            scores(j + 1, 3, 1)
-            scale_and_minimum(j + 1, 3, 1)
-            transpose_qk(j + 2, 0)
-            copy_qk(j + 2, 0, SCALAR)
-            scores(j + 1, 2, 0)
-            scale_and_minimum(j + 1, 2, 0)
-            exponential(j + 1, 3, 0)
-            exponential(j + 1, 3, 1)
-            transpose_qk(j + 2, 1)
-            scores(j + 1, 2, 1)
-            scale_and_minimum(j + 1, 2, 1)
-            copy_qk(j + 2, 1, VECTOR)
-            transpose_attn(j, 1)
-            copy_attn(j, 1, SCALAR)
-            scores(j + 1, 1)
-            scale_and_minimum(j + 1, 1, 0)
-            scale_and_minimum(j + 1, 1, 1)
-            exponential(j + 1, 2, 0)
-            exponential(j + 1, 2, 1)
-            transpose_attn(j, 2)
-            scores(j + 1, 0)
-            scale_and_minimum(j + 1, 0, 0)
-            scale_and_minimum(j + 1, 0, 1)
-            copy_attn(j, 2, VECTOR)
-            transpose_attn(j, 0)
-            copy_attn(j, 0, SCALAR)
+        def QV(b, U):
+            if ("vw", b) not in st:
+                vw_new = work.tile([P, 2 * D], U32, name="vw", align_bytes=64)
+                vs_new = work.tile([P, 2 * D], U8, name="vs", align_bytes=64)
+                st[("vw", b)] = (vw_new, vs_new)
+            vw, vs = st[("vw", b)]
+            nc.vector.quantize_mx(
+                out=vw[:, U * D : (U + 1) * D].bitcast(FP8X4),
+                scales=vs[:, U * D : (U + 1) * D],
+                in_=st[("vg", b)][:, U * 4 * D : (U + 1) * 4 * D],
+            )
 
-        def phase_mx(j):
-            for bank_no in range(2 * NT):
-                values(j + 1, bank_no)
-            quantise_values(j)
-            quantise_attn(j, 1, 2)
-            quantise_attn(j, 0, 0)
-            normalise_large(j + 1)
-            for it in (2, 3, 0, 1):
-                product(j, it)
-            for bank_no in range(7):
-                copy_values(j + 1, bank_no, (VECTOR, SCALAR)[bank_no % 2])
-            for it, h in LARGE_FIRST[4:]:
-                exponential(j + 1, it, h)
-            copy_values(j + 1, 7, SCALAR)
-            copy_out(j, 0, VECTOR)
-            copy_out(j, 2, SCALAR)
-            copy_out(j, 3, SCALAR)
-            store(j, 2, 2)
-            copy_out(j, 1, SCALAR)
-            store(j, 0, 2)
-            quantise_x(j + 2)
-            normalise_small(j + 1)
+        def TA(b, g):
+            ps = psum.tile([P, 2, H, P], F32, name="ps_a", tag="bank")
+            for gi in range(2):
+                it, U = SEGS[g][gi]
+                words = a_sb[b % 2][it][:].bitcast(F32)
+                for h in range(H):
+                    o = h * (AW[it] // 2) + U * P
+                    nc.tensor.transpose(ps[:, gi, h, :], words[:, o : o + P], id_f[:])
+            st[("TA", b, g)] = ps
 
-        make_constants()
-        load_qk(0)
-        nc.sync.dma_start(out=mask_sb[:], in_=mask.bitcast(I32)[0, 0:P, 0 : 2 * P])
-        load_x(0)
-        load_wv(0)
-        load_wv(1)
-        load_qk(1)
-        load_x(1)
-        for b in range(2, B):
-            load_x(b)
-            load_qk(b)
+        def CA(b, g, eng):
+            if ("ag", b) not in st:
+                ag_new = work.tile([P, 6 * 4 * P], BF16, name="ag", align_bytes=64)
+                st[("ag", b)] = ag_new
+            copy(
+                eng,
+                st[("ag", b)][:].bitcast(F32)[:, g * 512 : (g + 1) * 512].rearrange("p (g i h) -> p g i h", g=2, h=H),
+                st[("TA", b, g)][:].rearrange("p g h i -> p g i h"),
+            )
 
-        transpose_qk(0, 0)
-        copy_qk(0, 0, VECTOR)
-        transpose_qk(0, 1)
-        copy_qk(0, 1, SCALAR)
-        make_mask_bias()
-        for it, h in LARGE_FIRST[:4]:
-            scores(0, it, h)
-        scores(0, 1)
-        scores(0, 0)
-        transpose_x(0, 0)
-        transpose_x(0, 1)
-        scale_and_minimum(0, 3, 0)
-        exponential(0, 3, 0)
-        copy_x(0, 0, SCALAR)
-        copy_x(0, 1, SCALAR)
-        for it, h in LARGE_FIRST[1:]:
-            scale_and_minimum(0, it, h)
-        for pair in range(4):
-            transpose_wv(pair)
-        copy_wv(0, SCALAR)
-        copy_wv(1, SCALAR)
-        for it, h in LARGE_FIRST[1:]:
-            exponential(0, it, h)
-        copy_wv(2, VECTOR)
-        quantise_x(0)
-        copy_wv(3, VECTOR)
-        quantise_wv(0)
-        quantise_wv(1)
-        transpose_qk(1, 0)
-        transpose_qk(1, 1)
-        transpose_x(1, 0)
-        transpose_x(1, 1)
-        for bank_no in range(2 * NT):
-            values(0, bank_no)
-        copy_qk(1, 0, VECTOR)
-        copy_qk(1, 1, VECTOR)
-        normalise_large(0)
-        copy_x(1, 0, VECTOR)
-        normalise_small(0)
-        copy_x(1, 1, SCALAR)
-        copy_values(0, 0, VECTOR)
-        copy_values(0, 1, SCALAR)
-        copy_values(0, 2, SCALAR)
-        quantise_x(1)
-        copy_values(0, 3, VECTOR)
-        copy_values(0, 4, SCALAR)
-        copy_values(0, 5, VECTOR)
-        copy_values(0, 6, SCALAR)
-        copy_values(0, 7, SCALAR)
+        def QA(b, part):
+            if ("aw", b) not in st:
+                aw_new = work.tile([P, 6 * P], U32, name="aw", align_bytes=64)
+                as_new = work.tile([P, 6 * P], U8, name="asc", align_bytes=64)
+                st[("aw", b)] = (aw_new, as_new)
+            aw, asc = st[("aw", b)]
+            lo, hi = ((0, 256), (256, 768))[part]
+            nc.vector.quantize_mx(out=aw[:, lo:hi].bitcast(FP8X4), scales=asc[:, lo:hi], in_=st[("ag", b)][:, 4 * lo : 4 * hi])
 
-        for j in range(B - 2):
-            phase_plain(j)
-            phase_mx(j)
+        def FO(b, it):
+            aw, asc = st[("aw", b)]
+            vw, vs = st[("vw", b)]
+            po = psum.tile([P, D], F32, name="po", tag="bank")
+            passes = [(it, 0)] + ([(it + 2, 1)] if it >= 2 else [])
+            for i, (seg, U) in enumerate(passes):
+                nc.tensor.matmul_mx(
+                    out=po[:],
+                    lhsT=aw[:, seg * P : (seg + 1) * P].bitcast(FP8X4),
+                    lhsT_scale=asc[:, seg * P : (seg + 1) * P],
+                    rhs=vw[:, U * D : (U + 1) * D].bitcast(FP8X4),
+                    rhs_scale=vs[:, U * D : (U + 1) * D],
+                    start=(i == 0),
+                    stop=(i == len(passes) - 1),
+                )
+            st[("FO", b, it)] = po
 
-        j, last = B - 2, B - 1
-        scores(last, 3, 0)
-        scale_and_minimum(last, 3, 0)
-        scores(last, 3, 1)
-        scale_and_minimum(last, 3, 1)
-        exponential(last, 3, 0)
-        scores(last, 2, 0)
-        scale_and_minimum(last, 2, 0)
-        exponential(last, 3, 1)
-        scores(last, 2, 1)
-        scale_and_minimum(last, 2, 1)
-        exponential(last, 2, 0)
-        exponential(last, 2, 1)
-        quantise_values(j)
-        transpose_attn(j, 1)
-        copy_attn(j, 1, SCALAR)
-        scores(last, 1)
-        transpose_attn(j, 2)
-        copy_attn(j, 2, VECTOR)
-        normalise_large(last)
-        scale_and_minimum(last, 1, 0)
-        scale_and_minimum(last, 1, 1)
-        scores(last, 0)
-        scale_and_minimum(last, 0, 0)
-        scale_and_minimum(last, 0, 1)
-        transpose_attn(j, 0)
-        copy_attn(j, 0, SCALAR)
-        for bank_no in range(2 * NT):
-            values(last, bank_no)
-        quantise_attn(j, 1, 2)
-        copy_values(last, 0, VECTOR)
-        copy_values(last, 1, VECTOR)
-        quantise_attn(j, 0, 0)
-        copy_values(last, 2, SCALAR)
-        for it, h in LARGE_FIRST[4:]:
-            exponential(last, it, h)
-        reciprocals(last, 0)
-        normalise(last, 1, 0, GPSIMD)
-        normalise(last, 1, 1, VECTOR)
-        normalise(last, 0, 0, GPSIMD)
-        normalise(last, 0, 1, VECTOR)
-        for it in (2, 3, 0, 1):
-            product(j, it)
-        for bank_no in range(3, 7):
-            copy_values(last, bank_no, SCALAR)
-        copy_values(last, 7, VECTOR)
-        transpose_attn(last, 1)
-        transpose_attn(last, 2)
-        transpose_attn(last, 0)
-        copy_out(j, 3, VECTOR)
-        copy_out(j, 2, SCALAR)
-        store(j, 2, 2)
-        quantise_values(last)
-        copy_attn(last, 1, SCALAR)
-        copy_attn(last, 2, VECTOR)
-        quantise_attn(last, 1, 2)
-        copy_out(j, 1, SCALAR)
-        copy_out(j, 0, VECTOR)
-        store(j, 0, 2)
-        copy_attn(last, 0, SCALAR)
-        quantise_attn(last, 0, 0)
-        for it in (2, 3, 0, 1):
-            product(last, it)
-        for it, engine in ((2, SCALAR), (3, VECTOR), (0, SCALAR), (1, VECTOR)):
-            copy_out(last, it, engine)
-            store(last, it, 1)
+        def CO(b, it, eng):
+            if ("o", b) not in st:
+                o_new = work.tile([P, NT * D], F32, name="o_sb")
+                st[("o", b)] = o_new
+            copy(eng, st[("o", b)][:, it * D : (it + 1) * D], st[("FO", b, it)][:])
+
+        def ST(b, pr):
+            nc.sync.dma_start(
+                out=out[b, 2 * pr * P : (2 * pr + 2) * P, :].rearrange("(a p) d -> p a d", p=P),
+                in_=st[("o", b)][:, 2 * pr * D : (2 * pr + 2) * D].rearrange("p (a d) -> p a d", a=2),
+            )
+
+        def ST4(b, it):
+            nc.sync.dma_start(out=out[b, it * P : (it + 1) * P, :], in_=st[("o", b)][:, it * D : (it + 1) * D])
+
+        steps = {
+            "LX": LX, "LQ": LQ, "LK": LK, "LW": LW, "LM": LM, "INIT": INIT, "MB": MB, "TW": TW, "CW": CW, "QW": QW,
+            "TX": TX, "CX": CX, "QX": QX, "TQ": TQ, "CQ": CQ, "SC": SC, "RX": RX, "EX": EX, "RC": RC,
+            "NO": NO, "MV": MV, "CV": CV, "QV": QV, "TA": TA, "CA": CA, "QA": QA, "FO": FO, "CO": CO, "ST": ST, "ST4": ST4,
+        }
+        INIT()
+        LQ(0)
+        LK(0)
+        LM()
+        LW(0)
+        LW(1)
+        LX(0)
+        for b in range(1, B):
+            LQ(b)
+            LK(b)
+            LX(b)
+        for step in order():
+            steps[step[0]](*step[1:])

@@ -24,22 +24,22 @@ AW = (256, 256, 512, 512)
 SEGS = (((0, 0), (1, 0)), ((2, 0), (3, 0)), ((2, 1), (3, 1)))
 
 PERIOD = (
-    ("SC", 0, 3, 0), ("FO", -2, 2), ("MV", -1, 2), ("FO", -2, 3),
-    ("SC", 0, 3, 1), ("MV", -1, 3), ("MV", -1, 4), ("MV", -1, 5),
-    ("SC", 0, 2, 0), ("TA", -1, 0), ("TA", -1, 1), ("TA", -1, 2), ("TX", 0, 0), ("TX", 0, 1),
-    ("SC", 0, 2, 1), ("MV", -1, 6), ("MV", -1, 7),
-    ("SC", 0, 1), ("TQ", 1, 0), ("TQ", 1, 1),
-    ("SC", 0, 0), ("FO", -1, 0), ("MV", 0, 0), ("FO", -1, 1), ("MV", 0, 1),
+    ("SC", 0, 3, 0), ("SC", 0, 3, 1), ("FO", -2, 0), ("FO", -2, 1), ("MV", -1, 2), ("FO", -2, 2), ("FO", -2, 3),
+    ("SC", 0, 2, 0), ("SC", 0, 2, 1), ("MV", -1, 3), ("MV", -1, 4), ("TX", 0, 0), ("TX", 0, 1), ("MV", -1, 5),
+    ("SC", 0, 1), ("SC", 0, 0), ("MV", -1, 6), ("MV", -1, 7), ("TA", -1, 1), ("TA", -1, 2), ("TA", -1, 0),
+    ("TQ", 1, 0), ("TQ", 1, 1), ("MV", 0, 0), ("MV", 0, 1),
 )
-LAG_COPY = 3.0
-LAG_MAX = 3.0
-LAG_EXP = 5.5
-LAG_QUANT = 3.0
-LAG_QUANT_A = 5.0
-LAG_SUM = 0.05
-LAG_STORE = 6.0
+LAG_COPY = 2
+LAG_MAX = 2
+LAG_EXP = 8
+LAG_QUANT_X = 3
+LAG_QUANT_V = 6
+LAG_QUANT_A = 2
+LAG_SUM = 6
+LAG_NORM = 1
+LAG_STORE = 8
 COPY_OF = {"TX": "CX", "TQ": "CQ", "TA": "CA", "MV": "CV", "FO": "CO"}
-ENGINES = {"CX": "vs", "CQ": "ss", "CA": "svs", "CV": "vvsssvvs", "CO": "sssv", "CW": "svvs"}
+ENGINES = {"CX": "ss", "CQ": "vs", "CA": "sss", "CV": "svsvsvsv", "CO": "svsv", "CW": "svvs"}
 
 
 def order():
@@ -68,9 +68,9 @@ def order():
                 at[(copy, b) + arg] = slot + LAG_COPY
                 add(slot + LAG_COPY, (copy, b) + arg + (ENGINES[copy][arg[0]],))
     for b in range(B):
-        add(max(at[("CX", b, g)] for g in range(2)) + LAG_QUANT, ("QX", b))
+        add(max(at[("CX", b, g)] for g in range(2)) + LAG_QUANT_X, ("QX", b))
         for u in range(2):
-            add(max(at[("CV", b, 4 * u + c)] for c in range(4)) + LAG_QUANT, ("QV", b, u))
+            add(max(at[("CV", b, 4 * u + c)] for c in range(4)) + LAG_QUANT_V, ("QV", b, u))
         add(at[("CA", b, 0)] + LAG_QUANT_A, ("QA", b, 0))
         add(max(at[("CA", b, g)] for g in (1, 2)) + LAG_QUANT_A, ("QA", b, 1))
         for half, tiles in enumerate(((3, 2), (1, 0))):
@@ -78,7 +78,7 @@ def order():
             add(slot, ("RC", b, half))
             for j, it in enumerate(tiles):
                 for h in range(H):
-                    add(slot + LAG_SUM + 0.001 * (2 * j + h), ("NO", b, it, h, "g"))
+                    add(slot + LAG_NORM + 0.001 * (2 * j + h), ("NO", b, it, h, "g"))
         for pr in range(2):
             add(max(at[("CO", b, 2 * pr + i)] for i in range(2)) + LAG_STORE, ("ST", b, pr))
     add(-1, ("MB",))
@@ -87,7 +87,7 @@ def order():
         add(slot, ("TW", g))
         add(slot + LAG_COPY, ("CW", g, ENGINES["CW"][g]))
         if i % 2:
-            add(slot + LAG_COPY + LAG_QUANT, ("QW", i // 2))
+            add(slot + LAG_COPY + LAG_QUANT_X, ("QW", i // 2))
     return [item[2] for item in sorted(items)]
 
 

@@ -24,22 +24,22 @@ AW = (256, 256, 512, 512)
 SEGS = (((0, 0), (1, 0)), ((2, 0), (3, 0)), ((2, 1), (3, 1)))
 
 PERIOD = (
-    ("SC", 0, 3, 0), ("SC", 0, 3, 1), ("FO", -2, 0), ("FO", -2, 1), ("MV", -1, 2), ("FO", -2, 2), ("FO", -2, 3),
-    ("SC", 0, 2, 0), ("SC", 0, 2, 1), ("MV", -1, 3), ("MV", -1, 4), ("TX", 0, 0), ("TX", 0, 1), ("MV", -1, 5),
-    ("SC", 0, 1), ("SC", 0, 0), ("MV", -1, 6), ("MV", -1, 7), ("TA", -1, 1), ("TA", -1, 2), ("TA", -1, 0),
-    ("TQ", 1, 0), ("TQ", 1, 1), ("MV", 0, 0), ("MV", 0, 1),
+    ("SC", 0, 3, 0), ("SC", 0, 1), ("MV", -2, 0), ("MV", -2, 1), ("MV", -2, 2), ("MV", -2, 3),
+    ("SC", 0, 0), ("FO", -3, 0), ("SC", 0, 2, 1), ("TQ", 1, 0), ("MV", -2, 4), ("FO", -3, 1), ("FO", -3, 2),
+    ("TQ", 1, 1), ("TA", -2, 1), ("SC", 0, 2, 0), ("SC", 0, 3, 1), ("TX", 0, 1), ("TX", 0, 0), ("TA", -2, 2),
+    ("MV", -2, 5), ("MV", -2, 6), ("MV", -2, 7), ("TA", -1, 0), ("FO", -3, 3),
 )
-LAG_COPY = 2
-LAG_MAX = 2
-LAG_EXP = 8
-LAG_QUANT_X = 3
-LAG_QUANT_V = 6
-LAG_QUANT_A = 2
-LAG_SUM = 6
-LAG_NORM = 1
-LAG_STORE = 8
+LAG_COPY = 4
+LAG_MAX = 3
+LAG_EXP = 9
+LAG_QUANT_X = 16
+LAG_QUANT_V = 6.5
+LAG_QUANT_A = 7
+LAG_SUM = 9
+LAG_NORM = 8
+LAG_STORE = 6
 COPY_OF = {"TX": "CX", "TQ": "CQ", "TA": "CA", "MV": "CV", "FO": "CO"}
-ENGINES = {"CX": "ss", "CQ": "vs", "CA": "sss", "CV": "svsvsvsv", "CO": "svsv", "CW": "svvs"}
+ENGINES = {"CX": "ss", "CQ": "ss", "CA": "sss", "CV": "vvvsvvvs", "CO": "ssss", "CW": "svvs"}
 
 
 def order():
@@ -49,7 +49,7 @@ def order():
     def add(slot, step):
         items.append((slot, len(items), step))
 
-    for period in range(-1, B + 2):
+    for period in range(-1, B + 3):
         for i, entry in enumerate(PERIOD):
             name, b = entry[0], period + entry[1]
             arg = entry[2:]

@@ -24,22 +24,32 @@ AW = (256, 256, 512, 512)
 SEGS = (((0, 0), (1, 0)), ((2, 0), (3, 0)), ((2, 1), (3, 1)))
 
 PERIOD = (
-    ("SC", 0, 3, 0), ("SC", 0, 1), ("MV", -2, 0), ("MV", -2, 1), ("MV", -2, 2), ("MV", -2, 3),
-    ("SC", 0, 0), ("FO", -3, 0), ("SC", 0, 2, 1), ("TQ", 1, 0), ("MV", -2, 4), ("FO", -3, 1), ("FO", -3, 2),
-    ("TQ", 1, 1), ("TA", -2, 1), ("SC", 0, 2, 0), ("SC", 0, 3, 1), ("TX", 0, 1), ("TX", 0, 0), ("TA", -2, 2),
-    ("MV", -2, 5), ("MV", -2, 6), ("MV", -2, 7), ("TA", -1, 0), ("FO", -3, 3),
+    ("SC", 0, 1), ("MV", -2, 0), ("MV", -2, 1), ("SC", 0, 0), ("FO", -3, 0), ("TA", -2, 2),
+    ("MV", -2, 2), ("FO", -3, 1), ("MV", -2, 3), ("SC", 0, 3, 0), ("MV", -2, 4), ("TQ", 1, 0),
+    ("SC", 0, 3, 1), ("MV", -2, 5), ("TQ", 1, 1), ("MV", -2, 6), ("FO", -3, 2),
+    ("SC", 0, 2, 0), ("MV", -2, 7), ("FO", -3, 3), ("SC", 0, 2, 1), ("TX", 0, 1), ("TA", -2, 1), ("TA", -1, 0),
+    ("TX", 0, 0),
 )
-LAG_COPY = 4
-LAG_MAX = 3
-LAG_EXP = 9
-LAG_QUANT_X = 16
-LAG_QUANT_V = 6.5
-LAG_QUANT_A = 7
-LAG_SUM = 9
-LAG_NORM = 8
+LAG_COPY = 6.5
+LAG_MAX = 6.5
+LAG_EXP = 8
+LAG_QUANT_X = 2
+LAG_QUANT = 1.5
+LAG_SUM = 0.5
+LAG_NORM = 1
 LAG_STORE = 6
+STOPS = (2.05, 14.05)
 COPY_OF = {"TX": "CX", "TQ": "CQ", "TA": "CA", "MV": "CV", "FO": "CO"}
-ENGINES = {"CX": "ss", "CQ": "ss", "CA": "sss", "CV": "vvvsvvvs", "CO": "ssss", "CW": "svvs"}
+HEAD_W = (
+    (0.5, ("TW", 2)), (1, ("CW", 2, "s")), (1.5, ("TW", 1)), (2, ("CW", 1, "s")), (2.6, ("TW", 3)),
+    (7, ("CW", 3, "v")), (27.5, ("QW", 0)), (31.5, ("QW", 1)),
+)
+ENGINES = {"CX": "ss", "CQ": "ss", "CA": "sss", "CV": "vvvsvvvs", "CO": "ssss"}
+
+
+def next_stop(slot):
+    period = len(PERIOD)
+    return min(stop + period * math.ceil((slot - stop) / period) for stop in STOPS)
 
 
 def order():
@@ -54,7 +64,7 @@ def order():
             name, b = entry[0], period + entry[1]
             arg = entry[2:]
             slot = period * len(PERIOD) + i
-            if not 0 <= b < B:
+            if not 0 <= b < B or entry[:2] == ("TQ", 1) and b == 0:
                 continue
             add(slot, (name, b) + arg)
             if name == "SC":
@@ -68,26 +78,21 @@ def order():
                 at[(copy, b) + arg] = slot + LAG_COPY
                 add(slot + LAG_COPY, (copy, b) + arg + (ENGINES[copy][arg[0]],))
     for b in range(B):
-        add(max(at[("CX", b, g)] for g in range(2)) + LAG_QUANT_X, ("QX", b))
+        add(next_stop(max(at[("CX", b, g)] for g in range(2)) + LAG_QUANT_X), ("QX", b))
         for u in range(2):
-            add(max(at[("CV", b, 4 * u + c)] for c in range(4)) + LAG_QUANT_V, ("QV", b, u))
-        add(at[("CA", b, 0)] + LAG_QUANT_A, ("QA", b, 0))
-        add(max(at[("CA", b, g)] for g in (1, 2)) + LAG_QUANT_A, ("QA", b, 1))
+            add(next_stop(max(at[("CV", b, 4 * u + c)] for c in range(4)) + LAG_QUANT) + 0.01 + 0.001 * u, ("QV", b, u))
+        add(next_stop(at[("CA", b, 0)] + LAG_QUANT) + 0.02, ("QA", b, 0))
+        add(next_stop(max(at[("CA", b, g)] for g in (1, 2)) + LAG_QUANT) + 0.021, ("QA", b, 1))
         for half, tiles in enumerate(((3, 2), (1, 0))):
-            slot = max(at[("EX", b, it, h)] for it in tiles for h in range(H)) + LAG_SUM
+            slot = next_stop(max(at[("EX", b, it, h)] for it in tiles for h in range(H)) + LAG_SUM - 0.25) + 0.25
             add(slot, ("RC", b, half))
             for j, it in enumerate(tiles):
                 for h in range(H):
                     add(slot + LAG_NORM + 0.001 * (2 * j + h), ("NO", b, it, h, "g"))
         for pr in range(2):
             add(max(at[("CO", b, 2 * pr + i)] for i in range(2)) + LAG_STORE, ("ST", b, pr))
-    add(-1, ("MB",))
-    for i, g in enumerate((0, 2, 1, 3)):
-        slot = 5 + 2 * i
-        add(slot, ("TW", g))
-        add(slot + LAG_COPY, ("CW", g, ENGINES["CW"][g]))
-        if i % 2:
-            add(slot + LAG_COPY + LAG_QUANT_X, ("QW", i // 2))
+    for slot, step in HEAD_W:
+        add(slot, step)
     return [item[2] for item in sorted(items)]
 
 
@@ -131,10 +136,10 @@ def tile_multiheadattention_pa_t_kernel(tc, q, k, x, Wv, mask, out):
                 out=k_sb[b][:].rearrange("p (a c) -> p a c", a=NT), in_=k[b].rearrange("(a p) h l -> p a (h l)", p=P)
             )
 
-        def LW(half):
+        def LW(g):
             nc.sync.dma_start(
-                out=wv_sb[:, half * 4 * D : (half + 1) * 4 * D].rearrange("p (r d) -> p r d", r=4),
-                in_=wv_view[:, half * 4 : (half + 1) * 4, :],
+                out=wv_sb[:, g * 2 * D : (g + 1) * 2 * D].rearrange("p (r d) -> p r d", r=2),
+                in_=wv_view[:, g * 2 : (g + 1) * 2, :],
             )
 
         def LM():
@@ -148,6 +153,14 @@ def tile_multiheadattention_pa_t_kernel(tc, q, k, x, Wv, mask, out):
         wvg = const.tile([P, 8 * D], BF16, name="wvg", align_bytes=64)
         wvw = const.tile([P, H * D], U32, name="wvw", align_bytes=64)
         wvs = const.tile([P, H * D], U8, name="wvs", align_bytes=64)
+
+        warm = const.tile([P, P], BF16, name="warm")
+
+        def WARM(count):
+            for i in range(count):
+                ps = psum.tile([P, 4, P], F32, name="ps_w", tag="bank")
+                for j in range(4):
+                    nc.tensor.matmul(out=ps[:, j, :], lhsT=warm[:], rhs=warm[:], start=True, stop=True)
 
         def INIT():
             make_identity(nc, id_bf[:])
@@ -216,7 +229,7 @@ def tile_multiheadattention_pa_t_kernel(tc, q, k, x, Wv, mask, out):
 
         def CQ(b, i, eng):
             dst = work.tile([P, H * S], BF16, name="qkT%d" % i)
-            copy(eng, dst[:], st[("TQ", b, i)][:].rearrange("l h a p -> l (h a p)"))
+            copy(eng, dst[:].bitcast(F32), st[("TQ", b, i)][:].rearrange("l h a p -> l (h a p)").bitcast(F32))
             st[("qk", b, i)] = dst
 
         def sc_head(b, it, h, view):
@@ -381,6 +394,10 @@ def tile_multiheadattention_pa_t_kernel(tc, q, k, x, Wv, mask, out):
             copy(eng, st[("o", b)][:, it * D : (it + 1) * D], st[("FO", b, it)][:])
 
         def ST(b, pr):
+            if b == B - 1:
+                ST4(b, 2 * pr)
+                ST4(b, 2 * pr + 1)
+                return
             nc.sync.dma_start(
                 out=out[b, 2 * pr * P : (2 * pr + 2) * P, :].rearrange("(a p) d -> p a d", p=P),
                 in_=st[("o", b)][:, 2 * pr * D : (2 * pr + 2) * D].rearrange("p (a d) -> p a d", a=2),
@@ -390,20 +407,30 @@ def tile_multiheadattention_pa_t_kernel(tc, q, k, x, Wv, mask, out):
             nc.sync.dma_start(out=out[b, it * P : (it + 1) * P, :], in_=st[("o", b)][:, it * D : (it + 1) * D])
 
         steps = {
-            "LX": LX, "LQ": LQ, "LK": LK, "LW": LW, "LM": LM, "INIT": INIT, "MB": MB, "TW": TW, "CW": CW, "QW": QW,
+            "TW": TW, "CW": CW, "QW": QW,
             "TX": TX, "CX": CX, "QX": QX, "TQ": TQ, "CQ": CQ, "SC": SC, "RX": RX, "EX": EX, "RC": RC,
-            "NO": NO, "MV": MV, "CV": CV, "QV": QV, "TA": TA, "CA": CA, "QA": QA, "FO": FO, "CO": CO, "ST": ST, "ST4": ST4,
+            "NO": NO, "MV": MV, "CV": CV, "QV": QV, "TA": TA, "CA": CA, "QA": QA, "FO": FO, "CO": CO, "ST": ST,
         }
+        nc.vector.memset(warm[:].bitcast(I32), 0)
+        WARM(4)
         INIT()
         LQ(0)
         LK(0)
         LM()
-        LW(0)
-        LW(1)
+        for g in (0, 2, 1, 3):
+            LW(g)
         LX(0)
         for b in range(1, B):
             LQ(b)
             LK(b)
             LX(b)
+        TQ(0, 0)
+        CQ(0, 0, "s")
+        TQ(0, 1)
+        MB()
+        CQ(0, 1, "v")
+        WARM(2)
+        TW(0)
+        CW(0, "s")
         for step in order():
             steps[step[0]](*step[1:])

from contextlib import ExitStack
import math

import concourse.mybir as mybir
from concourse.masks import make_identity

F32 = mybir.dt.float32
BF16 = mybir.dt.bfloat16
I32 = mybir.dt.int32
U32 = mybir.dt.uint32
U8 = mybir.dt.uint8
FP8X4 = mybir.dt.float8_e4m3fn_x4
ALU = mybir.AluOpType
ACT = mybir.ActivationFunctionType
AX = mybir.AxisListType

B, S, D, H, L = 8, 512, 512, 2, 128
P = 128
NT = S // P
FLOPS = 2 * B * S * D * H * D + 2 * B * H * S * S * L + 2 * B * S * H * S * D
SCALE = 1.0 / math.sqrt(L)
BIG = float(2 ** 100)
AW = (256, 256, 512, 512)
SEGS = (((0, 0), (1, 0)), ((2, 0), (3, 0)), ((2, 1), (3, 1)))

PERIOD = (
    ("SC", 0, 1), ("MV", -2, 0), ("MV", -2, 1), ("SC", 0, 0), ("FO", -3, 0), ("TA", -2, 2),
    ("MV", -2, 2), ("FO", -3, 1), ("MV", -2, 3), ("SC", 0, 3, 0), ("MV", -2, 4), ("TQ", 1, 0),
    ("SC", 0, 3, 1), ("MV", -2, 5), ("TQ", 1, 1), ("MV", -2, 6), ("FO", -3, 2),
    ("SC", 0, 2, 0), ("MV", -2, 7), ("FO", -3, 3), ("SC", 0, 2, 1), ("TX", 0, 1), ("TA", -2, 1), ("TA", -1, 0),
    ("TX", 0, 0),
)
LAG_COPY = 6.5
LAG_MAX = 6.5
LAG_EXP = 8
LAG_QUANT_X = 2
LAG_QUANT = 1.5
LAG_SUM = 0.5
LAG_NORM = 1
LAG_STORE = 6
STOPS = (2.05, 14.05)
COPY_OF = {"TX": "CX", "TQ": "CQ", "TA": "CA", "MV": "CV", "FO": "CO"}
HEAD_W = (
    (0.5, ("TW", 2)), (1, ("CW", 2, "s")), (1.5, ("TW", 1)), (2, ("CW", 1, "s")), (2.6, ("TW", 3)),
    (7, ("CW", 3, "v")), (27.5, ("QW", 0)), (31.5, ("QW", 1)),
)
ENGINES = {"CX": "ss", "CQ": "ss", "CA": "sss", "CV": "vvvsvvvs", "CO": "ssss"}


def next_stop(slot):
    period = len(PERIOD)
    return min(stop + period * math.ceil((slot - stop) / period) for stop in STOPS)


def order():
    items = []
    at = {}

    def add(slot, step):
        items.append((slot, len(items), step))

    for period in range(-1, B + 3):
        for i, entry in enumerate(PERIOD):
            name, b = entry[0], period + entry[1]
            arg = entry[2:]
            slot = period * len(PERIOD) + i
            if not 0 <= b < B or entry[:2] == ("TQ", 1) and b == 0:
                continue
            add(slot, (name, b) + arg)
            if name == "SC":
                it = arg[0]
                for h in range(H) if it < 2 else (arg[1],):
                    add(slot + LAG_MAX + 0.01 * h, ("RX", b, it, h))
                    at[("EX", b, it, h)] = slot + LAG_MAX + LAG_EXP + 0.01 * h
                    add(at[("EX", b, it, h)], ("EX", b, it, h))
            else:
                copy = COPY_OF[name]
                at[(copy, b) + arg] = slot + LAG_COPY
                add(slot + LAG_COPY, (copy, b) + arg + (ENGINES[copy][arg[0]],))
    for b in range(B):
        add(next_stop(max(at[("CX", b, g)] for g in range(2)) + LAG_QUANT_X), ("QX", b))
        for u in range(2):
            add(next_stop(max(at[("CV", b, 4 * u + c)] for c in range(4)) + LAG_QUANT) + 0.01 + 0.001 * u, ("QV", b, u))
        add(next_stop(at[("CA", b, 0)] + LAG_QUANT) + 0.02, ("QA", b, 0))
        add(next_stop(max(at[("CA", b, g)] for g in (1, 2)) + LAG_QUANT) + 0.021, ("QA", b, 1))
        for half, tiles in enumerate(((3, 2), (1, 0))):
            slot = next_stop(max(at[("EX", b, it, h)] for it in tiles for h in range(H)) + LAG_SUM - 0.25) + 0.25
            add(slot, ("RC", b, half))
            for j, it in enumerate(tiles):
                for h in range(H):
                    add(slot + LAG_NORM + 0.001 * (2 * j + h), ("NO", b, it, h, "g"))
        for pr in range(2):
            add(max(at[("CO", b, 2 * pr + i)] for i in range(2)) + LAG_STORE, ("ST", b, pr))
    for slot, step in HEAD_W:
        add(slot, step)
    return [item[2] for item in sorted(items)]


def tile_multiheadattention_pa_t_kernel(tc, q, k, x, Wv, mask, out):
    nc = tc.nc
    with ExitStack() as ctx:
        ctx.enter_context(tc.manual_schedule())
        const = ctx.enter_context(tc.tile_pool(name="const", bufs=1))
        loads = ctx.enter_context(tc.tile_pool(name="loads", bufs=1))
        work = ctx.enter_context(tc.tile_pool(name="work", bufs=2))
        small = ctx.enter_context(tc.tile_pool(name="small", bufs=3))
        psum = ctx.enter_context(tc.psum_pool(name="psum", bufs=8))
        st = {}

        def copy(eng, dst, src):
            if eng == "v":
                nc.vector.tensor_copy(out=dst, in_=src)
            else:
                nc.scalar.copy(out=dst, in_=src)

        x_sb = [loads.tile([P, NT * D], BF16, name="x_sb%d" % b) for b in range(B)]
        q_sb = [loads.tile([P, NT * H * L], BF16, name="q_sb%d" % b) for b in range(B)]
        k_sb = [loads.tile([P, NT * H * L], BF16, name="k_sb%d" % b) for b in range(B)]
        wv_sb = loads.tile([P, 8 * D], BF16, name="wv_sb")
        mk_i = loads.tile([P, 2 * P], I32, name="mk_i")
        mask32 = mask.bitcast(I32)
        wv_view = Wv.rearrange("(r p) d -> p r d", p=P)

        def LX(b):
            nc.sync.dma_start(
                out=x_sb[b][:].rearrange("p (u c) -> p u c", u=2), in_=x[b].rearrange("(u p e) d -> p u (e d)", u=2, e=2)
            )

        def LQ(b):
            nc.sync.dma_start(
                out=q_sb[b][:].rearrange("p (a c) -> p a c", a=NT), in_=q[b].rearrange("(a p) h l -> p a (h l)", p=P)
            )

        def LK(b):
            nc.sync.dma_start(
                out=k_sb[b][:].rearrange("p (a c) -> p a c", a=NT), in_=k[b].rearrange("(a p) h l -> p a (h l)", p=P)
            )

        def LW(g):
            nc.sync.dma_start(
                out=wv_sb[:, g * 2 * D : (g + 1) * 2 * D].rearrange("p (r d) -> p r d", r=2),
                in_=wv_view[:, g * 2 : (g + 1) * 2, :],
            )

        def LM():
            nc.sync.dma_start(out=mk_i[:], in_=mask32[0, 0:P, 0 : 2 * P])

        id_f = const.tile([P, P], F32, name="id_f")
        id_bf = const.tile([P, P], BF16, name="id_bf")
        mk_f = const.tile([P, P], F32, name="mk_f")
        mb = const.tile([P, P], BF16, name="mb")
        a_sb = [[const.tile([P, H * AW[it]], BF16, name="a_sb%d_%d" % (par, it)) for it in range(NT)] for par in range(2)]
        wvg = const.tile([P, 8 * D], BF16, name="wvg", align_bytes=64)
        wvw = const.tile([P, H * D], U32, name="wvw", align_bytes=64)
        wvs = const.tile([P, H * D], U8, name="wvs", align_bytes=64)

        warm = const.tile([P, P], BF16, name="warm")

        def WARM(count):
            for i in range(count):
                ps = psum.tile([P, 4, P], F32, name="ps_w", tag="bank")
                for j in range(4):
                    nc.tensor.matmul(out=ps[:, j, :], lhsT=warm[:], rhs=warm[:], start=True, stop=True)

        def INIT():
            make_identity(nc, id_bf[:])
            make_identity(nc, id_f[:])
            for par in range(2):
                for it in range(NT):
                    n = (it + 1) * P
                    if n < AW[it]:
                        nc.gpsimd.memset(a_sb[par][it][:].rearrange("p (h j) -> p h j", h=H)[:, :, n:], 0.0)

        def MB():
            nc.vector.tensor_copy(out=mk_f[:], in_=mk_i[:].rearrange("p (j w) -> p j w", w=2)[:, :, 0])
            nc.vector.tensor_scalar(out=mb[:], in0=mk_f[:], scalar1=1.0, scalar2=BIG, op0=ALU.subtract, op1=ALU.mult)

        def TW(g):
            src = wv_sb[:].bitcast(F32)
            ps = psum.tile([P, 2, 2, P], F32, name="ps_wv", tag="bank")
            for rr in range(2):
                for u in range(2):
                    o = (2 * g + rr) * 256 + u * P
                    nc.tensor.transpose(ps[:, rr, u, :], src[:, o : o + P], id_f[:])
            st[("TW", g)] = ps

        def CW(g, eng):
            dst = wvg[:].bitcast(F32).rearrange("w (r h c u) -> w h r c u", r=4, h=H, u=2)
            r0 = 2 * g % 4
            copy(eng, dst[:, g // 2, r0 : r0 + 2, :, :], st[("TW", g)][:].rearrange("w r u c -> w r c u"))

        def QW(h):
            nc.vector.quantize_mx(
                out=wvw[:, h * D : (h + 1) * D].bitcast(FP8X4),
                scales=wvs[:, h * D : (h + 1) * D],
                in_=wvg[:, h * 4 * D : (h + 1) * 4 * D],
            )

        def TX(b, g):
            src = x_sb[b][:].bitcast(F32)
            ps = psum.tile([P, 2, 2, P], F32, name="ps_x", tag="bank")
            for a2 in range(2):
                for u in range(2):
                    o = (2 * g + a2) * 256 + u * P
                    nc.tensor.transpose(ps[:, a2, u, :], src[:, o : o + P], id_f[:])
            st[("TX", b, g)] = ps

        def CX(b, g, eng):
            if ("xg", b) not in st:
                xg_new = work.tile([P, NT * D], BF16, name="xg", align_bytes=64)
                st[("xg", b)] = xg_new
            dst = st[("xg", b)][:].bitcast(F32).rearrange("w (a p u) -> w a p u", a=NT, u=2)
            copy(eng, dst[:, 2 * g : 2 * g + 2, :, :], st[("TX", b, g)][:].rearrange("w a u p -> w a p u"))

        def QX(b):
            xw = work.tile([P, S], U32, name="xw", align_bytes=64)
            xs = work.tile([P, S], U8, name="xs", align_bytes=64)
            nc.vector.quantize_mx(out=xw[:].bitcast(FP8X4), scales=xs[:], in_=st[("xg", b)][:])
            st[("xw", b)] = (xw, xs)

        def TQ(b, i):
            src = (q_sb[b], k_sb[b])[i]
            ps = psum.tile([P, H, NT, P], BF16, name="ps_qk", tag="bank")
            for h in range(H):
                for a in range(NT):
                    o = a * H * L + h * L
                    nc.tensor.transpose(ps[:, h, a, :], src[:, o : o + L], id_bf[:])
            st[("TQ", b, i)] = ps

        def CQ(b, i, eng):
            dst = work.tile([P, H * S], BF16, name="qkT%d" % i)
            copy(eng, dst[:].bitcast(F32), st[("TQ", b, i)][:].rearrange("l h a p -> l (h a p)").bitcast(F32))
            st[("qk", b, i)] = dst

        def sc_head(b, it, h, view):
            qT = st[("qk", b, 0)]
            kT = st[("qk", b, 1)]
            n = (it + 1) * P
            lhsT = qT[:, h * S + it * P : h * S + (it + 1) * P]
            nc.tensor.matmul(out=view[:, 0:n], lhsT=lhsT, rhs=kT[:, h * S : h * S + n], start=True, stop=False)
            nc.tensor.matmul(out=view[:, it * P : n], lhsT=id_bf[:], rhs=mb[:], start=False, stop=True)

        def SC(b, it, h=0):
            n = (it + 1) * P
            if it < 2:
                ps = psum.tile([P, H, n], F32, name="ps_s", tag="bank")
                for hh in range(H):
                    sc_head(b, it, hh, ps[:, hh, :])
                    st[("S", b, it, hh)] = ps[:, hh, :]
                st[("S2", b, it)] = ps
            else:
                ps1 = psum.tile([P, n], F32, name="ps_s1", tag="bank")
                sc_head(b, it, h, ps1[:])
                st[("S", b, it, h)] = ps1[:]

        def RX(b, it, h):
            n = (it + 1) * P
            if ("nm", b) not in st:
                nm_new = small.tile([P, 2 * NT], F32, name="nm")
                sm_new = small.tile([P, 2 * NT], F32, name="sm")
                rc_new = small.tile([P, 2 * NT], F32, name="rc")
                st[("nm", b)] = (nm_new, sm_new, rc_new)
            if ("e", b, it) not in st:
                e_new = work.tile([P, H * n], F32, name="e_sb%d" % it)
                st[("e", b, it)] = e_new
            c = 2 * it + h
            nc.vector.tensor_scalar(
                out=st[("e", b, it)][:, h * n : (h + 1) * n],
                in0=st[("S", b, it, h)],
                scalar1=-SCALE,
                scalar2=None,
                op0=ALU.mult,
                op1=ALU.min,
                accum_out=st[("nm", b)][0][:, c : c + 1],
            )

        def EX(b, it, h):
            n = (it + 1) * P
            c = 2 * it + h
            nm, sm, rc = st[("nm", b)]
            e_sl = st[("e", b, it)][:, h * n : (h + 1) * n]
            nc.scalar.activation(
                out=e_sl, in_=e_sl, func=ACT.Exp, bias=nm[:, c : c + 1], scale=-1.0, accum_out=sm[:, c : c + 1]
            )

        def RC(b, half):
            nm, sm, rc = st[("nm", b)]
            lo = 4 - 4 * half
            nc.vector.reciprocal(out=rc[:, lo : lo + 4], in_=sm[:, lo : lo + 4])

        def NO(b, it, h, eng):
            n = (it + 1) * P
            c = 2 * it + h
            dst = a_sb[b % 2][it][:, h * AW[it] : h * AW[it] + n]
            src = st[("e", b, it)][:, h * n : (h + 1) * n]
            rcol = st[("nm", b)][2][:, c : c + 1]
            if eng == "g":
                nc.gpsimd.tensor_scalar(out=dst, in0=src, scalar1=rcol, scalar2=0.0, op0=ALU.mult, op1=ALU.add)
            else:
                nc.vector.tensor_scalar(out=dst, in0=src, scalar1=rcol, scalar2=None, op0=ALU.mult)

        def MV(b, j):
            xw, xs = st[("xw", b)]
            U = j // 4
            c = j % 4
            ps = psum.tile([P, 2, H * P], F32, name="ps_v", tag="bank")
            col = c * H * P
            for e in range(2):
                a = 2 * U + e
                nc.tensor.matmul_mx(
                    out=ps[:, e, :],
                    lhsT=xw[:, a * P : (a + 1) * P].bitcast(FP8X4),
                    lhsT_scale=xs[:, a * P : (a + 1) * P],
                    rhs=wvw[:, col : col + H * P].bitcast(FP8X4),
                    rhs_scale=wvs[:, col : col + H * P],
                    start=True,
                    stop=True,
                )
            st[("MV", b, j)] = ps

        def CV(b, j, eng):
            if ("vg", b) not in st:
                vg_new = work.tile([P, 2 * 4 * D], BF16, name="vg", align_bytes=64)
                st[("vg", b)] = vg_new
            o = j * 4 * P
            copy(
                eng,
                st[("vg", b)][:, o : o + 4 * P].rearrange("p (d h e) -> p d h e", h=H, e=2),
                st[("MV", b, j)][:].rearrange("p e (h d) -> p d h e", h=H),
            )

        def QV(b, U):
            if ("vw", b) not in st:
                vw_new = work.tile([P, 2 * D], U32, name="vw", align_bytes=64)
                vs_new = work.tile([P, 2 * D], U8, name="vs", align_bytes=64)
                st[("vw", b)] = (vw_new, vs_new)
            vw, vs = st[("vw", b)]
            nc.vector.quantize_mx(
                out=vw[:, U * D : (U + 1) * D].bitcast(FP8X4),
                scales=vs[:, U * D : (U + 1) * D],
                in_=st[("vg", b)][:, U * 4 * D : (U + 1) * 4 * D],
            )

        def TA(b, g):
            ps = psum.tile([P, 2, H, P], F32, name="ps_a", tag="bank")
            for gi in range(2):
                it, U = SEGS[g][gi]
                words = a_sb[b % 2][it][:].bitcast(F32)
                for h in range(H):
                    o = h * (AW[it] // 2) + U * P
                    nc.tensor.transpose(ps[:, gi, h, :], words[:, o : o + P], id_f[:])
            st[("TA", b, g)] = ps

        def CA(b, g, eng):
            if ("ag", b) not in st:
                ag_new = work.tile([P, 6 * 4 * P], BF16, name="ag", align_bytes=64)
                st[("ag", b)] = ag_new
            copy(
                eng,
                st[("ag", b)][:].bitcast(F32)[:, g * 512 : (g + 1) * 512].rearrange("p (g i h) -> p g i h", g=2, h=H),
                st[("TA", b, g)][:].rearrange("p g h i -> p g i h"),
            )

        def QA(b, part):
            if ("aw", b) not in st:
                aw_new = work.tile([P, 6 * P], U32, name="aw", align_bytes=64)
                as_new = work.tile([P, 6 * P], U8, name="asc", align_bytes=64)
                st[("aw", b)] = (aw_new, as_new)
            aw, asc = st[("aw", b)]
            lo, hi = ((0, 256), (256, 768))[part]
            nc.vector.quantize_mx(out=aw[:, lo:hi].bitcast(FP8X4), scales=asc[:, lo:hi], in_=st[("ag", b)][:, 4 * lo : 4 * hi])

        def FO(b, it):
            aw, asc = st[("aw", b)]
            vw, vs = st[("vw", b)]
            po = psum.tile([P, D], F32, name="po", tag="bank")
            passes = [(it, 0)] + ([(it + 2, 1)] if it >= 2 else [])
            for i, (seg, U) in enumerate(passes):
                nc.tensor.matmul_mx(
                    out=po[:],
                    lhsT=aw[:, seg * P : (seg + 1) * P].bitcast(FP8X4),
                    lhsT_scale=asc[:, seg * P : (seg + 1) * P],
                    rhs=vw[:, U * D : (U + 1) * D].bitcast(FP8X4),
                    rhs_scale=vs[:, U * D : (U + 1) * D],
                    start=(i == 0),
                    stop=(i == len(passes) - 1),
                )
            st[("FO", b, it)] = po

        def CO(b, it, eng):
            if ("o", b) not in st:
                o_new = work.tile([P, NT * D], F32, name="o_sb")
                st[("o", b)] = o_new
            copy(eng, st[("o", b)][:, it * D : (it + 1) * D], st[("FO", b, it)][:])

        def ST(b, pr):
            if b == B - 1:
                ST4(b, 2 * pr)
                ST4(b, 2 * pr + 1)
                return
            nc.sync.dma_start(
                out=out[b, 2 * pr * P : (2 * pr + 2) * P, :].rearrange("(a p) d -> p a d", p=P),
                in_=st[("o", b)][:, 2 * pr * D : (2 * pr + 2) * D].rearrange("p (a d) -> p a d", a=2),
            )

        def ST4(b, it):
            nc.sync.dma_start(out=out[b, it * P : (it + 1) * P, :], in_=st[("o", b)][:, it * D : (it + 1) * D])

        steps = {
            "TW": TW, "CW": CW, "QW": QW,
            "TX": TX, "CX": CX, "QX": QX, "TQ": TQ, "CQ": CQ, "SC": SC, "RX": RX, "EX": EX, "RC": RC,
            "NO": NO, "MV": MV, "CV": CV, "QV": QV, "TA": TA, "CA": CA, "QA": QA, "FO": FO, "CO": CO, "ST": ST,
        }
        nc.vector.memset(warm[:].bitcast(I32), 0)
        WARM(4)
        INIT()
        LQ(0)
        LK(0)
        LM()
        for g in (0, 2, 1, 3):
            LW(g)
        LX(0)
        for b in range(1, B):
            LQ(b)
            LK(b)
            LX(b)
        TQ(0, 0)
        CQ(0, 0, "s")
        TQ(0, 1)
        MB()
        CQ(0, 1, "v")
        WARM(2)
        TW(0)
        CW(0, "s")
        for step in order():
            steps[step[0]](*step[1:])
